import numpy as np
import ml_dtypes


def mxq(x, axis, fmt="e4m3"):
    dtype, down = {"e4m3": (ml_dtypes.float8_e4m3fn, 7), "e5m2": (ml_dtypes.float8_e5m2, 14)}[fmt]
    v = np.moveaxis(np.asarray(x, np.float32).astype(ml_dtypes.bfloat16).astype(np.float64), axis, -1)
    blocks = v.reshape(v.shape[:-1] + (-1, 32))
    amax = np.abs(blocks).max(-1, keepdims=True)
    byte = np.maximum(np.where(amax > 0, np.frexp(amax)[1] - 1 + 127, 0) - down, 1)
    scale = np.exp2(byte - 127.0)
    codes = (blocks / scale).astype(np.float32).astype(dtype).astype(np.float64)
    return np.moveaxis((codes * scale).reshape(v.shape), -1, axis)


WIDE = False


def mx_kscale(k):
    if not WIDE:
        return np.ones(k)
    levels = np.array([10, -10, 5, -5, 0])
    a = np.random.permutation(np.resize(levels, k // 512 * 4)).reshape(k // 512, 4)
    idx = np.arange(k)
    return np.exp2(a[idx // 512, idx % 128 // 32])


BF16 = ml_dtypes.bfloat16


def bf(x):
    return np.asarray(x, np.float32).astype(BF16)


def f64(x):
    return np.asarray(x).astype(np.float64)


B, S, H, NH, D, C = 1, 1024, 1024, 4, 256, 512
V = S


def setup_inputs():
    s = mx_kscale(H)
    return {
        "qh": bf(np.random.standard_normal((NH, B, S, D)) * 1.4),
        "kh": bf(np.random.standard_normal((NH, B, S, D)) * 1.4),
        "v": bf(np.random.standard_normal((B, S, H)) * s),
        "Wv": bf(np.random.standard_normal((H, V)) * 2.0 / np.sqrt(H) / s[:, None]),
        "bv": bf(np.random.standard_normal(V) * 0.3),
    }


def reference(qh, kh, v, Wv, bv):
    qh, kh = f64(qh), f64(kh)
    vv = (mxq(f64(v), 2, "e4m3") @ mxq(f64(Wv), 0, "e4m3")) + f64(bv)
    vq = mxq(vv, 1, "e4m3")
    mask = np.triu(np.full((S, S), -np.inf), 1)
    out = np.zeros((B, S, V))
    for r in range(0, S, C):
        t = r + C
        sc = qh[:, :, r:t] @ kh[:, :, :t].transpose(0, 1, 3, 2) * D ** (-0.5) + mask[r:t, :t]
        e = np.exp(sc - sc.max(-1, keepdims=True))
        p = e / e.sum(-1, keepdims=True)
        out[:, r:t] = (mxq(p, 3, "e4m3") @ vq[:, :t]).mean(0)
    return out

@@ -1,0 +1,357 @@
+from contextlib import ExitStack
+
+import concourse.masks as masks
+import concourse.mybir as mybir
+
+F32 = mybir.dt.float32
+BF16 = mybir.dt.bfloat16
+U32 = mybir.dt.uint32
+U8 = mybir.dt.uint8
+FP8X4 = mybir.dt.float8_e4m3fn_x4
+ALU = mybir.AluOpType
+ACT = mybir.ActivationFunctionType
+AXIS = mybir.AxisListType
+
+P = 128
+NH, S, D, H, V = 4, 1024, 256, 1024, 1024
+K_PASS = 512
+BANK = 512
+S_TILES = S // P
+TILES_PER_GROUP = K_PASS // P
+SCALE = D ** -0.5
+MASKED = -1.0e30
+
+FLOPS = 2 * S * H * V + NH * 2 * (512 * 512 + 512 * 1024) * (D + V)
+
+
+def tile_interpretablemultiheadattention_pa_kernel(tc, qh, kh, v, Wv, bv, out):
+    nc = tc.nc
+    with ExitStack() as ctx:
+        const = ctx.enter_context(tc.tile_pool(name="const", bufs=1))
+        keep = ctx.enter_context(tc.tile_pool(name="keep", bufs=1))
+        raw_qk = ctx.enter_context(tc.tile_pool(name="raw_qk", bufs=2 * S_TILES))
+        stage = ctx.enter_context(tc.tile_pool(name="stage", bufs=2))
+        soft = ctx.enter_context(tc.tile_pool(name="soft", bufs=3))
+        stats = ctx.enter_context(tc.tile_pool(name="stats", bufs=6))
+        psum_acc = ctx.enter_context(tc.psum_pool(name="psum_acc", bufs=1))
+        psum_mm = ctx.enter_context(tc.psum_pool(name="psum_mm", bufs=4))
+        psum_tr = ctx.enter_context(tc.psum_pool(name="psum_tr", bufs=2))
+
+        ident_f = const.tile([P, P], F32, name="ident_f")
+        masks.make_identity(nc, ident_f[:])
+        ident_b = const.tile([P, P], BF16, name="ident_b")
+        masks.make_identity(nc, ident_b[:])
+        causal_f = const.tile([P, P], F32, name="causal_f")
+        nc.gpsimd.memset(causal_f[:], 0.0)
+        nc.gpsimd.affine_select(
+            out=causal_f[:],
+            in_=causal_f[:],
+            compare_op=ALU.is_ge,
+            fill=MASKED,
+            base=0,
+            pattern=[[-1, P]],
+            channel_multiplier=1,
+        )
+        causal_b = const.tile([P, P], BF16, name="causal_b")
+        nc.vector.tensor_copy(out=causal_b[:], in_=causal_f[:])
+        ones_b = const.tile([P, P], BF16, name="ones_b")
+        nc.vector.memset(ones_b[:], 1.0)
+        bias_row = const.tile([P, V], BF16, name="bias_row")
+        nc.vector.memset(bias_row[:], 0.0)
+
+        p_tiles = []
+        for m in range(TILES_PER_GROUP):
+            pair = []
+            for b in range(2):
+                p_tile = keep.tile([P, 2 * K_PASS], BF16, name="p_%d_%d" % (m, b))
+                if m < TILES_PER_GROUP - 1:
+                    nc.vector.memset(p_tile[:, K_PASS + P * (m + 1) :], 0.0)
+                pair.append(p_tile)
+            p_tiles.append(pair)
+
+        nc.sync.dma_start(out=bias_row[0:1, :], in_=bv.rearrange("(o c) -> o c", o=1))
+
+        q_rows = qh.rearrange("n o (j p) d -> j p (n o) d", p=P)
+        k_rows = kh.rearrange("n o (j p) d -> j p (n o) d", p=P)
+        q_raw = []
+        k_raw = []
+
+        def load_qk(j):
+            for rows, raws, name in ((k_rows, k_raw, "k"), (q_rows, q_raw, "q")):
+                raw = raw_qk.tile([P, NH * D], BF16, name="%s_raw%d" % (name, j), tag="raw_qk")
+                nc.sync.dma_start(out=raw[:].rearrange("p (n d) -> p n d", n=NH), in_=rows[j])
+                raws.append(raw)
+
+        w_raw = keep.tile([P, 4 * 2 * V], BF16, name="w_raw")
+        w_rows = Wv.rearrange("(a p e) c -> a p (e c)", a=4, p=P, e=2)
+        v_raw = keep.tile([P, 4 * 2 * H], BF16, name="v_raw")
+        v_rows = v.rearrange("o (a p e) h -> (o a) p (e h)", a=4, p=P, e=2)
+
+        load_qk(0)
+        for a in range(4):
+            nc.sync.dma_start(out=w_raw[:, a * 2 * V : (a + 1) * 2 * V], in_=w_rows[a])
+        for a in range(4):
+            nc.sync.dma_start(out=v_raw[:, a * 2 * H : (a + 1) * 2 * H], in_=v_rows[a])
+        for j in range(1, S_TILES):
+            load_qk(j)
+
+        bias_all = const.tile([P, V], F32, name="bias_all")
+        for half in range(V // BANK):
+            cols = slice(half * BANK, (half + 1) * BANK)
+            bias_ps = psum_mm.tile([P, BANK], F32, name="bias_ps", tag="mm")
+            nc.tensor.matmul(out=bias_ps[:], lhsT=ones_b[:], rhs=bias_row[:, cols], start=True, stop=True)
+            nc.scalar.copy(out=bias_all[:, cols], in_=bias_ps[:])
+
+        qT = keep.tile([P, NH * S], F32, name="qT")
+        kT = keep.tile([P, NH * S], F32, name="kT")
+
+        def transpose_qk(j):
+            for raws, dst in ((k_raw, kT), (q_raw, qT)):
+                words = raws[j][:].bitcast(F32)
+                tr = psum_tr.tile([P, BANK], F32, name="tr_qk", tag="tr")
+                for n in range(NH):
+                    nc.tensor.transpose(tr[:, n * P : (n + 1) * P], words[:, n * P : (n + 1) * P], ident_f[:])
+                nc.scalar.copy(
+                    out=dst[:].rearrange("p (n s) -> p n s", n=NH)[:, :, j * P : (j + 1) * P],
+                    in_=tr[:].rearrange("p (n s) -> p n s", n=NH),
+                )
+
+        qT_b = qT[:].bitcast(BF16).rearrange("p (n s e) -> p n s e", n=NH, e=2)
+        kT_b = kT[:].bitcast(BF16).rearrange("p (n s e) -> p n s e", n=NH, e=2)
+
+        w_codes = keep.tile([P, 2 * V], U32, name="w_codes", align_bytes=64)
+        w_scales = keep.tile([P, 2 * V], U8, name="w_scales", align_bytes=64)
+        for G in range(H // K_PASS):
+            rows_t_c = w_raw[:, G * 4 * V : (G + 1) * 4 * V].rearrange("p (t c) -> p t c", t=4)
+            for half in range(V // BANK):
+                w_grouped = stage.tile([P, 4 * BANK], BF16, name="w_grouped", align_bytes=64)
+                nc.vector.tensor_copy(
+                    out=w_grouped[:].rearrange("p (c i t) -> p c t i", i=4, t=4),
+                    in_=rows_t_c[:, :, half * BANK : (half + 1) * BANK].rearrange("p t (c i) -> p c t i", i=4),
+                )
+                cols = slice(G * V + half * BANK, G * V + (half + 1) * BANK)
+                nc.vector.quantize_mx(
+                    out=w_codes[:, cols].bitcast(FP8X4), scales=w_scales[:, cols], in_=w_grouped[:]
+                )
+
+        v_codes = keep.tile([P, S_TILES * 2 * P], U32, name="v_codes", align_bytes=64)
+        v_scales = keep.tile([P, S_TILES * 2 * P], U8, name="v_scales", align_bytes=64)
+        v_words = v_raw[:].bitcast(F32)
+        for st in range(S_TILES):
+            tr = psum_tr.tile([P, BANK], F32, name="tr_v", tag="tr")
+            for b in range(4):
+                nc.tensor.transpose(
+                    tr[:, b * P : (b + 1) * P],
+                    v_words[:, st * (H // 2) + b * P : st * (H // 2) + (b + 1) * P],
+                    ident_f[:],
+                )
+            v_grouped = stage.tile([P, 2 * K_PASS], BF16, name="v_grouped", align_bytes=64)
+            nc.scalar.copy(
+                out=v_grouped[:].bitcast(F32).rearrange("p (g s u) -> p g s u", g=2, u=2),
+                in_=tr[:].rearrange("p (g u s) -> p g s u", g=2, u=2),
+            )
+            cols = slice(st * 2 * P, (st + 1) * 2 * P)
+            nc.vector.quantize_mx(out=v_codes[:, cols].bitcast(FP8X4), scales=v_scales[:, cols], in_=v_grouped[:])
+
+        transpose_qk(0)
+
+        vv_codes = keep.tile([P, 2 * V], U32, name="vv_codes", align_bytes=64)
+        vv_scales = keep.tile([P, 2 * V], U8, name="vv_scales", align_bytes=64)
+        for g in range(S // K_PASS):
+            for half in range(V // BANK):
+                vv_grouped = stage.tile([P, 4 * BANK], BF16, name="vv_grouped", align_bytes=64)
+                for quarter in range(BANK // P):
+                    c0 = half * BANK + quarter * P
+                    vv_ps = psum_mm.tile([P, BANK], F32, name="vv_ps", tag="mm")
+                    for t in range(4):
+                        for G in range(H // K_PASS):
+                            lcols = slice(((4 * g + t) * 2 + G) * P, ((4 * g + t) * 2 + G + 1) * P)
+                            rcols = slice(G * V + c0, G * V + c0 + P)
+                            nc.tensor.matmul_mx(
+                                out=vv_ps[:, t * P : (t + 1) * P],
+                                lhsT=v_codes[:, lcols].bitcast(FP8X4),
+                                lhsT_scale=v_scales[:, lcols],
+                                rhs=w_codes[:, rcols].bitcast(FP8X4),
+                                rhs_scale=w_scales[:, rcols],
+                                start=(G == 0),
+                                stop=(G == H // K_PASS - 1),
+                            )
+                    nc.vector.tensor_tensor(
+                        out=vv_grouped[:, quarter * 4 * P : (quarter + 1) * 4 * P].rearrange("p (c t) -> p c t", t=4),
+                        in0=vv_ps[:].rearrange("p (t c) -> p c t", t=4),
+                        in1=bias_all[:, c0 : c0 + P].unsqueeze(2).to_broadcast([P, P, 4]),
+                        op=ALU.add,
+                    )
+                cols = slice(g * V + half * BANK, g * V + (half + 1) * BANK)
+                nc.vector.quantize_mx(
+                    out=vv_codes[:, cols].bitcast(FP8X4), scales=vv_scales[:, cols], in_=vv_grouped[:]
+                )
+
+        blocks = [(qt, n) for qt in range(S_TILES) for n in range(NH)]
+        score_banks = {}
+        shifts = {}
+        e_tiles = {}
+        row_sums = {}
+        tr_banks = {}
+        p_operands = {}
+        acc = {}
+
+        def shape_of(i):
+            qt, n = blocks[i]
+            diag_group = qt // TILES_PER_GROUP
+            m = qt % TILES_PER_GROUP
+            diag_cols = P * (m + 1)
+            return qt, n, diag_group, m, diag_cols
+
+        def scores(i):
+            qt, n, diag_group, m, diag_cols = shape_of(i)
+            q_cols = slice(qt * P, (qt + 1) * P)
+            banks = []
+            if diag_group == 1:
+                sc_full = psum_mm.tile([P, BANK], F32, name="sc_full", tag="mm")
+                for e in range(2):
+                    nc.tensor.matmul(
+                        out=sc_full[:],
+                        lhsT=qT_b[:, n, q_cols, e],
+                        rhs=kT_b[:, n, 0:K_PASS, e],
+                        start=(e == 0),
+                        stop=(e == 1),
+                    )
+                banks.append((sc_full, K_PASS, 0))
+            sc_diag = psum_mm.tile([P, BANK], F32, name="sc_diag", tag="mm")
+            k0 = diag_group * K_PASS
+            for e in range(2):
+                nc.tensor.matmul(
+                    out=sc_diag[:, :diag_cols],
+                    lhsT=qT_b[:, n, q_cols, e],
+                    rhs=kT_b[:, n, k0 : k0 + diag_cols, e],
+                    start=(e == 0),
+                    stop=False,
+                )
+            nc.tensor.matmul(
+                out=sc_diag[:, diag_cols - P : diag_cols], lhsT=ident_b[:], rhs=causal_b[:], start=False, stop=True
+            )
+            banks.append((sc_diag, diag_cols, K_PASS))
+            score_banks[i] = banks
+
+        def row_maximum(i):
+            banks = score_banks[i]
+            row_max = stats.tile([P, 2], F32, name="row_max")
+            for b, (bank, width, col) in enumerate(banks):
+                nc.vector.reduce_max(out=row_max[:, b : b + 1], in_=bank[:, :width], axis=AXIS.X)
+            shift = stats.tile([P, 1], F32, name="shift")
+            if len(banks) == 2:
+                nc.vector.tensor_scalar(
+                    out=shift[:], in0=row_max[:, 0:1], scalar1=row_max[:, 1:2], scalar2=-SCALE,
+                    op0=ALU.max, op1=ALU.mult,
+                )
+            else:
+                nc.vector.tensor_scalar(
+                    out=shift[:], in0=row_max[:, 0:1], scalar1=-SCALE, scalar2=None, op0=ALU.mult
+                )
+            shifts[i] = shift
+
+        def exponentials(i):
+            e_tile = soft.tile([P, 2 * K_PASS], F32, name="e_tile")
+            sums = stats.tile([P, 2], F32, name="sums")
+            for b, (bank, width, col) in enumerate(score_banks[i]):
+                nc.scalar.activation(
+                    out=e_tile[:, col : col + width],
+                    in_=bank[:, :width],
+                    func=ACT.Exp,
+                    bias=shifts[i][:],
+                    scale=SCALE,
+                    accum_out=sums[:, b : b + 1],
+                )
+            e_tiles[i] = e_tile
+            row_sums[i] = sums
+
+        def normalise(i):
+            qt, n, diag_group, m, diag_cols = shape_of(i)
+            sums = row_sums[i]
+            recip = stats.tile([P, 1], F32, name="recip")
+            if diag_group == 1:
+                total = stats.tile([P, 1], F32, name="total")
+                nc.vector.tensor_tensor(out=total[:], in0=sums[:, 0:1], in1=sums[:, 1:2], op=ALU.add)
+                nc.vector.reciprocal(out=recip[:], in_=total[:])
+            else:
+                nc.vector.reciprocal(out=recip[:], in_=sums[:, 0:1])
+            used = slice(K_PASS * (1 - diag_group), K_PASS + diag_cols)
+            nc.vector.tensor_scalar(
+                out=p_tiles[m][n % 2][:, used], in0=e_tiles[i][:, used], scalar1=recip[:], scalar2=None, op0=ALU.mult
+            )
+
+        def transposes(i):
+            qt, n, diag_group, m, diag_cols = shape_of(i)
+            p_words = p_tiles[m][n % 2][:].bitcast(F32)
+            w0 = K_PASS * (1 - diag_group) // 2
+            tr = psum_tr.tile([P, BANK], F32, name="tr_p", tag="tr")
+            for b in range(2 * (diag_group + 1)):
+                nc.tensor.transpose(
+                    tr[:, b * P : (b + 1) * P], p_words[:, w0 + b * P : w0 + (b + 1) * P], ident_f[:]
+                )
+            tr_banks[i] = tr
+
+        def quantise(i):
+            qt, n, diag_group, m, diag_cols = shape_of(i)
+            n_groups = diag_group + 1
+            p_grouped = soft.tile([P, 2 * K_PASS], BF16, name="p_grouped", align_bytes=64)
+            nc.scalar.copy(
+                out=p_grouped[:].bitcast(F32)[:, : n_groups * 2 * P].rearrange(
+                    "p (g q u) -> p g q u", g=n_groups, u=2
+                ),
+                in_=tr_banks[i][:, : n_groups * 2 * P].rearrange("p (g u q) -> p g q u", g=n_groups, u=2),
+            )
+            p_codes = soft.tile([P, 2 * P], U32, name="p_codes", align_bytes=64)
+            p_scales = soft.tile([P, 2 * P], U8, name="p_scales", align_bytes=64)
+            nc.vector.quantize_mx(
+                out=p_codes[:, : n_groups * P].bitcast(FP8X4),
+                scales=p_scales[:, : n_groups * P],
+                in_=p_grouped[:, : n_groups * K_PASS],
+            )
+            p_operands[i] = (p_codes, p_scales)
+
+        def weighted_sum(i):
+            qt, n, diag_group, m, diag_cols = shape_of(i)
+            n_groups = diag_group + 1
+            p_codes, p_scales = p_operands[i]
+            if n == 0:
+                acc[qt] = [psum_acc.tile([P, BANK], F32, name="acc%d" % half) for half in range(V // BANK)]
+            for group in range(n_groups):
+                lcols = slice(group * P, (group + 1) * P)
+                for half in range(V // BANK):
+                    rcols = slice(group * V + half * BANK, group * V + (half + 1) * BANK)
+                    nc.tensor.matmul_mx(
+                        out=acc[qt][half][:],
+                        lhsT=p_codes[:, lcols].bitcast(FP8X4),
+                        lhsT_scale=p_scales[:, lcols],
+                        rhs=vv_codes[:, rcols].bitcast(FP8X4),
+                        rhs_scale=vv_scales[:, rcols],
+                        start=(n == 0 and group == 0),
+                        stop=(n == NH - 1 and group == n_groups - 1),
+                    )
+            if n == NH - 1:
+                o_tile = stage.tile([P, V], F32, name="o_tile")
+                nc.scalar.mul(out=o_tile[:, :BANK], in_=acc[qt][0][:], mul=1.0 / NH)
+                nc.vector.tensor_scalar(
+                    out=o_tile[:, BANK:], in0=acc[qt][1][:], scalar1=1.0 / NH, scalar2=None, op0=ALU.mult
+                )
+                nc.sync.dma_start(out=out[0, qt * P : (qt + 1) * P, :], in_=o_tile[:])
+
+        with tc.manual_schedule():
+            for step in range(len(blocks) + 3):
+                if step < len(blocks):
+                    scores(step)
+                    row_maximum(step)
+                if 0 <= step - 1 < len(blocks):
+                    exponentials(step - 1)
+                if 0 <= step - 2 < len(blocks):
+                    transposes(step - 2)
+                if 0 <= step - 1 < len(blocks):
+                    normalise(step - 1)
+                if 0 <= step - 2 < len(blocks):
+                    quantise(step - 2)
+                if 0 <= step - 3 < len(blocks):
+                    weighted_sum(step - 3)
+                if step < len(blocks) and step % NH == 0 and step // NH + 1 < S_TILES:
+                    transpose_qk(step // NH + 1)

@@ -24,18 +24,30 @@ MASKED = -1.0e30
 FLOPS = 2 * S * H * V + NH * 2 * (512 * 512 + 512 * 1024) * (D + V)
 
 
+LAG_EXP = 1
+LAG_NORM = 2
+LAG_TRANSPOSE = 3
+LAG_COPY = 4
+LAG_QUANT = 5
+LAG_SUM = 6
+LAG_OUT = 7
+
+
 def tile_interpretablemultiheadattention_pa_kernel(tc, qh, kh, v, Wv, bv, out):
     nc = tc.nc
     with ExitStack() as ctx:
         const = ctx.enter_context(tc.tile_pool(name="const", bufs=1))
         keep = ctx.enter_context(tc.tile_pool(name="keep", bufs=1))
         raw_qk = ctx.enter_context(tc.tile_pool(name="raw_qk", bufs=2 * S_TILES))
+        w_stage = ctx.enter_context(tc.tile_pool(name="w_stage", bufs=4))
         stage = ctx.enter_context(tc.tile_pool(name="stage", bufs=2))
         soft = ctx.enter_context(tc.tile_pool(name="soft", bufs=3))
         stats = ctx.enter_context(tc.tile_pool(name="stats", bufs=6))
-        psum_acc = ctx.enter_context(tc.psum_pool(name="psum_acc", bufs=1))
-        psum_mm = ctx.enter_context(tc.psum_pool(name="psum_mm", bufs=4))
-        psum_tr = ctx.enter_context(tc.psum_pool(name="psum_tr", bufs=2))
+        psum = ctx.enter_context(tc.psum_pool(name="psum", bufs=1))
+        ctx.enter_context(tc.manual_schedule())
+
+        def bank(name):
+            return psum.tile([P, BANK], F32, name=name, tag=name)
 
         ident_f = const.tile([P, P], F32, name="ident_f")
         masks.make_identity(nc, ident_f[:])
@@ -52,8 +64,10 @@ def tile_interpretablemultiheadattention_pa_kernel(tc, qh, kh, v, Wv, bv, out):
             pattern=[[-1, P]],
             channel_multiplier=1,
         )
-        causal_b = const.tile([P, P], BF16, name="causal_b")
-        nc.vector.tensor_copy(out=causal_b[:], in_=causal_f[:])
+        warm_in = const.tile([P, 1], F32, name="warm_in")
+        warm_out = const.tile([P, 1], F32, name="warm_out")
+        nc.vector.memset(warm_in[:], 0.0)
+        nc.scalar.activation(out=warm_out[:], in_=warm_in[:], func=ACT.Exp)
         ones_b = const.tile([P, P], BF16, name="ones_b")
         nc.vector.memset(ones_b[:], 1.0)
         bias_row = const.tile([P, V], BF16, name="bias_row")
@@ -68,64 +82,102 @@ def tile_interpretablemultiheadattention_pa_kernel(tc, qh, kh, v, Wv, bv, out):
                     nc.vector.memset(p_tile[:, K_PASS + P * (m + 1) :], 0.0)
                 pair.append(p_tile)
             p_tiles.append(pair)
+        causal_b = const.tile([P, P], BF16, name="causal_b")
+        nc.vector.tensor_copy(out=causal_b[:], in_=causal_f[:])
 
         nc.sync.dma_start(out=bias_row[0:1, :], in_=bv.rearrange("(o c) -> o c", o=1))
 
-        q_rows = qh.rearrange("n o (j p) d -> j p (n o) d", p=P)
-        k_rows = kh.rearrange("n o (j p) d -> j p (n o) d", p=P)
-        q_raw = []
-        k_raw = []
+        rows_of = {
+            "q": qh.rearrange("n o (j p) d -> j p (n o) d", p=P),
+            "k": kh.rearrange("n o (j p) d -> j p (n o) d", p=P),
+        }
+        raw_of = {}
 
         def load_qk(j):
-            for rows, raws, name in ((k_rows, k_raw, "k"), (q_rows, q_raw, "q")):
+            for name in ("k", "q"):
                 raw = raw_qk.tile([P, NH * D], BF16, name="%s_raw%d" % (name, j), tag="raw_qk")
-                nc.sync.dma_start(out=raw[:].rearrange("p (n d) -> p n d", n=NH), in_=rows[j])
-                raws.append(raw)
+                nc.sync.dma_start(out=raw[:].rearrange("p (n d) -> p n d", n=NH), in_=rows_of[name][j])
+                raw_of[(name, j)] = raw
 
         w_raw = keep.tile([P, 4 * 2 * V], BF16, name="w_raw")
         w_rows = Wv.rearrange("(a p e) c -> a p (e c)", a=4, p=P, e=2)
         v_raw = keep.tile([P, 4 * 2 * H], BF16, name="v_raw")
         v_rows = v.rearrange("o (a p e) h -> (o a) p (e h)", a=4, p=P, e=2)
 
-        load_qk(0)
+        def load_v(a):
+            nc.sync.dma_start(out=v_raw[:, a * 2 * H : (a + 1) * 2 * H], in_=v_rows[a])
+
+        load_v(0)
+        load_v(1)
         for a in range(4):
             nc.sync.dma_start(out=w_raw[:, a * 2 * V : (a + 1) * 2 * V], in_=w_rows[a])
-        for a in range(4):
-            nc.sync.dma_start(out=v_raw[:, a * 2 * H : (a + 1) * 2 * H], in_=v_rows[a])
-        for j in range(1, S_TILES):
+        load_qk(0)
+        load_qk(1)
+        load_v(2)
+        load_v(3)
+        for j in range(2, S_TILES):
             load_qk(j)
 
         bias_all = const.tile([P, V], F32, name="bias_all")
         for half in range(V // BANK):
             cols = slice(half * BANK, (half + 1) * BANK)
-            bias_ps = psum_mm.tile([P, BANK], F32, name="bias_ps", tag="mm")
+            bias_ps = bank("mm%d" % half)
             nc.tensor.matmul(out=bias_ps[:], lhsT=ones_b[:], rhs=bias_row[:, cols], start=True, stop=True)
             nc.scalar.copy(out=bias_all[:, cols], in_=bias_ps[:])
 
-        qT = keep.tile([P, NH * S], F32, name="qT")
-        kT = keep.tile([P, NH * S], F32, name="kT")
+        words_T = {"q": keep.tile([P, NH * S], F32, name="qT"), "k": keep.tile([P, NH * S], F32, name="kT")}
 
-        def transpose_qk(j):
-            for raws, dst in ((k_raw, kT), (q_raw, qT)):
-                words = raws[j][:].bitcast(F32)
-                tr = psum_tr.tile([P, BANK], F32, name="tr_qk", tag="tr")
-                for n in range(NH):
-                    nc.tensor.transpose(tr[:, n * P : (n + 1) * P], words[:, n * P : (n + 1) * P], ident_f[:])
-                nc.scalar.copy(
-                    out=dst[:].rearrange("p (n s) -> p n s", n=NH)[:, :, j * P : (j + 1) * P],
-                    in_=tr[:].rearrange("p (n s) -> p n s", n=NH),
+        def qk_transposes(name, j, tr):
+            words = raw_of[(name, j)][:].bitcast(F32)
+            for n in range(NH):
+                nc.tensor.transpose(tr[:, n * P : (n + 1) * P], words[:, n * P : (n + 1) * P], ident_f[:])
+
+        def qk_copy(name, j, tr):
+            nc.scalar.copy(
+                out=words_T[name][:].rearrange("p (n s) -> p n s", n=NH)[:, :, j * P : (j + 1) * P],
+                in_=tr[:].rearrange("p (n s) -> p n s", n=NH),
+            )
+
+        qT_b = words_T["q"][:].bitcast(BF16).rearrange("p (n s e) -> p n s e", n=NH, e=2)
+        kT_b = words_T["k"][:].bitcast(BF16).rearrange("p (n s e) -> p n s e", n=NH, e=2)
+
+        v_codes = keep.tile([P, S_TILES * 2 * P], U32, name="v_codes", align_bytes=64)
+        v_scales = keep.tile([P, S_TILES * 2 * P], U8, name="v_scales", align_bytes=64)
+        v_words = v_raw[:].bitcast(F32)
+
+        def v_transposes(st, tr):
+            for b in range(4):
+                nc.tensor.transpose(
+                    tr[:, b * P : (b + 1) * P],
+                    v_words[:, st * (H // 2) + b * P : st * (H // 2) + (b + 1) * P],
+                    ident_f[:],
                 )
 
-        qT_b = qT[:].bitcast(BF16).rearrange("p (n s e) -> p n s e", n=NH, e=2)
-        kT_b = kT[:].bitcast(BF16).rearrange("p (n s e) -> p n s e", n=NH, e=2)
+        def v_copy(tr):
+            v_grouped = soft.tile([P, 2 * K_PASS], BF16, name="v_grouped", align_bytes=64)
+            nc.scalar.copy(
+                out=v_grouped[:].bitcast(F32).rearrange("p (g s u) -> p g s u", g=2, u=2),
+                in_=tr[:].rearrange("p (g u s) -> p g s u", g=2, u=2),
+            )
+            return v_grouped
+
+        def v_quantise(st, v_grouped):
+            cols = slice(st * 2 * P, (st + 1) * 2 * P)
+            nc.vector.quantize_mx(out=v_codes[:, cols].bitcast(FP8X4), scales=v_scales[:, cols], in_=v_grouped[:])
+
+        for st, name in enumerate(("tr0", "tr1", "mm2", "mm3")):
+            tr = bank(name)
+            v_transposes(st, tr)
+            v_quantise(st, v_copy(tr))
 
         w_codes = keep.tile([P, 2 * V], U32, name="w_codes", align_bytes=64)
         w_scales = keep.tile([P, 2 * V], U8, name="w_scales", align_bytes=64)
         for G in range(H // K_PASS):
             rows_t_c = w_raw[:, G * 4 * V : (G + 1) * 4 * V].rearrange("p (t c) -> p t c", t=4)
             for half in range(V // BANK):
-                w_grouped = stage.tile([P, 4 * BANK], BF16, name="w_grouped", align_bytes=64)
-                nc.vector.tensor_copy(
+                w_grouped = w_stage.tile([P, 4 * BANK], BF16, name="w_grouped", align_bytes=64)
+                regroup = nc.vector.tensor_copy if half == 0 else nc.scalar.copy
+                regroup(
                     out=w_grouped[:].rearrange("p (c i t) -> p c t i", i=4, t=4),
                     in_=rows_t_c[:, :, half * BANK : (half + 1) * BANK].rearrange("p t (c i) -> p c t i", i=4),
                 )
@@ -134,67 +186,73 @@ def tile_interpretablemultiheadattention_pa_kernel(tc, qh, kh, v, Wv, bv, out):
                     out=w_codes[:, cols].bitcast(FP8X4), scales=w_scales[:, cols], in_=w_grouped[:]
                 )
 
-        v_codes = keep.tile([P, S_TILES * 2 * P], U32, name="v_codes", align_bytes=64)
-        v_scales = keep.tile([P, S_TILES * 2 * P], U8, name="v_scales", align_bytes=64)
-        v_words = v_raw[:].bitcast(F32)
-        for st in range(S_TILES):
-            tr = psum_tr.tile([P, BANK], F32, name="tr_v", tag="tr")
-            for b in range(4):
-                nc.tensor.transpose(
-                    tr[:, b * P : (b + 1) * P],
-                    v_words[:, st * (H // 2) + b * P : st * (H // 2) + (b + 1) * P],
-                    ident_f[:],
-                )
-            v_grouped = stage.tile([P, 2 * K_PASS], BF16, name="v_grouped", align_bytes=64)
-            nc.scalar.copy(
-                out=v_grouped[:].bitcast(F32).rearrange("p (g s u) -> p g s u", g=2, u=2),
-                in_=tr[:].rearrange("p (g u s) -> p g s u", g=2, u=2),
-            )
-            cols = slice(st * 2 * P, (st + 1) * 2 * P)
-            nc.vector.quantize_mx(out=v_codes[:, cols].bitcast(FP8X4), scales=v_scales[:, cols], in_=v_grouped[:])
-
-        transpose_qk(0)
-
         vv_codes = keep.tile([P, 2 * V], U32, name="vv_codes", align_bytes=64)
         vv_scales = keep.tile([P, 2 * V], U8, name="vv_scales", align_bytes=64)
-        for g in range(S // K_PASS):
-            for half in range(V // BANK):
-                vv_grouped = stage.tile([P, 4 * BANK], BF16, name="vv_grouped", align_bytes=64)
-                for quarter in range(BANK // P):
-                    c0 = half * BANK + quarter * P
-                    vv_ps = psum_mm.tile([P, BANK], F32, name="vv_ps", tag="mm")
-                    for t in range(4):
-                        for G in range(H // K_PASS):
-                            lcols = slice(((4 * g + t) * 2 + G) * P, ((4 * g + t) * 2 + G + 1) * P)
-                            rcols = slice(G * V + c0, G * V + c0 + P)
-                            nc.tensor.matmul_mx(
-                                out=vv_ps[:, t * P : (t + 1) * P],
-                                lhsT=v_codes[:, lcols].bitcast(FP8X4),
-                                lhsT_scale=v_scales[:, lcols],
-                                rhs=w_codes[:, rcols].bitcast(FP8X4),
-                                rhs_scale=w_scales[:, rcols],
-                                start=(G == 0),
-                                stop=(G == H // K_PASS - 1),
-                            )
-                    nc.vector.tensor_tensor(
-                        out=vv_grouped[:, quarter * 4 * P : (quarter + 1) * 4 * P].rearrange("p (c t) -> p c t", t=4),
-                        in0=vv_ps[:].rearrange("p (t c) -> p c t", t=4),
-                        in1=bias_all[:, c0 : c0 + P].unsqueeze(2).to_broadcast([P, P, 4]),
-                        op=ALU.add,
+        UNITS = V // P
+
+        def value_passes(g, unit, vv_ps):
+            for t in range(4):
+                for G in range(H // K_PASS):
+                    lcols = slice(((4 * g + t) * 2 + G) * P, ((4 * g + t) * 2 + G + 1) * P)
+                    rcols = slice(G * V + unit * P, G * V + (unit + 1) * P)
+                    nc.tensor.matmul_mx(
+                        out=vv_ps[:, t * P : (t + 1) * P],
+                        lhsT=v_codes[:, lcols].bitcast(FP8X4),
+                        lhsT_scale=v_scales[:, lcols],
+                        rhs=w_codes[:, rcols].bitcast(FP8X4),
+                        rhs_scale=w_scales[:, rcols],
+                        start=(G == 0),
+                        stop=(G == H // K_PASS - 1),
                     )
-                cols = slice(g * V + half * BANK, g * V + (half + 1) * BANK)
-                nc.vector.quantize_mx(
-                    out=vv_codes[:, cols].bitcast(FP8X4), scales=vv_scales[:, cols], in_=vv_grouped[:]
-                )
+
+        def value_add(unit, vv_ps, vv_grouped):
+            quarter = unit % 4
+            nc.vector.tensor_tensor(
+                out=vv_grouped[:, quarter * 4 * P : (quarter + 1) * 4 * P].rearrange("p (c t) -> p c t", t=4),
+                in0=vv_ps[:].rearrange("p (t c) -> p c t", t=4),
+                in1=bias_all[:, unit * P : (unit + 1) * P].unsqueeze(2).to_broadcast([P, P, 4]),
+                op=ALU.add,
+            )
+
+        def value_quantise(g, half, vv_grouped):
+            cols = slice(g * V + half * BANK, g * V + (half + 1) * BANK)
+            nc.vector.quantize_mx(
+                out=vv_codes[:, cols].bitcast(FP8X4), scales=vv_scales[:, cols], in_=vv_grouped[:]
+            )
+
+        def first_qk(j):
+            for name, bank_name in (("k", "tr0"), ("q", "tr1")):
+                tr = bank(bank_name)
+                qk_transposes(name, j, tr)
+                qk_copy(name, j, tr)
+
+        first_qk(0)
+        for unit in range(UNITS):
+            if unit % 4 == 0:
+                vv_grouped = stage.tile([P, 4 * BANK], BF16, name="vv_grouped", align_bytes=64)
+            vv_ps = bank("mm%d" % (unit % 4))
+            value_passes(0, unit, vv_ps)
+            value_add(unit, vv_ps, vv_grouped)
+            if unit % 4 == 3:
+                value_quantise(0, unit // 4, vv_grouped)
+                if unit == 3:
+                    first_qk(1)
 
         blocks = [(qt, n) for qt in range(S_TILES) for n in range(NH)]
+        LIGHT = TILES_PER_GROUP * NH
         score_banks = {}
+        row_maxima = {}
         shifts = {}
         e_tiles = {}
         row_sums = {}
+        recips = {}
         tr_banks = {}
+        p_groupeds = {}
         p_operands = {}
         acc = {}
+
+        def live(i):
+            return 0 <= i < len(blocks)
 
         def shape_of(i):
             qt, n = blocks[i]
@@ -203,98 +261,124 @@ def tile_interpretablemultiheadattention_pa_kernel(tc, qh, kh, v, Wv, bv, out):
             diag_cols = P * (m + 1)
             return qt, n, diag_group, m, diag_cols
 
-        def scores(i):
+        def score_matmul(i, sc, k0, width, e, start, stop):
+            qt, n = blocks[i]
+            nc.tensor.matmul(
+                out=sc[:, :width],
+                lhsT=qT_b[:, n, qt * P : (qt + 1) * P, e],
+                rhs=kT_b[:, n, k0 : k0 + width, e],
+                start=start,
+                stop=stop,
+            )
+
+        def scores_first(i):
+            if not live(i):
+                return
             qt, n, diag_group, m, diag_cols = shape_of(i)
-            q_cols = slice(qt * P, (qt + 1) * P)
-            banks = []
             if diag_group == 1:
-                sc_full = psum_mm.tile([P, BANK], F32, name="sc_full", tag="mm")
-                for e in range(2):
-                    nc.tensor.matmul(
-                        out=sc_full[:],
-                        lhsT=qT_b[:, n, q_cols, e],
-                        rhs=kT_b[:, n, 0:K_PASS, e],
-                        start=(e == 0),
-                        stop=(e == 1),
-                    )
-                banks.append((sc_full, K_PASS, 0))
-            sc_diag = psum_mm.tile([P, BANK], F32, name="sc_diag", tag="mm")
-            k0 = diag_group * K_PASS
-            for e in range(2):
-                nc.tensor.matmul(
-                    out=sc_diag[:, :diag_cols],
-                    lhsT=qT_b[:, n, q_cols, e],
-                    rhs=kT_b[:, n, k0 : k0 + diag_cols, e],
-                    start=(e == 0),
-                    stop=False,
-                )
+                sc_full = bank("mm%d" % (2 * (i % 2)))
+                sc_diag = bank("mm%d" % (2 * (i % 2) + 1))
+                score_matmul(i, sc_full, 0, K_PASS, 0, True, False)
+                score_matmul(i, sc_full, 0, K_PASS, 1, False, True)
+                score_banks[i] = [(sc_full, K_PASS, 0), (sc_diag, diag_cols, K_PASS)]
+            else:
+                sc_diag = bank("mm%d" % (i % 2))
+                score_matmul(i, sc_diag, 0, diag_cols, 0, True, False)
+                score_banks[i] = [(sc_diag, diag_cols, K_PASS)]
+
+        def scores_second(i):
+            if not live(i):
+                return
+            qt, n, diag_group, m, diag_cols = shape_of(i)
+            sc_diag = score_banks[i][-1][0]
+            if diag_group == 1:
+                score_matmul(i, sc_diag, K_PASS, diag_cols, 0, True, False)
+            score_matmul(i, sc_diag, diag_group * K_PASS, diag_cols, 1, False, False)
             nc.tensor.matmul(
                 out=sc_diag[:, diag_cols - P : diag_cols], lhsT=ident_b[:], rhs=causal_b[:], start=False, stop=True
             )
-            banks.append((sc_diag, diag_cols, K_PASS))
-            score_banks[i] = banks
 
-        def row_maximum(i):
-            banks = score_banks[i]
-            row_max = stats.tile([P, 2], F32, name="row_max")
-            for b, (bank, width, col) in enumerate(banks):
-                nc.vector.reduce_max(out=row_max[:, b : b + 1], in_=bank[:, :width], axis=AXIS.X)
+        def maximum_first(i):
+            if not live(i):
+                return
+            row_maxima[i] = stats.tile([P, 2], F32, name="row_max")
+            if len(score_banks[i]) == 2:
+                sc_full = score_banks[i][0][0]
+                nc.vector.reduce_max(out=row_maxima[i][:, 1:2], in_=sc_full[:], axis=AXIS.X)
+
+        def maximum_second(i):
+            if not live(i):
+                return
+            sc_diag, width, col = score_banks[i][-1]
+            row_max = row_maxima[i]
+            nc.vector.reduce_max(out=row_max[:, 0:1], in_=sc_diag[:, :width], axis=AXIS.X)
             shift = stats.tile([P, 1], F32, name="shift")
-            if len(banks) == 2:
-                nc.vector.tensor_scalar(
+            if len(score_banks[i]) == 2:
+                nc.gpsimd.tensor_scalar(
                     out=shift[:], in0=row_max[:, 0:1], scalar1=row_max[:, 1:2], scalar2=-SCALE,
                     op0=ALU.max, op1=ALU.mult,
                 )
             else:
-                nc.vector.tensor_scalar(
-                    out=shift[:], in0=row_max[:, 0:1], scalar1=-SCALE, scalar2=None, op0=ALU.mult
+                nc.gpsimd.tensor_scalar(
+                    out=shift[:], in0=row_max[:, 0:1], scalar1=-SCALE, scalar2=0.0, op0=ALU.mult, op1=ALU.add
                 )
             shifts[i] = shift
 
         def exponentials(i):
+            if not live(i):
+                return
             e_tile = soft.tile([P, 2 * K_PASS], F32, name="e_tile")
             sums = stats.tile([P, 2], F32, name="sums")
-            for b, (bank, width, col) in enumerate(score_banks[i]):
+            for b, (sc, width, col) in enumerate(score_banks[i]):
                 nc.scalar.activation(
                     out=e_tile[:, col : col + width],
-                    in_=bank[:, :width],
+                    in_=sc[:, :width],
                     func=ACT.Exp,
                     bias=shifts[i][:],
                     scale=SCALE,
                     accum_out=sums[:, b : b + 1],
                 )
             e_tiles[i] = e_tile
-            row_sums[i] = sums
+            if len(score_banks[i]) == 2:
+                total = stats.tile([P, 1], F32, name="total")
+                nc.gpsimd.tensor_tensor(out=total[:], in0=sums[:, 0:1], in1=sums[:, 1:2], op=ALU.add)
+                row_sums[i] = total
+            else:
+                row_sums[i] = sums
+
+        def reciprocal(i):
+            if not live(i):
+                return
+            recips[i] = stats.tile([P, 1], F32, name="recip")
+            nc.vector.reciprocal(out=recips[i][:], in_=row_sums[i][:, 0:1])
 
         def normalise(i):
+            if not live(i):
+                return
             qt, n, diag_group, m, diag_cols = shape_of(i)
-            sums = row_sums[i]
-            recip = stats.tile([P, 1], F32, name="recip")
-            if diag_group == 1:
-                total = stats.tile([P, 1], F32, name="total")
-                nc.vector.tensor_tensor(out=total[:], in0=sums[:, 0:1], in1=sums[:, 1:2], op=ALU.add)
-                nc.vector.reciprocal(out=recip[:], in_=total[:])
-            else:
-                nc.vector.reciprocal(out=recip[:], in_=sums[:, 0:1])
             used = slice(K_PASS * (1 - diag_group), K_PASS + diag_cols)
             nc.vector.tensor_scalar(
-                out=p_tiles[m][n % 2][:, used], in0=e_tiles[i][:, used], scalar1=recip[:], scalar2=None, op0=ALU.mult
+                out=p_tiles[m][n % 2][:, used], in0=e_tiles[i][:, used], scalar1=recips[i][:], scalar2=None,
+                op0=ALU.mult,
             )
 
         def transposes(i):
+            if not live(i):
+                return
             qt, n, diag_group, m, diag_cols = shape_of(i)
             p_words = p_tiles[m][n % 2][:].bitcast(F32)
             w0 = K_PASS * (1 - diag_group) // 2
-            tr = psum_tr.tile([P, BANK], F32, name="tr_p", tag="tr")
+            tr = bank("tr%d" % (i % 2))
             for b in range(2 * (diag_group + 1)):
                 nc.tensor.transpose(
                     tr[:, b * P : (b + 1) * P], p_words[:, w0 + b * P : w0 + (b + 1) * P], ident_f[:]
                 )
             tr_banks[i] = tr
 
-        def quantise(i):
-            qt, n, diag_group, m, diag_cols = shape_of(i)
-            n_groups = diag_group + 1
+        def copy_out(i):
+            if not live(i):
+                return
+            n_groups = shape_of(i)[2] + 1
             p_grouped = soft.tile([P, 2 * K_PASS], BF16, name="p_grouped", align_bytes=64)
             nc.scalar.copy(
                 out=p_grouped[:].bitcast(F32)[:, : n_groups * 2 * P].rearrange(
@@ -302,21 +386,29 @@ def tile_interpretablemultiheadattention_pa_kernel(tc, qh, kh, v, Wv, bv, out):
                 ),
                 in_=tr_banks[i][:, : n_groups * 2 * P].rearrange("p (g u q) -> p g q u", g=n_groups, u=2),
             )
+            p_groupeds[i] = p_grouped
+
+        def quantise(i):
+            if not live(i):
+                return
+            n_groups = shape_of(i)[2] + 1
             p_codes = soft.tile([P, 2 * P], U32, name="p_codes", align_bytes=64)
             p_scales = soft.tile([P, 2 * P], U8, name="p_scales", align_bytes=64)
             nc.vector.quantize_mx(
                 out=p_codes[:, : n_groups * P].bitcast(FP8X4),
                 scales=p_scales[:, : n_groups * P],
-                in_=p_grouped[:, : n_groups * K_PASS],
+                in_=p_groupeds[i][:, : n_groups * K_PASS],
             )
             p_operands[i] = (p_codes, p_scales)
 
         def weighted_sum(i):
+            if not live(i):
+                return
             qt, n, diag_group, m, diag_cols = shape_of(i)
             n_groups = diag_group + 1
             p_codes, p_scales = p_operands[i]
             if n == 0:
-                acc[qt] = [psum_acc.tile([P, BANK], F32, name="acc%d" % half) for half in range(V // BANK)]
+                acc[qt] = [bank("acc%d" % half) for half in range(V // BANK)]
             for group in range(n_groups):
                 lcols = slice(group * P, (group + 1) * P)
                 for half in range(V // BANK):
@@ -330,28 +422,63 @@ def tile_interpretablemultiheadattention_pa_kernel(tc, qh, kh, v, Wv, bv, out):
                         start=(n == 0 and group == 0),
                         stop=(n == NH - 1 and group == n_groups - 1),
                     )
-            if n == NH - 1:
-                o_tile = stage.tile([P, V], F32, name="o_tile")
-                nc.scalar.mul(out=o_tile[:, :BANK], in_=acc[qt][0][:], mul=1.0 / NH)
-                nc.vector.tensor_scalar(
-                    out=o_tile[:, BANK:], in0=acc[qt][1][:], scalar1=1.0 / NH, scalar2=None, op0=ALU.mult
-                )
-                nc.sync.dma_start(out=out[0, qt * P : (qt + 1) * P, :], in_=o_tile[:])
 
-        with tc.manual_schedule():
-            for step in range(len(blocks) + 3):
-                if step < len(blocks):
-                    scores(step)
-                    row_maximum(step)
-                if 0 <= step - 1 < len(blocks):
-                    exponentials(step - 1)
-                if 0 <= step - 2 < len(blocks):
-                    transposes(step - 2)
-                if 0 <= step - 1 < len(blocks):
-                    normalise(step - 1)
-                if 0 <= step - 2 < len(blocks):
-                    quantise(step - 2)
-                if 0 <= step - 3 < len(blocks):
-                    weighted_sum(step - 3)
-                if step < len(blocks) and step % NH == 0 and step // NH + 1 < S_TILES:
-                    transpose_qk(step // NH + 1)
+        def store_out(i):
+            if not live(i) or blocks[i][1] != NH - 1:
+                return
+            qt = blocks[i][0]
+            o_tile = stage.tile([P, V], F32, name="o_tile")
+            nc.scalar.mul(out=o_tile[:, :BANK], in_=acc[qt][0][:], mul=1.0 / NH)
+            nc.vector.tensor_scalar(
+                out=o_tile[:, BANK:], in0=acc[qt][1][:], scalar1=1.0 / NH, scalar2=None, op0=ALU.mult
+            )
+            nc.sync.dma_start(out=out[0, qt * P : (qt + 1) * P, :], in_=o_tile[:])
+
+        later_tiles = [("v", st) for st in range(4, S_TILES)]
+        for j in range(2, S_TILES):
+            later_tiles.extend([("k", j), ("q", j)])
+        assert len(later_tiles) == LIGHT
+        later_banks = {}
+        later_grouped = {}
+        FIRST_UNIT_STEP = 6
+        unit_banks = {}
+        unit_grouped = {}
+
+        for s in range(len(blocks) + LAG_OUT):
+            store_out(s - LAG_OUT)
+            if s - 1 in later_banks:
+                name, idx = later_tiles[s - 1]
+                if name == "v":
+                    later_grouped[s - 1] = v_copy(later_banks[s - 1])
+                else:
+                    qk_copy(name, idx, later_banks[s - 1])
+            last_unit = s - 1 - FIRST_UNIT_STEP
+            if last_unit in unit_banks:
+                if last_unit % 4 == 0:
+                    unit_grouped[last_unit // 4] = stage.tile([P, 4 * BANK], BF16, name="vv_grouped", align_bytes=64)
+                value_add(last_unit, unit_banks[last_unit], unit_grouped[last_unit // 4])
+            copy_out(s - LAG_COPY)
+            quantise(s - LAG_QUANT)
+            reciprocal(s - LAG_NORM)
+            scores_first(s)
+            maximum_first(s)
+            exponentials(s - LAG_EXP)
+            normalise(s - LAG_NORM)
+            if s - 2 in later_grouped:
+                v_quantise(later_tiles[s - 2][1], later_grouped[s - 2])
+            if last_unit in unit_banks and last_unit % 4 == 3:
+                value_quantise(1, last_unit // 4, unit_grouped[last_unit // 4])
+            transposes(s - LAG_TRANSPOSE)
+            if s < LIGHT:
+                name, idx = later_tiles[s]
+                later_banks[s] = bank("mm2")
+                if name == "v":
+                    v_transposes(idx, later_banks[s])
+                else:
+                    qk_transposes(name, idx, later_banks[s])
+            scores_second(s)
+            maximum_second(s)
+            weighted_sum(s - LAG_SUM)
+            if 0 <= s - FIRST_UNIT_STEP < UNITS:
+                unit_banks[s - FIRST_UNIT_STEP] = bank("mm3")
+                value_passes(1, s - FIRST_UNIT_STEP, unit_banks[s - FIRST_UNIT_STEP])

@@ -85,8 +85,6 @@ def tile_interpretablemultiheadattention_pa_kernel(tc, qh, kh, v, Wv, bv, out):
         causal_b = const.tile([P, P], BF16, name="causal_b")
         nc.vector.tensor_copy(out=causal_b[:], in_=causal_f[:])
 
-        nc.sync.dma_start(out=bias_row[0:1, :], in_=bv.rearrange("(o c) -> o c", o=1))
-
         rows_of = {
             "q": qh.rearrange("n o (j p) d -> j p (n o) d", p=P),
             "k": kh.rearrange("n o (j p) d -> j p (n o) d", p=P),
@@ -100,7 +98,8 @@ def tile_interpretablemultiheadattention_pa_kernel(tc, qh, kh, v, Wv, bv, out):
                 raw_of[(name, j)] = raw
 
         w_raw = keep.tile([P, 4 * 2 * V], BF16, name="w_raw")
-        w_rows = Wv.rearrange("(a p e) c -> a p (e c)", a=4, p=P, e=2)
+        w_rows = Wv.rearrange("(a p e) c -> a p e c", a=4, p=P, e=2)
+        w_raw_aec = w_raw[:].rearrange("p (a e c) -> p a e c", a=4, e=2)
         v_raw = keep.tile([P, 4 * 2 * H], BF16, name="v_raw")
         v_rows = v.rearrange("o (a p e) h -> (o a) p (e h)", a=4, p=P, e=2)
 
@@ -109,21 +108,18 @@ def tile_interpretablemultiheadattention_pa_kernel(tc, qh, kh, v, Wv, bv, out):
 
         load_v(0)
         load_v(1)
-        for a in range(4):
-            nc.sync.dma_start(out=w_raw[:, a * 2 * V : (a + 1) * 2 * V], in_=w_rows[a])
+        for half in range(V // BANK):
+            cols = slice(half * BANK, (half + 1) * BANK)
+            for a in range(4):
+                nc.sync.dma_start(out=w_raw_aec[:, a, :, cols], in_=w_rows[a][:, :, cols])
+            if half == 0:
+                nc.sync.dma_start(out=bias_row[0:1, :], in_=bv.rearrange("(o c) -> o c", o=1))
         load_qk(0)
         load_qk(1)
         load_v(2)
         load_v(3)
         for j in range(2, S_TILES):
             load_qk(j)
-
-        bias_all = const.tile([P, V], F32, name="bias_all")
-        for half in range(V // BANK):
-            cols = slice(half * BANK, (half + 1) * BANK)
-            bias_ps = bank("mm%d" % half)
-            nc.tensor.matmul(out=bias_ps[:], lhsT=ones_b[:], rhs=bias_row[:, cols], start=True, stop=True)
-            nc.scalar.copy(out=bias_all[:, cols], in_=bias_ps[:])
 
         words_T = {"q": keep.tile([P, NH * S], F32, name="qT"), "k": keep.tile([P, NH * S], F32, name="kT")}
 
@@ -170,13 +166,20 @@ def tile_interpretablemultiheadattention_pa_kernel(tc, qh, kh, v, Wv, bv, out):
             v_transposes(st, tr)
             v_quantise(st, v_copy(tr))
 
+        bias_all = const.tile([P, V], F32, name="bias_all")
+        for half in range(V // BANK):
+            cols = slice(half * BANK, (half + 1) * BANK)
+            bias_ps = bank("mm%d" % half)
+            nc.tensor.matmul(out=bias_ps[:], lhsT=ones_b[:], rhs=bias_row[:, cols], start=True, stop=True)
+            nc.scalar.copy(out=bias_all[:, cols], in_=bias_ps[:])
+
         w_codes = keep.tile([P, 2 * V], U32, name="w_codes", align_bytes=64)
         w_scales = keep.tile([P, 2 * V], U8, name="w_scales", align_bytes=64)
-        for G in range(H // K_PASS):
-            rows_t_c = w_raw[:, G * 4 * V : (G + 1) * 4 * V].rearrange("p (t c) -> p t c", t=4)
-            for half in range(V // BANK):
+        for half in range(V // BANK):
+            for G in range(H // K_PASS):
+                rows_t_c = w_raw[:, G * 4 * V : (G + 1) * 4 * V].rearrange("p (t c) -> p t c", t=4)
                 w_grouped = w_stage.tile([P, 4 * BANK], BF16, name="w_grouped", align_bytes=64)
-                regroup = nc.vector.tensor_copy if half == 0 else nc.scalar.copy
+                regroup = nc.vector.tensor_copy if G == 0 else nc.scalar.copy
                 regroup(
                     out=w_grouped[:].rearrange("p (c i t) -> p c t i", i=4, t=4),
                     in_=rows_t_c[:, :, half * BANK : (half + 1) * BANK].rearrange("p t (c i) -> p c t i", i=4),
@@ -188,13 +191,19 @@ def tile_interpretablemultiheadattention_pa_kernel(tc, qh, kh, v, Wv, bv, out):
 
         vv_codes = keep.tile([P, 2 * V], U32, name="vv_codes", align_bytes=64)
         vv_scales = keep.tile([P, 2 * V], U8, name="vv_scales", align_bytes=64)
-        UNITS = V // P
+        UNITS = (S // K_PASS) * (V // P)
+        unit_banks = {}
+        unit_grouped = {}
 
-        def value_passes(g, unit, vv_ps):
+        def value_passes(unit, bank_name):
+            g = unit // (V // P)
+            c0 = unit % (V // P) * P
+            vv_ps = bank(bank_name)
+            unit_banks[unit] = vv_ps
             for t in range(4):
                 for G in range(H // K_PASS):
                     lcols = slice(((4 * g + t) * 2 + G) * P, ((4 * g + t) * 2 + G + 1) * P)
-                    rcols = slice(G * V + unit * P, G * V + (unit + 1) * P)
+                    rcols = slice(G * V + c0, G * V + c0 + P)
                     nc.tensor.matmul_mx(
                         out=vv_ps[:, t * P : (t + 1) * P],
                         lhsT=v_codes[:, lcols].bitcast(FP8X4),
@@ -205,19 +214,28 @@ def tile_interpretablemultiheadattention_pa_kernel(tc, qh, kh, v, Wv, bv, out):
                         stop=(G == H // K_PASS - 1),
                     )
 
-        def value_add(unit, vv_ps, vv_grouped):
+        def value_add(unit):
+            if unit not in unit_banks:
+                return
             quarter = unit % 4
+            c0 = unit % (V // P) * P
+            if quarter == 0:
+                unit_grouped[unit // 4] = stage.tile([P, 4 * BANK], BF16, name="vv_grouped", align_bytes=64)
             nc.vector.tensor_tensor(
-                out=vv_grouped[:, quarter * 4 * P : (quarter + 1) * 4 * P].rearrange("p (c t) -> p c t", t=4),
-                in0=vv_ps[:].rearrange("p (t c) -> p c t", t=4),
-                in1=bias_all[:, unit * P : (unit + 1) * P].unsqueeze(2).to_broadcast([P, P, 4]),
+                out=unit_grouped[unit // 4][:, quarter * 4 * P : (quarter + 1) * 4 * P].rearrange(
+                    "p (c t) -> p c t", t=4
+                ),
+                in0=unit_banks[unit][:].rearrange("p (t c) -> p c t", t=4),
+                in1=bias_all[:, c0 : c0 + P].unsqueeze(2).to_broadcast([P, P, 4]),
                 op=ALU.add,
             )
 
-        def value_quantise(g, half, vv_grouped):
-            cols = slice(g * V + half * BANK, g * V + (half + 1) * BANK)
+        def value_quantise(unit):
+            if unit not in unit_banks or unit % 4 != 3:
+                return
+            cols = slice((unit // 4) * BANK, (unit // 4 + 1) * BANK)
             nc.vector.quantize_mx(
-                out=vv_codes[:, cols].bitcast(FP8X4), scales=vv_scales[:, cols], in_=vv_grouped[:]
+                out=vv_codes[:, cols].bitcast(FP8X4), scales=vv_scales[:, cols], in_=unit_grouped[unit // 4][:]
             )
 
         def first_qk(j):
@@ -226,17 +244,13 @@ def tile_interpretablemultiheadattention_pa_kernel(tc, qh, kh, v, Wv, bv, out):
                 qk_transposes(name, j, tr)
                 qk_copy(name, j, tr)
 
+        UNITS_AHEAD = 4
+        for unit in range(UNITS_AHEAD):
+            value_passes(unit, "mm%d" % unit)
+            value_add(unit)
+        value_quantise(UNITS_AHEAD - 1)
         first_qk(0)
-        for unit in range(UNITS):
-            if unit % 4 == 0:
-                vv_grouped = stage.tile([P, 4 * BANK], BF16, name="vv_grouped", align_bytes=64)
-            vv_ps = bank("mm%d" % (unit % 4))
-            value_passes(0, unit, vv_ps)
-            value_add(unit, vv_ps, vv_grouped)
-            if unit % 4 == 3:
-                value_quantise(0, unit // 4, vv_grouped)
-                if unit == 3:
-                    first_qk(1)
+        first_qk(1)
 
         blocks = [(qt, n) for qt in range(S_TILES) for n in range(NH)]
         LIGHT = TILES_PER_GROUP * NH
@@ -339,12 +353,14 @@ def tile_interpretablemultiheadattention_pa_kernel(tc, qh, kh, v, Wv, bv, out):
                     accum_out=sums[:, b : b + 1],
                 )
             e_tiles[i] = e_tile
-            if len(score_banks[i]) == 2:
-                total = stats.tile([P, 1], F32, name="total")
-                nc.gpsimd.tensor_tensor(out=total[:], in0=sums[:, 0:1], in1=sums[:, 1:2], op=ALU.add)
-                row_sums[i] = total
-            else:
-                row_sums[i] = sums
+            row_sums[i] = sums
+
+        def sum_of_sums(i):
+            if not live(i) or len(score_banks[i]) == 1:
+                return
+            total = stats.tile([P, 1], F32, name="total")
+            nc.vector.tensor_tensor(out=total[:], in0=row_sums[i][:, 0:1], in1=row_sums[i][:, 1:2], op=ALU.add)
+            row_sums[i] = total
 
         def reciprocal(i):
             if not live(i):
@@ -438,47 +454,36 @@ def tile_interpretablemultiheadattention_pa_kernel(tc, qh, kh, v, Wv, bv, out):
         for j in range(2, S_TILES):
             later_tiles.extend([("k", j), ("q", j)])
         assert len(later_tiles) == LIGHT
-        later_banks = {}
         later_grouped = {}
-        FIRST_UNIT_STEP = 6
-        unit_banks = {}
-        unit_grouped = {}
 
         for s in range(len(blocks) + LAG_OUT):
             store_out(s - LAG_OUT)
-            if s - 1 in later_banks:
-                name, idx = later_tiles[s - 1]
-                if name == "v":
-                    later_grouped[s - 1] = v_copy(later_banks[s - 1])
-                else:
-                    qk_copy(name, idx, later_banks[s - 1])
-            last_unit = s - 1 - FIRST_UNIT_STEP
-            if last_unit in unit_banks:
-                if last_unit % 4 == 0:
-                    unit_grouped[last_unit // 4] = stage.tile([P, 4 * BANK], BF16, name="vv_grouped", align_bytes=64)
-                value_add(last_unit, unit_banks[last_unit], unit_grouped[last_unit // 4])
+            if s > 0:
+                value_add(s - 1 + UNITS_AHEAD)
             copy_out(s - LAG_COPY)
+            sum_of_sums(s - LAG_NORM)
             quantise(s - LAG_QUANT)
             reciprocal(s - LAG_NORM)
             scores_first(s)
             maximum_first(s)
             exponentials(s - LAG_EXP)
             normalise(s - LAG_NORM)
-            if s - 2 in later_grouped:
-                v_quantise(later_tiles[s - 2][1], later_grouped[s - 2])
-            if last_unit in unit_banks and last_unit % 4 == 3:
-                value_quantise(1, last_unit // 4, unit_grouped[last_unit // 4])
+            if s - 1 in later_grouped:
+                v_quantise(later_tiles[s - 1][1], later_grouped[s - 1])
+            if s > 0:
+                value_quantise(s - 1 + UNITS_AHEAD)
             transposes(s - LAG_TRANSPOSE)
             if s < LIGHT:
                 name, idx = later_tiles[s]
-                later_banks[s] = bank("mm2")
+                tr = bank("mm2")
                 if name == "v":
-                    v_transposes(idx, later_banks[s])
+                    v_transposes(idx, tr)
+                    later_grouped[s] = v_copy(tr)
                 else:
-                    qk_transposes(name, idx, later_banks[s])
+                    qk_transposes(name, idx, tr)
+                    qk_copy(name, idx, tr)
             scores_second(s)
             maximum_second(s)
             weighted_sum(s - LAG_SUM)
-            if 0 <= s - FIRST_UNIT_STEP < UNITS:
-                unit_banks[s - FIRST_UNIT_STEP] = bank("mm3")
-                value_passes(1, s - FIRST_UNIT_STEP, unit_banks[s - FIRST_UNIT_STEP])
+            if s + UNITS_AHEAD < UNITS:
+                value_passes(s + UNITS_AHEAD, "mm3")

@@ -7,6 +7,7 @@ F32 = mybir.dt.float32
 BF16 = mybir.dt.bfloat16
 U32 = mybir.dt.uint32
 U8 = mybir.dt.uint8
+I32 = mybir.dt.int32
 FP8X4 = mybir.dt.float8_e4m3fn_x4
 ALU = mybir.AluOpType
 ACT = mybir.ActivationFunctionType
@@ -38,7 +39,7 @@ def tile_interpretablemultiheadattention_pa_kernel(tc, qh, kh, v, Wv, bv, out):
     with ExitStack() as ctx:
         const = ctx.enter_context(tc.tile_pool(name="const", bufs=1))
         keep = ctx.enter_context(tc.tile_pool(name="keep", bufs=1))
-        raw_qk = ctx.enter_context(tc.tile_pool(name="raw_qk", bufs=2 * S_TILES))
+        raw_qk = ctx.enter_context(tc.tile_pool(name="raw_qk", bufs=12))
         w_stage = ctx.enter_context(tc.tile_pool(name="w_stage", bufs=4))
         stage = ctx.enter_context(tc.tile_pool(name="stage", bufs=2))
         soft = ctx.enter_context(tc.tile_pool(name="soft", bufs=3))
@@ -73,17 +74,19 @@ def tile_interpretablemultiheadattention_pa_kernel(tc, qh, kh, v, Wv, bv, out):
         bias_row = const.tile([P, V], BF16, name="bias_row")
         nc.vector.memset(bias_row[:], 0.0)
 
-        p_tiles = []
-        for m in range(TILES_PER_GROUP):
-            pair = []
-            for b in range(2):
-                p_tile = keep.tile([P, 2 * K_PASS], BF16, name="p_%d_%d" % (m, b))
-                if m < TILES_PER_GROUP - 1:
-                    nc.vector.memset(p_tile[:, K_PASS + P * (m + 1) :], 0.0)
-                pair.append(p_tile)
-            p_tiles.append(pair)
+        p_two = []
+        for b in range(2):
+            p_tile = keep.tile([P, 2 * K_PASS], BF16, name="p_two%d" % b)
+            for u in range(2):
+                nc.vector.memset(p_tile[:, K_PASS + 256 * u + 192 : K_PASS + 256 * (u + 1)], 0.0)
+            p_two.append(p_tile)
         causal_b = const.tile([P, P], BF16, name="causal_b")
-        nc.vector.tensor_copy(out=causal_b[:], in_=causal_f[:])
+        nc.vector.tensor_copy(
+            out=causal_b[:].rearrange("p (u w e) -> p u w e", u=2, e=2),
+            in_=causal_f[:].rearrange("p (w u e) -> p u w e", u=2, e=2),
+        )
+        packed_scales = keep.tile([P, 4 * V], U8, name="packed_scales", align_bytes=64)
+        nc.gpsimd.memset(packed_scales[:].bitcast(U32), 0)
 
         rows_of = {
             "q": qh.rearrange("n o (j p) d -> j p (n o) d", p=P),
@@ -91,20 +94,22 @@ def tile_interpretablemultiheadattention_pa_kernel(tc, qh, kh, v, Wv, bv, out):
         }
         raw_of = {}
 
-        def load_qk(j):
-            for name in ("k", "q"):
-                raw = raw_qk.tile([P, NH * D], BF16, name="%s_raw%d" % (name, j), tag="raw_qk")
-                nc.sync.dma_start(out=raw[:].rearrange("p (n d) -> p n d", n=NH), in_=rows_of[name][j])
-                raw_of[(name, j)] = raw
+        def load_qk(name, j):
+            raw = raw_qk.tile([P, NH * D], BF16, name="%s_raw%d" % (name, j), tag="raw_qk")
+            nc.sync.dma_start(out=raw[:].rearrange("p (n d) -> p n d", n=NH), in_=rows_of[name][j])
+            raw_of[(name, j)] = raw
 
         w_raw = keep.tile([P, 4 * 2 * V], BF16, name="w_raw")
         w_rows = Wv.rearrange("(a p e) c -> a p e c", a=4, p=P, e=2)
         w_raw_aec = w_raw[:].rearrange("p (a e c) -> p a e c", a=4, e=2)
         v_raw = keep.tile([P, 4 * 2 * H], BF16, name="v_raw")
-        v_rows = v.rearrange("o (a p e) h -> (o a) p (e h)", a=4, p=P, e=2)
+        v_rows = v.rearrange("o (g p t) h -> (o g) p (t h)", p=P, t=4)
 
         def load_v(a):
-            nc.sync.dma_start(out=v_raw[:, a * 2 * H : (a + 1) * 2 * H], in_=v_rows[a])
+            g, pair = a // 2, a % 2
+            nc.sync.dma_start(
+                out=v_raw[:, a * 2 * H : (a + 1) * 2 * H], in_=v_rows[g][:, pair * 2 * H : (pair + 1) * 2 * H]
+            )
 
         load_v(0)
         load_v(1)
@@ -114,12 +119,14 @@ def tile_interpretablemultiheadattention_pa_kernel(tc, qh, kh, v, Wv, bv, out):
                 nc.sync.dma_start(out=w_raw_aec[:, a, :, cols], in_=w_rows[a][:, :, cols])
             if half == 0:
                 nc.sync.dma_start(out=bias_row[0:1, :], in_=bv.rearrange("(o c) -> o c", o=1))
-        load_qk(0)
-        load_qk(1)
+        first_tiles = [("k", 0), ("k", 1), ("k", 2), ("k", 3), ("q", 3), ("q", 2), ("q", 1), ("q", 0)]
+        later_qk = [("k", 4), ("k", 5), ("k", 6), ("k", 7), ("q", 7), ("q", 6), ("q", 5), ("q", 4)]
+        for name, j in first_tiles:
+            load_qk(name, j)
         load_v(2)
         load_v(3)
-        for j in range(2, S_TILES):
-            load_qk(j)
+        for name, j in later_qk:
+            load_qk(name, j)
 
         words_T = {"q": keep.tile([P, NH * S], F32, name="qT"), "k": keep.tile([P, NH * S], F32, name="kT")}
 
@@ -129,13 +136,19 @@ def tile_interpretablemultiheadattention_pa_kernel(tc, qh, kh, v, Wv, bv, out):
                 nc.tensor.transpose(tr[:, n * P : (n + 1) * P], words[:, n * P : (n + 1) * P], ident_f[:])
 
         def qk_copy(name, j, tr):
-            nc.scalar.copy(
-                out=words_T[name][:].rearrange("p (n s) -> p n s", n=NH)[:, :, j * P : (j + 1) * P],
-                in_=tr[:].rearrange("p (n s) -> p n s", n=NH),
-            )
+            if name == "q":
+                nc.scalar.copy(
+                    out=words_T["q"][:].rearrange("p (n s) -> p n s", n=NH)[:, :, j * P : (j + 1) * P],
+                    in_=tr[:].rearrange("p (n s) -> p n s", n=NH),
+                )
+            else:
+                nc.scalar.copy(
+                    out=words_T["k"][:, j * NH * P : (j + 1) * NH * P].rearrange("p (u x e) -> p u x e", u=2, e=2),
+                    in_=tr[:].rearrange("p (x u e) -> p u x e", u=2, e=2),
+                )
 
         qT_b = words_T["q"][:].bitcast(BF16).rearrange("p (n s e) -> p n s e", n=NH, e=2)
-        kT_b = words_T["k"][:].bitcast(BF16).rearrange("p (n s e) -> p n s e", n=NH, e=2)
+        kT_b = words_T["k"][:].bitcast(BF16).rearrange("p (j u n c e) -> p j u n c e", j=S_TILES, u=2, n=NH, e=2)
 
         v_codes = keep.tile([P, S_TILES * 2 * P], U32, name="v_codes", align_bytes=64)
         v_scales = keep.tile([P, S_TILES * 2 * P], U8, name="v_scales", align_bytes=64)
@@ -238,211 +251,346 @@ def tile_interpretablemultiheadattention_pa_kernel(tc, qh, kh, v, Wv, bv, out):
                 out=vv_codes[:, cols].bitcast(FP8X4), scales=vv_scales[:, cols], in_=unit_grouped[unit // 4][:]
             )
 
-        def first_qk(j):
-            for name, bank_name in (("k", "tr0"), ("q", "tr1")):
-                tr = bank(bank_name)
-                qk_transposes(name, j, tr)
-                qk_copy(name, j, tr)
+        def replicate(g):
+            cols = slice(g * V, (g + 1) * V)
+            for m in range(2):
+                codes = packed_codes[(g, m)]
+                scales = packed_scales[:, (2 * g + m) * V : (2 * g + m + 1) * V]
+                rows = 32 * (m + 1)
+                for r in range(0, P, rows):
+                    nc.sync.dma_start(out=codes[r : r + rows, :].bitcast(I32), in_=vv_codes[0:rows, cols].bitcast(I32))
+                for r in range(0, P, 32):
+                    src = r % rows
+                    nc.sync.dma_start(
+                        out=scales[r : r + 4, :].bitcast(I32), in_=vv_scales[src : src + 4, cols].bitcast(I32)
+                    )
+
+        packed_codes = {}
+        for g in range(2):
+            for m in range(2):
+                packed_codes[(g, m)] = keep.tile([P, V], U32, name="packed%d%d" % (g, m), align_bytes=64)
 
         UNITS_AHEAD = 4
         for unit in range(UNITS_AHEAD):
             value_passes(unit, "mm%d" % unit)
             value_add(unit)
         value_quantise(UNITS_AHEAD - 1)
-        first_qk(0)
-        first_qk(1)
+        for idx, (name, j) in enumerate(first_tiles):
+            tr = bank("tr%d" % (idx % 2))
+            qk_transposes(name, j, tr)
+            qk_copy(name, j, tr)
 
-        blocks = [(qt, n) for qt in range(S_TILES) for n in range(NH)]
-        LIGHT = TILES_PER_GROUP * NH
-        score_banks = {}
-        row_maxima = {}
+        HALF = K_PASS // 2
+        jobs = []
+        for qt in (3, 2, 1, 0, 7, 6, 5, 4):
+            m = qt % TILES_PER_GROUP
+            pack = {0: 4, 1: 2, 2: 1, 3: 1}[m]
+            heavy = qt >= TILES_PER_GROUP
+            if heavy:
+                for n in range(NH):
+                    jobs.append((qt, m, pack, True, [n]))
+            else:
+                for n in range(0, NH, pack):
+                    jobs.append((qt, m, pack, False, list(range(n, n + pack))))
+        LIGHT = 11
+        TILES_OF = {}
+        for qt in range(S_TILES):
+            m = qt % TILES_PER_GROUP
+            TILES_OF[qt] = {0: 1, 1: 2, 2: 4, 3: 4}[m] + (NH if qt >= TILES_PER_GROUP else 0)
+
+        diag_bank = {}
+        full_bank = {}
+        diag_max = {}
         shifts = {}
-        e_tiles = {}
-        row_sums = {}
+        e_full = {}
+        e_diag = {}
+        sums_of = {}
         recips = {}
+        p_full = {}
+        p_diag = {}
         tr_banks = {}
         p_groupeds = {}
         p_operands = {}
         acc = {}
+        done = {}
 
         def live(i):
-            return 0 <= i < len(blocks)
+            return 0 <= i < len(jobs)
 
-        def shape_of(i):
-            qt, n = blocks[i]
-            diag_group = qt // TILES_PER_GROUP
-            m = qt % TILES_PER_GROUP
-            diag_cols = P * (m + 1)
-            return qt, n, diag_group, m, diag_cols
+        def diag_key(i):
+            qt, m, pack, heavy, heads = jobs[i]
+            return (qt, heads[0] // pack)
 
-        def score_matmul(i, sc, k0, width, e, start, stop):
-            qt, n = blocks[i]
-            nc.tensor.matmul(
-                out=sc[:, :width],
-                lhsT=qT_b[:, n, qt * P : (qt + 1) * P, e],
-                rhs=kT_b[:, n, k0 : k0 + width, e],
-                start=start,
-                stop=stop,
-            )
+        def opens(i):
+            qt, m, pack, heavy, heads = jobs[i]
+            return heads[0] % pack == 0
+
+        def closes(i):
+            qt, m, pack, heavy, heads = jobs[i]
+            return heads[-1] % pack == pack - 1
+
+        def diag_heads(i):
+            qt, m, pack, heavy, heads = jobs[i]
+            n0 = heads[0] // pack * pack
+            return list(range(n0, n0 + pack))
+
+        def score_calls(i):
+            qt, m, pack, heavy, heads = jobs[i]
+            calls = []
+            if heavy:
+                sc = bank("mm%d" % (2 * (i % 2) + 1))
+                full_bank[i] = sc
+                for e in range(2):
+                    calls.append((
+                        sc[:].rearrange("p (u j c) -> p u j c", u=2, c=64),
+                        qT_b[:, heads[0], qt * P : (qt + 1) * P, e],
+                        kT_b[:, 0:TILES_PER_GROUP, :, heads[0], :, e].rearrange("p j u c -> p u j c"),
+                        e == 0,
+                        e == 1,
+                    ))
+            n_first = len(calls)
+            if opens(i):
+                if heavy:
+                    name = "mm%d" % (2 * ((i + (heads[0] // 2 if pack == 2 else 0)) % 2))
+                else:
+                    name = "mm%d" % (i % 2)
+                sc = bank(name)
+                diag_bank[diag_key(i)] = sc
+                width = P * (m + 1)
+                j0 = qt // TILES_PER_GROUP * TILES_PER_GROUP
+                for h, n in enumerate(diag_heads(i)):
+                    region = sc[:, h * width : (h + 1) * width].rearrange("p (u x) -> p u x", u=2)
+                    for e in range(2):
+                        calls.append((
+                            region.rearrange("p u (j c) -> p u j c", c=64),
+                            qT_b[:, n, qt * P : (qt + 1) * P, e],
+                            kT_b[:, j0 : j0 + m + 1, :, n, :, e].rearrange("p j u c -> p u j c"),
+                            e == 0,
+                            False,
+                        ))
+                    calls.append((
+                        region[:, :, 64 * m : 64 * (m + 1)],
+                        ident_b[:],
+                        causal_b[:].rearrange("p (u c) -> p u c", u=2),
+                        False,
+                        True,
+                    ))
+            if not heavy:
+                n_first = len(calls) // 2
+            return calls[:n_first], calls[n_first:]
+
+        second_calls = {}
+
+        def emit(calls):
+            for out_ap, lhsT, rhs, start, stop in calls:
+                nc.tensor.matmul(out=out_ap, lhsT=lhsT, rhs=rhs, start=start, stop=stop)
 
         def scores_first(i):
-            if not live(i):
-                return
-            qt, n, diag_group, m, diag_cols = shape_of(i)
-            if diag_group == 1:
-                sc_full = bank("mm%d" % (2 * (i % 2)))
-                sc_diag = bank("mm%d" % (2 * (i % 2) + 1))
-                score_matmul(i, sc_full, 0, K_PASS, 0, True, False)
-                score_matmul(i, sc_full, 0, K_PASS, 1, False, True)
-                score_banks[i] = [(sc_full, K_PASS, 0), (sc_diag, diag_cols, K_PASS)]
-            else:
-                sc_diag = bank("mm%d" % (i % 2))
-                score_matmul(i, sc_diag, 0, diag_cols, 0, True, False)
-                score_banks[i] = [(sc_diag, diag_cols, K_PASS)]
+            if live(i):
+                first, second_calls[i] = score_calls(i)
+                emit(first)
 
         def scores_second(i):
-            if not live(i):
-                return
-            qt, n, diag_group, m, diag_cols = shape_of(i)
-            sc_diag = score_banks[i][-1][0]
-            if diag_group == 1:
-                score_matmul(i, sc_diag, K_PASS, diag_cols, 0, True, False)
-            score_matmul(i, sc_diag, diag_group * K_PASS, diag_cols, 1, False, False)
-            nc.tensor.matmul(
-                out=sc_diag[:, diag_cols - P : diag_cols], lhsT=ident_b[:], rhs=causal_b[:], start=False, stop=True
-            )
+            if live(i):
+                emit(second_calls[i])
+
+        full_max = {}
 
         def maximum_first(i):
-            if not live(i):
-                return
-            row_maxima[i] = stats.tile([P, 2], F32, name="row_max")
-            if len(score_banks[i]) == 2:
-                sc_full = score_banks[i][0][0]
-                nc.vector.reduce_max(out=row_maxima[i][:, 1:2], in_=sc_full[:], axis=AXIS.X)
+            if live(i) and jobs[i][3]:
+                full_max[i] = stats.tile([P, 1], F32, name="full_max")
+                nc.vector.reduce_max(out=full_max[i][:], in_=full_bank[i][:], axis=AXIS.X)
 
         def maximum_second(i):
             if not live(i):
                 return
-            sc_diag, width, col = score_banks[i][-1]
-            row_max = row_maxima[i]
-            nc.vector.reduce_max(out=row_max[:, 0:1], in_=sc_diag[:, :width], axis=AXIS.X)
-            shift = stats.tile([P, 1], F32, name="shift")
-            if len(score_banks[i]) == 2:
+            qt, m, pack, heavy, heads = jobs[i]
+            key = diag_key(i)
+            if opens(i):
+                diag_max[key] = stats.tile([P, pack], F32, name="diag_max%d" % pack)
+                width = P * (m + 1)
+                nc.vector.reduce_max(
+                    out=diag_max[key][:],
+                    in_=diag_bank[key][:, : pack * width].rearrange("p (h x) -> p h x", h=pack),
+                    axis=AXIS.X,
+                )
+            if heavy:
+                h = heads[0] % pack
+                shift = stats.tile([P, 1], F32, name="shift")
                 nc.gpsimd.tensor_scalar(
-                    out=shift[:], in0=row_max[:, 0:1], scalar1=row_max[:, 1:2], scalar2=-SCALE,
+                    out=shift[:], in0=diag_max[key][:, h : h + 1], scalar1=full_max[i][:], scalar2=-SCALE,
                     op0=ALU.max, op1=ALU.mult,
                 )
             else:
+                shift = stats.tile([P, pack], F32, name="shift%d" % pack)
                 nc.gpsimd.tensor_scalar(
-                    out=shift[:], in0=row_max[:, 0:1], scalar1=-SCALE, scalar2=0.0, op0=ALU.mult, op1=ALU.add
+                    out=shift[:], in0=diag_max[key][:], scalar1=-SCALE, scalar2=0.0, op0=ALU.mult, op1=ALU.add
                 )
             shifts[i] = shift
+
+        def diag_region(tile_ap, i, h):
+            m = jobs[i][1]
+            c = 64 * (m + 1)
+            return tile_ap.rearrange("p (u x) -> p u x", u=2)[:, :, h * c : (h + 1) * c]
 
         def exponentials(i):
             if not live(i):
                 return
-            e_tile = soft.tile([P, 2 * K_PASS], F32, name="e_tile")
-            sums = stats.tile([P, 2], F32, name="sums")
-            for b, (sc, width, col) in enumerate(score_banks[i]):
+            qt, m, pack, heavy, heads = jobs[i]
+            key = diag_key(i)
+            width = P * (m + 1)
+            if pack == 1:
+                e_tile = soft.tile([P, 2 * K_PASS], F32, name="e_tile")
+                e_full[i] = e_tile[:, :K_PASS]
+                e_diag[key] = e_tile[:, K_PASS:]
+            else:
+                if heavy:
+                    e_tile = soft.tile([P, K_PASS], F32, name="e_full")
+                    e_full[i] = e_tile[:]
+                if opens(i):
+                    e_tile = soft.tile([P, K_PASS], F32, name="e_diag")
+                    e_diag[key] = e_tile[:]
+            sums = stats.tile([P, 4], F32, name="sums")
+            if heavy:
                 nc.scalar.activation(
-                    out=e_tile[:, col : col + width],
-                    in_=sc[:, :width],
+                    out=e_full[i], in_=full_bank[i][:], func=ACT.Exp, bias=shifts[i][:], scale=SCALE,
+                    accum_out=sums[:, 1:2],
+                )
+            for b, n in enumerate(heads):
+                h = n % pack
+                nc.scalar.activation(
+                    out=diag_region(e_diag[key], i, h),
+                    in_=diag_bank[key][:, h * width : (h + 1) * width].rearrange("p (u x) -> p u x", u=2),
                     func=ACT.Exp,
-                    bias=shifts[i][:],
+                    bias=shifts[i][:, b : b + 1],
                     scale=SCALE,
                     accum_out=sums[:, b : b + 1],
                 )
-            e_tiles[i] = e_tile
-            row_sums[i] = sums
+            sums_of[i] = sums
 
         def sum_of_sums(i):
-            if not live(i) or len(score_banks[i]) == 1:
-                return
-            total = stats.tile([P, 1], F32, name="total")
-            nc.vector.tensor_tensor(out=total[:], in0=row_sums[i][:, 0:1], in1=row_sums[i][:, 1:2], op=ALU.add)
-            row_sums[i] = total
+            if live(i) and jobs[i][3]:
+                total = stats.tile([P, 1], F32, name="total")
+                nc.vector.tensor_tensor(out=total[:], in0=sums_of[i][:, 0:1], in1=sums_of[i][:, 1:2], op=ALU.add)
+                sums_of[i] = total
 
         def reciprocal(i):
-            if not live(i):
-                return
-            recips[i] = stats.tile([P, 1], F32, name="recip")
-            nc.vector.reciprocal(out=recips[i][:], in_=row_sums[i][:, 0:1])
+            if live(i):
+                count = len(jobs[i][4])
+                recips[i] = stats.tile([P, count], F32, name="recip%d" % count)
+                nc.vector.reciprocal(out=recips[i][:], in_=sums_of[i][:, :count])
 
         def normalise(i):
             if not live(i):
                 return
-            qt, n, diag_group, m, diag_cols = shape_of(i)
-            used = slice(K_PASS * (1 - diag_group), K_PASS + diag_cols)
-            nc.vector.tensor_scalar(
-                out=p_tiles[m][n % 2][:, used], in0=e_tiles[i][:, used], scalar1=recips[i][:], scalar2=None,
-                op0=ALU.mult,
-            )
+            qt, m, pack, heavy, heads = jobs[i]
+            key = diag_key(i)
+            if m == 2:
+                p_tile = p_two[i % 2]
+                p_full[i] = p_tile[:, :K_PASS]
+                p_diag[key] = p_tile[:, K_PASS:]
+            elif pack == 1:
+                p_tile = soft.tile([P, 2 * K_PASS], BF16, name="p_tile")
+                p_full[i] = p_tile[:, :K_PASS]
+                p_diag[key] = p_tile[:, K_PASS:]
+            else:
+                if heavy:
+                    p_tile = soft.tile([P, K_PASS], BF16, name="p_full")
+                    p_full[i] = p_tile[:]
+                if opens(i):
+                    p_tile = soft.tile([P, K_PASS], BF16, name="p_diag")
+                    p_diag[key] = p_tile[:]
+            if heavy:
+                nc.vector.tensor_scalar(
+                    out=p_full[i], in0=e_full[i], scalar1=recips[i][:], scalar2=None, op0=ALU.mult
+                )
+            for b, n in enumerate(heads):
+                h = n % pack
+                nc.vector.tensor_scalar(
+                    out=diag_region(p_diag[key], i, h), in0=diag_region(e_diag[key], i, h),
+                    scalar1=recips[i][:, b : b + 1], scalar2=None, op0=ALU.mult,
+                )
+
+        def tiles_of(i):
+            qt, m, pack, heavy, heads = jobs[i]
+            g = qt // TILES_PER_GROUP
+            tiles = []
+            if heavy:
+                tiles.append((p_full[i], vv_codes, vv_scales, 0))
+            if closes(i):
+                if pack == 1:
+                    tiles.append((p_diag[diag_key(i)], vv_codes, vv_scales, g * V))
+                else:
+                    tiles.append(
+                        (p_diag[diag_key(i)], packed_codes[(g, m)], packed_scales[:, (2 * g + m) * V : (2 * g + m + 1) * V], 0)
+                    )
+            return tiles
 
         def transposes(i):
             if not live(i):
                 return
-            qt, n, diag_group, m, diag_cols = shape_of(i)
-            p_words = p_tiles[m][n % 2][:].bitcast(F32)
-            w0 = K_PASS * (1 - diag_group) // 2
             tr = bank("tr%d" % (i % 2))
-            for b in range(2 * (diag_group + 1)):
-                nc.tensor.transpose(
-                    tr[:, b * P : (b + 1) * P], p_words[:, w0 + b * P : w0 + (b + 1) * P], ident_f[:]
-                )
+            for slot, tile in enumerate(tiles_of(i)):
+                p_words = tile[0].bitcast(F32)
+                for u in range(2):
+                    nc.tensor.transpose(
+                        tr[:, (2 * slot + u) * P : (2 * slot + u + 1) * P], p_words[:, u * P : (u + 1) * P], ident_f[:]
+                    )
             tr_banks[i] = tr
 
         def copy_out(i):
             if not live(i):
                 return
-            n_groups = shape_of(i)[2] + 1
+            n_tiles = len(tiles_of(i))
             p_grouped = soft.tile([P, 2 * K_PASS], BF16, name="p_grouped", align_bytes=64)
             nc.scalar.copy(
-                out=p_grouped[:].bitcast(F32)[:, : n_groups * 2 * P].rearrange(
-                    "p (g q u) -> p g q u", g=n_groups, u=2
+                out=p_grouped[:].bitcast(F32)[:, : n_tiles * 2 * P].rearrange(
+                    "p (g q u) -> p g q u", g=n_tiles, u=2
                 ),
-                in_=tr_banks[i][:, : n_groups * 2 * P].rearrange("p (g u q) -> p g q u", g=n_groups, u=2),
+                in_=tr_banks[i][:, : n_tiles * 2 * P].rearrange("p (g u q) -> p g q u", g=n_tiles, u=2),
             )
             p_groupeds[i] = p_grouped
 
         def quantise(i):
             if not live(i):
                 return
-            n_groups = shape_of(i)[2] + 1
+            n_tiles = len(tiles_of(i))
             p_codes = soft.tile([P, 2 * P], U32, name="p_codes", align_bytes=64)
             p_scales = soft.tile([P, 2 * P], U8, name="p_scales", align_bytes=64)
             nc.vector.quantize_mx(
-                out=p_codes[:, : n_groups * P].bitcast(FP8X4),
-                scales=p_scales[:, : n_groups * P],
-                in_=p_groupeds[i][:, : n_groups * K_PASS],
+                out=p_codes[:, : n_tiles * P].bitcast(FP8X4),
+                scales=p_scales[:, : n_tiles * P],
+                in_=p_groupeds[i][:, : n_tiles * K_PASS],
             )
             p_operands[i] = (p_codes, p_scales)
 
         def weighted_sum(i):
             if not live(i):
                 return
-            qt, n, diag_group, m, diag_cols = shape_of(i)
-            n_groups = diag_group + 1
+            qt = jobs[i][0]
             p_codes, p_scales = p_operands[i]
-            if n == 0:
+            if qt not in acc:
                 acc[qt] = [bank("acc%d" % half) for half in range(V // BANK)]
-            for group in range(n_groups):
-                lcols = slice(group * P, (group + 1) * P)
+                done[qt] = 0
+            for slot, (p_ap, codes, scales, c0) in enumerate(tiles_of(i)):
+                lcols = slice(slot * P, (slot + 1) * P)
                 for half in range(V // BANK):
-                    rcols = slice(group * V + half * BANK, group * V + (half + 1) * BANK)
+                    rcols = slice(c0 + half * BANK, c0 + (half + 1) * BANK)
                     nc.tensor.matmul_mx(
                         out=acc[qt][half][:],
                         lhsT=p_codes[:, lcols].bitcast(FP8X4),
                         lhsT_scale=p_scales[:, lcols],
-                        rhs=vv_codes[:, rcols].bitcast(FP8X4),
-                        rhs_scale=vv_scales[:, rcols],
-                        start=(n == 0 and group == 0),
-                        stop=(n == NH - 1 and group == n_groups - 1),
+                        rhs=codes[:, rcols].bitcast(FP8X4),
+                        rhs_scale=scales[:, rcols],
+                        start=(done[qt] == 0),
+                        stop=(done[qt] == TILES_OF[qt] - 1),
                     )
+                done[qt] += 1
 
         def store_out(i):
-            if not live(i) or blocks[i][1] != NH - 1:
+            if not live(i) or jobs[i][4][-1] != NH - 1:
                 return
-            qt = blocks[i][0]
+            qt = jobs[i][0]
             o_tile = stage.tile([P, V], F32, name="o_tile")
             nc.scalar.mul(out=o_tile[:, :BANK], in_=acc[qt][0][:], mul=1.0 / NH)
             nc.vector.tensor_scalar(
@@ -450,13 +598,10 @@ def tile_interpretablemultiheadattention_pa_kernel(tc, qh, kh, v, Wv, bv, out):
             )
             nc.sync.dma_start(out=out[0, qt * P : (qt + 1) * P, :], in_=o_tile[:])
 
-        later_tiles = [("v", st) for st in range(4, S_TILES)]
-        for j in range(2, S_TILES):
-            later_tiles.extend([("k", j), ("q", j)])
-        assert len(later_tiles) == LIGHT
+        later_tiles = [("v", st) for st in range(4, S_TILES)] + later_qk
         later_grouped = {}
 
-        for s in range(len(blocks) + LAG_OUT):
+        for s in range(len(jobs) + LAG_OUT):
             store_out(s - LAG_OUT)
             if s > 0:
                 value_add(s - 1 + UNITS_AHEAD)
@@ -472,10 +617,13 @@ def tile_interpretablemultiheadattention_pa_kernel(tc, qh, kh, v, Wv, bv, out):
                 v_quantise(later_tiles[s - 1][1], later_grouped[s - 1])
             if s > 0:
                 value_quantise(s - 1 + UNITS_AHEAD)
+                for g in range(2):
+                    if s - 1 + UNITS_AHEAD == 8 * g + 7:
+                        replicate(g)
             transposes(s - LAG_TRANSPOSE)
-            if s < LIGHT:
+            if s < len(later_tiles):
                 name, idx = later_tiles[s]
-                tr = bank("mm2")
+                tr = bank("mm2" if s < LIGHT else "mm0")
                 if name == "v":
                     v_transposes(idx, tr)
                     later_grouped[s] = v_copy(tr)
@@ -486,4 +634,4 @@ def tile_interpretablemultiheadattention_pa_kernel(tc, qh, kh, v, Wv, bv, out):
             maximum_second(s)
             weighted_sum(s - LAG_SUM)
             if s + UNITS_AHEAD < UNITS:
-                value_passes(s + UNITS_AHEAD, "mm3")
+                value_passes(s + UNITS_AHEAD, "mm3" if s < LIGHT else "mm1")

@@ -130,6 +130,8 @@ def tile_interpretablemultiheadattention_pa_kernel(tc, qh, kh, v, Wv, bv, out):
 
         words_T = {"q": keep.tile([P, NH * S], F32, name="qT"), "k": keep.tile([P, NH * S], F32, name="kT")}
 
+        kT_words = words_T["k"][:].rearrange("p (g n u j c) -> p g n u j c", g=2, n=NH, u=2, j=4)
+
         def qk_transposes(name, j, tr):
             words = raw_of[(name, j)][:].bitcast(F32)
             for n in range(NH):
@@ -142,13 +144,16 @@ def tile_interpretablemultiheadattention_pa_kernel(tc, qh, kh, v, Wv, bv, out):
                     in_=tr[:].rearrange("p (n s) -> p n s", n=NH),
                 )
             else:
-                nc.scalar.copy(
-                    out=words_T["k"][:, j * NH * P : (j + 1) * NH * P].rearrange("p (u x e) -> p u x e", u=2, e=2),
-                    in_=tr[:].rearrange("p (x u e) -> p u x e", u=2, e=2),
-                )
+                for u in range(2):
+                    nc.scalar.copy(
+                        out=kT_words[:, j // 4, :, u, j % 4, :].rearrange("p n (w e) -> p n w e", e=2),
+                        in_=tr[:].rearrange("p (n w u e) -> p n w u e", n=NH, u=2, e=2)[:, :, :, u, :],
+                    )
 
         qT_b = words_T["q"][:].bitcast(BF16).rearrange("p (n s e) -> p n s e", n=NH, e=2)
-        kT_b = words_T["k"][:].bitcast(BF16).rearrange("p (j u n c e) -> p j u n c e", j=S_TILES, u=2, n=NH, e=2)
+        kT_b = words_T["k"][:].bitcast(BF16).rearrange(
+            "p (g n u x e) -> p g n u x e", g=2, n=NH, u=2, e=2
+        )
 
         v_codes = keep.tile([P, S_TILES * 2 * P], U32, name="v_codes", align_bytes=64)
         v_scales = keep.tile([P, S_TILES * 2 * P], U8, name="v_scales", align_bytes=64)
@@ -342,9 +347,9 @@ def tile_interpretablemultiheadattention_pa_kernel(tc, qh, kh, v, Wv, bv, out):
                 full_bank[i] = sc
                 for e in range(2):
                     calls.append((
-                        sc[:].rearrange("p (u j c) -> p u j c", u=2, c=64),
+                        sc[:].rearrange("p (u x) -> p u x", u=2),
                         qT_b[:, heads[0], qt * P : (qt + 1) * P, e],
-                        kT_b[:, 0:TILES_PER_GROUP, :, heads[0], :, e].rearrange("p j u c -> p u j c"),
+                        kT_b[:, 0, heads[0], :, :, e],
                         e == 0,
                         e == 1,
                     ))
@@ -357,14 +362,13 @@ def tile_interpretablemultiheadattention_pa_kernel(tc, qh, kh, v, Wv, bv, out):
                 sc = bank(name)
                 diag_bank[diag_key(i)] = sc
                 width = P * (m + 1)
-                j0 = qt // TILES_PER_GROUP * TILES_PER_GROUP
                 for h, n in enumerate(diag_heads(i)):
                     region = sc[:, h * width : (h + 1) * width].rearrange("p (u x) -> p u x", u=2)
                     for e in range(2):
                         calls.append((
-                            region.rearrange("p u (j c) -> p u j c", c=64),
+                            region,
                             qT_b[:, n, qt * P : (qt + 1) * P, e],
-                            kT_b[:, j0 : j0 + m + 1, :, n, :, e].rearrange("p j u c -> p u j c"),
+                            kT_b[:, qt // TILES_PER_GROUP, n, :, : 64 * (m + 1), e],
                             e == 0,
                             False,
                         ))

@@ -29,7 +29,7 @@ LAG_EXP = 1
 LAG_NORM = 2
 LAG_TRANSPOSE = 3
 LAG_COPY = 4
-LAG_QUANT = 5
+
 LAG_SUM = 6
 LAG_OUT = 7
 
@@ -39,10 +39,11 @@ def tile_interpretablemultiheadattention_pa_kernel(tc, qh, kh, v, Wv, bv, out):
     with ExitStack() as ctx:
         const = ctx.enter_context(tc.tile_pool(name="const", bufs=1))
         keep = ctx.enter_context(tc.tile_pool(name="keep", bufs=1))
-        raw_qk = ctx.enter_context(tc.tile_pool(name="raw_qk", bufs=12))
+        raw_qk = ctx.enter_context(tc.tile_pool(name="raw_qk", bufs=10))
         w_stage = ctx.enter_context(tc.tile_pool(name="w_stage", bufs=4))
         stage = ctx.enter_context(tc.tile_pool(name="stage", bufs=2))
         soft = ctx.enter_context(tc.tile_pool(name="soft", bufs=3))
+        light = ctx.enter_context(tc.tile_pool(name="light", bufs=8))
         stats = ctx.enter_context(tc.tile_pool(name="stats", bufs=6))
         psum = ctx.enter_context(tc.psum_pool(name="psum", bufs=1))
         ctx.enter_context(tc.manual_schedule())
@@ -69,10 +70,7 @@ def tile_interpretablemultiheadattention_pa_kernel(tc, qh, kh, v, Wv, bv, out):
         warm_out = const.tile([P, 1], F32, name="warm_out")
         nc.vector.memset(warm_in[:], 0.0)
         nc.scalar.activation(out=warm_out[:], in_=warm_in[:], func=ACT.Exp)
-        ones_b = const.tile([P, P], BF16, name="ones_b")
-        nc.vector.memset(ones_b[:], 1.0)
-        bias_row = const.tile([P, V], BF16, name="bias_row")
-        nc.vector.memset(bias_row[:], 0.0)
+        bias_all = const.tile([P, V], BF16, name="bias_all")
 
         p_two = []
         for b in range(2):
@@ -89,15 +87,15 @@ def tile_interpretablemultiheadattention_pa_kernel(tc, qh, kh, v, Wv, bv, out):
         nc.gpsimd.memset(packed_scales[:].bitcast(U32), 0)
 
         rows_of = {
-            "q": qh.rearrange("n o (j p) d -> j p (n o) d", p=P),
-            "k": kh.rearrange("n o (j p) d -> j p (n o) d", p=P),
+            "q": qh.rearrange("n o (g p t) d -> (n o) g p (t d)", p=P, t=4),
+            "k": kh.rearrange("n o (g p t) d -> (n o) g p (t d)", p=P, t=4),
         }
         raw_of = {}
 
-        def load_qk(name, j):
-            raw = raw_qk.tile([P, NH * D], BF16, name="%s_raw%d" % (name, j), tag="raw_qk")
-            nc.sync.dma_start(out=raw[:].rearrange("p (n d) -> p n d", n=NH), in_=rows_of[name][j])
-            raw_of[(name, j)] = raw
+        def load_qk(name, n, g):
+            raw = raw_qk.tile([P, 4 * D], BF16, name="%s_raw%d%d" % (name, n, g), tag="raw_qk")
+            nc.sync.dma_start(out=raw[:], in_=rows_of[name][n, g])
+            raw_of[(name, n, g)] = raw
 
         w_raw = keep.tile([P, 4 * 2 * V], BF16, name="w_raw")
         w_rows = Wv.rearrange("(a p e) c -> a p e c", a=4, p=P, e=2)
@@ -111,49 +109,46 @@ def tile_interpretablemultiheadattention_pa_kernel(tc, qh, kh, v, Wv, bv, out):
                 out=v_raw[:, a * 2 * H : (a + 1) * 2 * H], in_=v_rows[g][:, pair * 2 * H : (pair + 1) * 2 * H]
             )
 
+        for n in range(2):
+            load_qk("k", n, 0)
+            load_qk("q", n, 0)
         load_v(0)
         load_v(1)
+        for n in range(2, NH):
+            load_qk("k", n, 0)
+            load_qk("q", n, 0)
         for half in range(V // BANK):
             cols = slice(half * BANK, (half + 1) * BANK)
             for a in range(4):
                 nc.sync.dma_start(out=w_raw_aec[:, a, :, cols], in_=w_rows[a][:, :, cols])
-            if half == 0:
-                nc.sync.dma_start(out=bias_row[0:1, :], in_=bv.rearrange("(o c) -> o c", o=1))
-        first_tiles = [("k", 0), ("k", 1), ("k", 2), ("k", 3), ("q", 3), ("q", 2), ("q", 1), ("q", 0)]
-        later_qk = [("k", 4), ("k", 5), ("k", 6), ("k", 7), ("q", 7), ("q", 6), ("q", 5), ("q", 4)]
-        for name, j in first_tiles:
-            load_qk(name, j)
+        nc.sync.dma_start(out=bias_all[:], in_=bv.partition_broadcast(P))
         load_v(2)
         load_v(3)
-        for name, j in later_qk:
-            load_qk(name, j)
-
+        for n in range(NH):
+            load_qk("k", n, 1)
+            load_qk("q", n, 1)
         words_T = {"q": keep.tile([P, NH * S], F32, name="qT"), "k": keep.tile([P, NH * S], F32, name="kT")}
 
-        kT_words = words_T["k"][:].rearrange("p (g n u j c) -> p g n u j c", g=2, n=NH, u=2, j=4)
+        def qk_transposes(name, n, g, tr):
+            words = raw_of[(name, n, g)][:].bitcast(F32)
+            for t in range(4):
+                nc.tensor.transpose(tr[:, t * P : (t + 1) * P], words[:, t * P : (t + 1) * P], ident_f[:])
 
-        def qk_transposes(name, j, tr):
-            words = raw_of[(name, j)][:].bitcast(F32)
-            for n in range(NH):
-                nc.tensor.transpose(tr[:, n * P : (n + 1) * P], words[:, n * P : (n + 1) * P], ident_f[:])
-
-        def qk_copy(name, j, tr):
+        def qk_copy(name, n, g, tr, copy):
+            out_words = words_T[name][:, (n * 2 + g) * K_PASS : (n * 2 + g + 1) * K_PASS]
             if name == "q":
-                nc.scalar.copy(
-                    out=words_T["q"][:].rearrange("p (n s) -> p n s", n=NH)[:, :, j * P : (j + 1) * P],
-                    in_=tr[:].rearrange("p (n s) -> p n s", n=NH),
+                copy(
+                    out=out_words.rearrange("p (s t) -> p s t", t=4),
+                    in_=tr[:].rearrange("p (t s) -> p s t", t=4),
                 )
             else:
-                for u in range(2):
-                    nc.scalar.copy(
-                        out=kT_words[:, j // 4, :, u, j % 4, :].rearrange("p n (w e) -> p n w e", e=2),
-                        in_=tr[:].rearrange("p (n w u e) -> p n w u e", n=NH, u=2, e=2)[:, :, :, u, :],
-                    )
+                copy(
+                    out=out_words.rearrange("p (u s e) -> p u s e", u=2, e=2),
+                    in_=tr[:].rearrange("p (u e s) -> p u s e", u=2, e=2),
+                )
 
         qT_b = words_T["q"][:].bitcast(BF16).rearrange("p (n s e) -> p n s e", n=NH, e=2)
-        kT_b = words_T["k"][:].bitcast(BF16).rearrange(
-            "p (g n u x e) -> p g n u x e", g=2, n=NH, u=2, e=2
-        )
+        kT_b = words_T["k"][:].bitcast(BF16).rearrange("p (n g u x e) -> p g n u x e", g=2, n=NH, u=2, e=2)
 
         v_codes = keep.tile([P, S_TILES * 2 * P], U32, name="v_codes", align_bytes=64)
         v_scales = keep.tile([P, S_TILES * 2 * P], U8, name="v_scales", align_bytes=64)
@@ -179,32 +174,31 @@ def tile_interpretablemultiheadattention_pa_kernel(tc, qh, kh, v, Wv, bv, out):
             cols = slice(st * 2 * P, (st + 1) * 2 * P)
             nc.vector.quantize_mx(out=v_codes[:, cols].bitcast(FP8X4), scales=v_scales[:, cols], in_=v_grouped[:])
 
-        for st, name in enumerate(("tr0", "tr1", "mm2", "mm3")):
-            tr = bank(name)
-            v_transposes(st, tr)
-            v_quantise(st, v_copy(tr))
-
-        bias_all = const.tile([P, V], F32, name="bias_all")
-        for half in range(V // BANK):
-            cols = slice(half * BANK, (half + 1) * BANK)
-            bias_ps = bank("mm%d" % half)
-            nc.tensor.matmul(out=bias_ps[:], lhsT=ones_b[:], rhs=bias_row[:, cols], start=True, stop=True)
-            nc.scalar.copy(out=bias_all[:, cols], in_=bias_ps[:])
-
         w_codes = keep.tile([P, 2 * V], U32, name="w_codes", align_bytes=64)
         w_scales = keep.tile([P, 2 * V], U8, name="w_scales", align_bytes=64)
-        for half in range(V // BANK):
-            for G in range(H // K_PASS):
+        w_groupeds = {}
+
+        def regroup_w(half, G, engine, piece, pieces):
+            if True:
                 rows_t_c = w_raw[:, G * 4 * V : (G + 1) * 4 * V].rearrange("p (t c) -> p t c", t=4)
-                w_grouped = w_stage.tile([P, 4 * BANK], BF16, name="w_grouped", align_bytes=64)
-                regroup = nc.vector.tensor_copy if G == 0 else nc.scalar.copy
+                if piece == 0:
+                    w_grouped = w_stage.tile([P, 4 * BANK], BF16, name="w_grouped", align_bytes=64)
+                    w_groupeds[(half, G)] = w_grouped
+                regroup = {"v": nc.vector.tensor_copy, "s": nc.scalar.copy, "g": nc.gpsimd.tensor_copy}[engine]
+                width = BANK // pieces
+                c0 = half * BANK + piece * width
                 regroup(
-                    out=w_grouped[:].rearrange("p (c i t) -> p c t i", i=4, t=4),
-                    in_=rows_t_c[:, :, half * BANK : (half + 1) * BANK].rearrange("p t (c i) -> p c t i", i=4),
+                    out=w_groupeds[(half, G)][:, 4 * piece * width : 4 * (piece + 1) * width].rearrange(
+                        "p (c i t) -> p c t i", i=4, t=4
+                    ),
+                    in_=rows_t_c[:, :, c0 : c0 + width].rearrange("p t (c i) -> p c t i", i=4),
                 )
+
+        def quantise_w(half):
+            for G in range(H // K_PASS):
                 cols = slice(G * V + half * BANK, G * V + (half + 1) * BANK)
                 nc.vector.quantize_mx(
-                    out=w_codes[:, cols].bitcast(FP8X4), scales=w_scales[:, cols], in_=w_grouped[:]
+                    out=w_codes[:, cols].bitcast(FP8X4), scales=w_scales[:, cols], in_=w_groupeds[(half, G)][:]
                 )
 
         vv_codes = keep.tile([P, 2 * V], U32, name="vv_codes", align_bytes=64)
@@ -275,16 +269,6 @@ def tile_interpretablemultiheadattention_pa_kernel(tc, qh, kh, v, Wv, bv, out):
             for m in range(2):
                 packed_codes[(g, m)] = keep.tile([P, V], U32, name="packed%d%d" % (g, m), align_bytes=64)
 
-        UNITS_AHEAD = 4
-        for unit in range(UNITS_AHEAD):
-            value_passes(unit, "mm%d" % unit)
-            value_add(unit)
-        value_quantise(UNITS_AHEAD - 1)
-        for idx, (name, j) in enumerate(first_tiles):
-            tr = bank("tr%d" % (idx % 2))
-            qk_transposes(name, j, tr)
-            qk_copy(name, j, tr)
-
         HALF = K_PASS // 2
         jobs = []
         for qt in (3, 2, 1, 0, 7, 6, 5, 4):
@@ -343,7 +327,7 @@ def tile_interpretablemultiheadattention_pa_kernel(tc, qh, kh, v, Wv, bv, out):
             qt, m, pack, heavy, heads = jobs[i]
             calls = []
             if heavy:
-                sc = bank("mm%d" % (2 * (i % 2) + 1))
+                sc = bank("mm%d" % (2 * ((i + 1) % 2) + 1))
                 full_bank[i] = sc
                 for e in range(2):
                     calls.append((
@@ -356,7 +340,7 @@ def tile_interpretablemultiheadattention_pa_kernel(tc, qh, kh, v, Wv, bv, out):
             n_first = len(calls)
             if opens(i):
                 if heavy:
-                    name = "mm%d" % (2 * ((i + (heads[0] // 2 if pack == 2 else 0)) % 2))
+                    name = "mm%d" % (2 * ((i + 1 + (heads[0] // 2 if pack == 2 else 0)) % 2))
                 else:
                     name = "mm%d" % (i % 2)
                 sc = bank(name)
@@ -475,7 +459,7 @@ def tile_interpretablemultiheadattention_pa_kernel(tc, qh, kh, v, Wv, bv, out):
         def sum_of_sums(i):
             if live(i) and jobs[i][3]:
                 total = stats.tile([P, 1], F32, name="total")
-                nc.vector.tensor_tensor(out=total[:], in0=sums_of[i][:, 0:1], in1=sums_of[i][:, 1:2], op=ALU.add)
+                (nc.gpsimd if SUM_G else nc.vector).tensor_tensor(out=total[:], in0=sums_of[i][:, 0:1], in1=sums_of[i][:, 1:2], op=ALU.add)
                 sums_of[i] = total
 
         def reciprocal(i):
@@ -505,15 +489,26 @@ def tile_interpretablemultiheadattention_pa_kernel(tc, qh, kh, v, Wv, bv, out):
                     p_tile = soft.tile([P, K_PASS], BF16, name="p_diag")
                     p_diag[key] = p_tile[:]
             if heavy:
-                nc.vector.tensor_scalar(
-                    out=p_full[i], in0=e_full[i], scalar1=recips[i][:], scalar2=None, op0=ALU.mult
-                )
+                if "F" in NORM_G:
+                    nc.gpsimd.tensor_scalar(
+                        out=p_full[i], in0=e_full[i], scalar1=recips[i][:], scalar2=0.0, op0=ALU.mult, op1=ALU.add
+                    )
+                else:
+                    nc.vector.tensor_scalar(
+                        out=p_full[i], in0=e_full[i], scalar1=recips[i][:], scalar2=None, op0=ALU.mult
+                    )
             for b, n in enumerate(heads):
                 h = n % pack
-                nc.vector.tensor_scalar(
-                    out=diag_region(p_diag[key], i, h), in0=diag_region(e_diag[key], i, h),
-                    scalar1=recips[i][:, b : b + 1], scalar2=None, op0=ALU.mult,
-                )
+                if ("D" if heavy else "L") in NORM_G:
+                    nc.gpsimd.tensor_scalar(
+                        out=diag_region(p_diag[key], i, h), in0=diag_region(e_diag[key], i, h),
+                        scalar1=recips[i][:, b : b + 1], scalar2=0.0, op0=ALU.mult, op1=ALU.add,
+                    )
+                else:
+                    nc.vector.tensor_scalar(
+                        out=diag_region(p_diag[key], i, h), in0=diag_region(e_diag[key], i, h),
+                        scalar1=recips[i][:, b : b + 1], scalar2=None, op0=ALU.mult,
+                    )
 
         def tiles_of(i):
             qt, m, pack, heavy, heads = jobs[i]
@@ -533,7 +528,12 @@ def tile_interpretablemultiheadattention_pa_kernel(tc, qh, kh, v, Wv, bv, out):
         def transposes(i):
             if not live(i):
                 return
-            tr = bank("tr%d" % (i % 2))
+            if jobs[i][3]:
+                tr = bank("tr%d" % (i % 2))[:]
+            else:
+                if i == 0:
+                    tr_banks["light"] = bank("tr0")
+                tr = tr_banks["light"][:, (i % 2) * 2 * P : (i % 2 + 1) * 2 * P]
             for slot, tile in enumerate(tiles_of(i)):
                 p_words = tile[0].bitcast(F32)
                 for u in range(2):
@@ -559,8 +559,12 @@ def tile_interpretablemultiheadattention_pa_kernel(tc, qh, kh, v, Wv, bv, out):
             if not live(i):
                 return
             n_tiles = len(tiles_of(i))
-            p_codes = soft.tile([P, 2 * P], U32, name="p_codes", align_bytes=64)
-            p_scales = soft.tile([P, 2 * P], U8, name="p_scales", align_bytes=64)
+            if jobs[i][3]:
+                p_codes = soft.tile([P, 2 * P], U32, name="p_codes", align_bytes=64)
+                p_scales = soft.tile([P, 2 * P], U8, name="p_scales", align_bytes=64)
+            else:
+                p_codes = light.tile([P, P], U32, name="l_codes", align_bytes=64)
+                p_scales = light.tile([P, P], U8, name="l_scales", align_bytes=64)
             nc.vector.quantize_mx(
                 out=p_codes[:, : n_tiles * P].bitcast(FP8X4),
                 scales=p_scales[:, : n_tiles * P],
@@ -568,15 +572,13 @@ def tile_interpretablemultiheadattention_pa_kernel(tc, qh, kh, v, Wv, bv, out):
             )
             p_operands[i] = (p_codes, p_scales)
 
-        def weighted_sum(i):
-            if not live(i):
-                return
+        def weighted_sum(i, slot):
             qt = jobs[i][0]
             p_codes, p_scales = p_operands[i]
             if qt not in acc:
                 acc[qt] = [bank("acc%d" % half) for half in range(V // BANK)]
                 done[qt] = 0
-            for slot, (p_ap, codes, scales, c0) in enumerate(tiles_of(i)):
+            for p_ap, codes, scales, c0 in [tiles_of(i)[slot]]:
                 lcols = slice(slot * P, (slot + 1) * P)
                 for half in range(V // BANK):
                     rcols = slice(c0 + half * BANK, c0 + (half + 1) * BANK)
@@ -591,51 +593,105 @@ def tile_interpretablemultiheadattention_pa_kernel(tc, qh, kh, v, Wv, bv, out):
                     )
                 done[qt] += 1
 
-        def store_out(i):
-            if not live(i) or jobs[i][4][-1] != NH - 1:
-                return
-            qt = jobs[i][0]
+        def store_out(qt):
             o_tile = stage.tile([P, V], F32, name="o_tile")
             nc.scalar.mul(out=o_tile[:, :BANK], in_=acc[qt][0][:], mul=1.0 / NH)
-            nc.vector.tensor_scalar(
-                out=o_tile[:, BANK:], in0=acc[qt][1][:], scalar1=1.0 / NH, scalar2=None, op0=ALU.mult
-            )
+            if EVAC == "s":
+                nc.scalar.mul(out=o_tile[:, BANK:], in_=acc[qt][1][:], mul=1.0 / NH)
+            else:
+                nc.vector.tensor_scalar(
+                    out=o_tile[:, BANK:], in0=acc[qt][1][:], scalar1=1.0 / NH, scalar2=None, op0=ALU.mult
+                )
             nc.sync.dma_start(out=out[0, qt * P : (qt + 1) * P, :], in_=o_tile[:])
 
-        later_tiles = [("v", st) for st in range(4, S_TILES)] + later_qk
-        later_grouped = {}
+        def take_tile(name, idx, bank_name):
+            tr = bank(bank_name)
+            if name == "v":
+                v_transposes(idx, tr)
+            else:
+                qk_transposes(name, idx % NH, idx // NH, tr)
+            tr_pending.append((name, idx, tr))
 
-        for s in range(len(jobs) + LAG_OUT):
-            store_out(s - LAG_OUT)
-            if s > 0:
-                value_add(s - 1 + UNITS_AHEAD)
-            copy_out(s - LAG_COPY)
+        def empty_tile(name, idx, tr, copy):
+            if name == "v":
+                v_pending.append((idx, v_copy(tr)))
+            else:
+                qk_copy(name, idx % NH, idx // NH, tr, copy)
+
+        EXTRA = {0: [("v", 0, "tr1"), ("k", 2, "acc0"), ("q", 2, "acc1")], 1: [("v", 1, "tr1"), ("k", 3, "acc0"), ("q", 3, "acc1")], 2: [("v", 2, "tr1"), ("v", 3, "acc0")], 4: [("v", 4, "tr1")], 5: [("v", 5, "tr1"), ("v", 6, "acc0"), ("v", 7, "acc1")], 6: [("k", 4, "tr1"), ("q", 4, "acc0")], 7: [("k", 5, "tr1"), ("q", 5, "acc0")], 8: [("k", 6, "tr1"), ("q", 6, "acc0")], 9: [("k", 7, "tr1"), ("q", 7, "acc0")]}
+        W_REGROUP = {1: [(0, 0, "v", 0, 1), (0, 1, "v", 0, 1)], 3: [(1, 0, "v", 0, 1), (1, 1, "v", 0, 1)]}
+        W_QUANT = {2: 0, 4: 1}
+        UNITS_AT = {3: [0, 1], 4: [2, 3], 5: [4, 5], 6: [6, 7], 7: [8, 9], 8: [10, 11], 9: [12, 13], 10: [14, 15]}
+        UNIT_BANKS = ["mm2", "mm3"]
+        PV_START = 10
+        PV_MAX = 2
+        SUM_G = False
+        EVAC = "v"
+        NORM_G = "LD"
+        PAIR = 0
+        tr_pending = []
+        v_pending = []
+        for idx, (name, n) in enumerate((("k", 0), ("q", 0), ("k", 1), ("q", 1))):
+            take_tile(name, n, ("acc0", "acc1", "mm2", "mm3")[idx])
+            empty_tile(name, n, tr_pending[idx][2], nc.vector.tensor_copy if idx % 2 else nc.scalar.copy)
+        tr_pending = []
+        add_pending = []
+        stores = []
+        pv_tiles = []
+        steps = len(jobs) + LAG_OUT + 1
+        s = 0
+        while s < steps or pv_tiles or stores:
+            for qt in stores:
+                store_out(qt)
+            stores = []
+            added = add_pending
+            add_pending = []
+            for unit in added:
+                value_add(unit)
+            for name, idx, tr in tr_pending:
+                empty_tile(name, idx, tr, nc.scalar.copy)
+            tr_pending = []
+            copy_out(s - (4 + (PAIR > 0)))
             sum_of_sums(s - LAG_NORM)
-            quantise(s - LAG_QUANT)
+            quantise(s - (5 + (PAIR > 0)))
             reciprocal(s - LAG_NORM)
             scores_first(s)
             maximum_first(s)
             exponentials(s - LAG_EXP)
             normalise(s - LAG_NORM)
-            if s - 1 in later_grouped:
-                v_quantise(later_tiles[s - 1][1], later_grouped[s - 1])
-            if s > 0:
-                value_quantise(s - 1 + UNITS_AHEAD)
-                for g in range(2):
-                    if s - 1 + UNITS_AHEAD == 8 * g + 7:
-                        replicate(g)
-            transposes(s - LAG_TRANSPOSE)
-            if s < len(later_tiles):
-                name, idx = later_tiles[s]
-                tr = bank("mm2" if s < LIGHT else "mm0")
-                if name == "v":
-                    v_transposes(idx, tr)
-                    later_grouped[s] = v_copy(tr)
-                else:
-                    qk_transposes(name, idx, tr)
-                    qk_copy(name, idx, tr)
+            for idx, v_grouped in v_pending:
+                v_quantise(idx, v_grouped)
+            v_pending = []
+            for unit in added:
+                value_quantise(unit)
+                if unit % 8 == 7:
+                    replicate(unit // 8)
+            for half, G, engine, piece, pieces in W_REGROUP.get(s, []):
+                regroup_w(half, G, engine, piece, pieces)
+            if s in W_QUANT:
+                quantise_w(W_QUANT[s])
+            if not PAIR:
+                transposes(s - 3)
+            elif s % 2 == PAIR - 1:
+                transposes(s - 4)
+                transposes(s - 3)
+            for name, idx, bank_name in EXTRA.get(s, []):
+                take_tile(name, idx, bank_name)
             scores_second(s)
             maximum_second(s)
-            weighted_sum(s - LAG_SUM)
-            if s + UNITS_AHEAD < UNITS:
-                value_passes(s + UNITS_AHEAD, "mm3" if s < LIGHT else "mm1")
+            if live(s - (5 + (PAIR > 0)) - 1):
+                pv_tiles.extend([(s - (5 + (PAIR > 0)) - 1, slot) for slot in range(len(tiles_of(s - (5 + (PAIR > 0)) - 1)))])
+            if s >= PV_START:
+                for count in range(PV_MAX):
+                    if pv_tiles:
+                        i, slot = pv_tiles[0]
+                        if stores:
+                            break
+                        pv_tiles = pv_tiles[1:]
+                        weighted_sum(i, slot)
+                        if done[jobs[i][0]] == TILES_OF[jobs[i][0]]:
+                            stores.append(jobs[i][0])
+            for idx, unit in enumerate(UNITS_AT.get(s, [])):
+                value_passes(unit, UNIT_BANKS[idx])
+                add_pending.append(unit)
+            s += 1

@@ -38,11 +38,14 @@ def tile_interpretablemultiheadattention_pa_kernel(tc, qh, kh, v, Wv, bv, out):
     nc = tc.nc
     with ExitStack() as ctx:
         const = ctx.enter_context(tc.tile_pool(name="const", bufs=1))
+        WARM = 4
         keep = ctx.enter_context(tc.tile_pool(name="keep", bufs=1))
         raw_qk = ctx.enter_context(tc.tile_pool(name="raw_qk", bufs=10))
         w_stage = ctx.enter_context(tc.tile_pool(name="w_stage", bufs=4))
         stage = ctx.enter_context(tc.tile_pool(name="stage", bufs=2))
+        out_stage = ctx.enter_context(tc.tile_pool(name="out_stage", bufs=3))
         soft = ctx.enter_context(tc.tile_pool(name="soft", bufs=3))
+        three = ctx.enter_context(tc.tile_pool(name="three", bufs=4))
         light = ctx.enter_context(tc.tile_pool(name="light", bufs=8))
         stats = ctx.enter_context(tc.tile_pool(name="stats", bufs=6))
         psum = ctx.enter_context(tc.psum_pool(name="psum", bufs=1))
@@ -66,25 +69,19 @@ def tile_interpretablemultiheadattention_pa_kernel(tc, qh, kh, v, Wv, bv, out):
             pattern=[[-1, P]],
             channel_multiplier=1,
         )
+        warm_b = const.tile([P, BANK], BF16, name="warm_b")
+        nc.vector.memset(warm_b[:], 0.0)
         warm_in = const.tile([P, 1], F32, name="warm_in")
         warm_out = const.tile([P, 1], F32, name="warm_out")
         nc.vector.memset(warm_in[:], 0.0)
         nc.scalar.activation(out=warm_out[:], in_=warm_in[:], func=ACT.Exp)
         bias_all = const.tile([P, V], BF16, name="bias_all")
 
-        p_two = []
-        for b in range(2):
-            p_tile = keep.tile([P, 2 * K_PASS], BF16, name="p_two%d" % b)
-            for u in range(2):
-                nc.vector.memset(p_tile[:, K_PASS + 256 * u + 192 : K_PASS + 256 * (u + 1)], 0.0)
-            p_two.append(p_tile)
         causal_b = const.tile([P, P], BF16, name="causal_b")
         nc.vector.tensor_copy(
             out=causal_b[:].rearrange("p (u w e) -> p u w e", u=2, e=2),
             in_=causal_f[:].rearrange("p (w u e) -> p u w e", u=2, e=2),
         )
-        packed_scales = keep.tile([P, 4 * V], U8, name="packed_scales", align_bytes=64)
-        nc.gpsimd.memset(packed_scales[:].bitcast(U32), 0)
 
         rows_of = {
             "q": qh.rearrange("n o (g p t) d -> (n o) g p (t d)", p=P, t=4),
@@ -97,36 +94,39 @@ def tile_interpretablemultiheadattention_pa_kernel(tc, qh, kh, v, Wv, bv, out):
             nc.sync.dma_start(out=raw[:], in_=rows_of[name][n, g])
             raw_of[(name, n, g)] = raw
 
-        w_raw = keep.tile([P, 4 * 2 * V], BF16, name="w_raw")
+        w_raw = [keep.tile([P, 4 * 2 * BANK], BF16, name="w_raw%d" % half, align_bytes=64) for half in range(V // BANK)]
         w_rows = Wv.rearrange("(a p e) c -> a p e c", a=4, p=P, e=2)
-        w_raw_aec = w_raw[:].rearrange("p (a e c) -> p a e c", a=4, e=2)
-        v_raw = keep.tile([P, 4 * 2 * H], BF16, name="v_raw")
+        v_raw = [keep.tile([P, 4 * H], BF16, name="v_raw%d" % g, align_bytes=64) for g in range(2)]
         v_rows = v.rearrange("o (g p t) h -> (o g) p (t h)", p=P, t=4)
 
         def load_v(a):
             g, pair = a // 2, a % 2
             nc.sync.dma_start(
-                out=v_raw[:, a * 2 * H : (a + 1) * 2 * H], in_=v_rows[g][:, pair * 2 * H : (pair + 1) * 2 * H]
+                out=v_raw[g][:, pair * 2 * H : (pair + 1) * 2 * H], in_=v_rows[g][:, pair * 2 * H : (pair + 1) * 2 * H]
             )
 
-        for n in range(2):
+        for n in range(3):
             load_qk("k", n, 0)
             load_qk("q", n, 0)
         load_v(0)
+        load_qk("k", 3, 0)
+        load_qk("q", 3, 0)
         load_v(1)
-        for n in range(2, NH):
-            load_qk("k", n, 0)
-            load_qk("q", n, 0)
         for half in range(V // BANK):
             cols = slice(half * BANK, (half + 1) * BANK)
             for a in range(4):
-                nc.sync.dma_start(out=w_raw_aec[:, a, :, cols], in_=w_rows[a][:, :, cols])
+                nc.sync.dma_start(
+                    out=w_raw[half][:].rearrange("p (a e c) -> p a e c", a=4, e=2)[:, a], in_=w_rows[a][:, :, cols]
+                )
         nc.sync.dma_start(out=bias_all[:], in_=bv.partition_broadcast(P))
         load_v(2)
         load_v(3)
         for n in range(NH):
             load_qk("k", n, 1)
             load_qk("q", n, 1)
+        warm_ps = bank("tr0")
+        for rep in range(WARM):
+            nc.tensor.matmul(out=warm_ps[:], lhsT=warm_b[:, :P], rhs=warm_b[:], start=True, stop=True)
         words_T = {"q": keep.tile([P, NH * S], F32, name="qT"), "k": keep.tile([P, NH * S], F32, name="kT")}
 
         def qk_transposes(name, n, g, tr):
@@ -152,13 +152,12 @@ def tile_interpretablemultiheadattention_pa_kernel(tc, qh, kh, v, Wv, bv, out):
 
         v_codes = keep.tile([P, S_TILES * 2 * P], U32, name="v_codes", align_bytes=64)
         v_scales = keep.tile([P, S_TILES * 2 * P], U8, name="v_scales", align_bytes=64)
-        v_words = v_raw[:].bitcast(F32)
 
         def v_transposes(st, tr):
             for b in range(4):
                 nc.tensor.transpose(
                     tr[:, b * P : (b + 1) * P],
-                    v_words[:, st * (H // 2) + b * P : st * (H // 2) + (b + 1) * P],
+                    v_raw[st // 4][:].bitcast(F32)[:, st % 4 * (H // 2) + b * P : st % 4 * (H // 2) + (b + 1) * P],
                     ident_f[:],
                 )
 
@@ -180,13 +179,13 @@ def tile_interpretablemultiheadattention_pa_kernel(tc, qh, kh, v, Wv, bv, out):
 
         def regroup_w(half, G, engine, piece, pieces):
             if True:
-                rows_t_c = w_raw[:, G * 4 * V : (G + 1) * 4 * V].rearrange("p (t c) -> p t c", t=4)
+                rows_t_c = w_raw[half][:, G * 4 * BANK : (G + 1) * 4 * BANK].rearrange("p (t c) -> p t c", t=4)
                 if piece == 0:
                     w_grouped = w_stage.tile([P, 4 * BANK], BF16, name="w_grouped", align_bytes=64)
                     w_groupeds[(half, G)] = w_grouped
                 regroup = {"v": nc.vector.tensor_copy, "s": nc.scalar.copy, "g": nc.gpsimd.tensor_copy}[engine]
                 width = BANK // pieces
-                c0 = half * BANK + piece * width
+                c0 = piece * width
                 regroup(
                     out=w_groupeds[(half, G)][:, 4 * piece * width : 4 * (piece + 1) * width].rearrange(
                         "p (c i t) -> p c t i", i=4, t=4
@@ -201,8 +200,19 @@ def tile_interpretablemultiheadattention_pa_kernel(tc, qh, kh, v, Wv, bv, out):
                     out=w_codes[:, cols].bitcast(FP8X4), scales=w_scales[:, cols], in_=w_groupeds[(half, G)][:]
                 )
 
-        vv_codes = keep.tile([P, 2 * V], U32, name="vv_codes", align_bytes=64)
-        vv_scales = keep.tile([P, 2 * V], U8, name="vv_scales", align_bytes=64)
+        OPERAND = V + V // 4
+        vv_tiles = []
+        for g in range(2):
+            vv_tile = keep.tile([P, OPERAND], U32, name="vv%d" % g, align_bytes=64)
+            nc.gpsimd.memset(vv_tile[:, V:], 0)
+            vv_tiles.append(vv_tile)
+
+        def codes_of(operand):
+            return operand[:, :V].bitcast(FP8X4)
+
+        def scales_of(operand):
+            return operand[:, V:].bitcast(U8)
+
         UNITS = (S // K_PASS) * (V // P)
         unit_banks = {}
         unit_grouped = {}
@@ -245,29 +255,44 @@ def tile_interpretablemultiheadattention_pa_kernel(tc, qh, kh, v, Wv, bv, out):
         def value_quantise(unit):
             if unit not in unit_banks or unit % 4 != 3:
                 return
-            cols = slice((unit // 4) * BANK, (unit // 4 + 1) * BANK)
+            operand = vv_tiles[unit // 8]
+            cols = slice(unit // 4 % 2 * BANK, (unit // 4 % 2 + 1) * BANK)
             nc.vector.quantize_mx(
-                out=vv_codes[:, cols].bitcast(FP8X4), scales=vv_scales[:, cols], in_=unit_grouped[unit // 4][:]
+                out=codes_of(operand)[:, cols], scales=scales_of(operand)[:, cols], in_=unit_grouped[unit // 4][:]
             )
 
-        def replicate(g):
-            cols = slice(g * V, (g + 1) * V)
-            for m in range(2):
-                codes = packed_codes[(g, m)]
-                scales = packed_scales[:, (2 * g + m) * V : (2 * g + m + 1) * V]
-                rows = 32 * (m + 1)
-                for r in range(0, P, rows):
-                    nc.sync.dma_start(out=codes[r : r + rows, :].bitcast(I32), in_=vv_codes[0:rows, cols].bitcast(I32))
-                for r in range(0, P, 32):
-                    src = r % rows
-                    nc.sync.dma_start(
-                        out=scales[r : r + 4, :].bitcast(I32), in_=vv_scales[src : src + 4, cols].bitcast(I32)
-                    )
+        QUARTERS = [(0, 0, 0, 0), (0, 1, 0, 1), (0, 1, 2, 0), (1, 2, 0, 1), (2, 0, 1, 2)]
+        packed = {}
 
-        packed_codes = {}
-        for g in range(2):
-            for m in range(2):
-                packed_codes[(g, m)] = keep.tile([P, V], U32, name="packed%d%d" % (g, m), align_bytes=64)
+        def replicate(g, x):
+            if (g, x) in ((0, 2), (0, 3)):
+                packed_tile = keep.tile([P, 2 * V], U32, name="packed_w%d" % x, tag="w_raw%d" % (x - 2), align_bytes=64)
+                operand = packed_tile[:, :OPERAND]
+            elif (g, x) in ((0, 4), (0, 1), (0, 0), (1, 2)):
+                packed_tile = w_stage.tile([P, OPERAND], U32, name="packed_s", tag="w_grouped", align_bytes=64)
+                operand = packed_tile[:]
+            elif x == 3:
+                packed_tile = keep.tile([P, 2 * V], U32, name="packed_v0", tag="v_raw0", align_bytes=64)
+                operand = packed_tile[:, :OPERAND]
+            elif x == 4:
+                packed_tile = keep.tile([P, 2 * V], U32, name="packed_v1", tag="v_raw1", align_bytes=64)
+                operand = packed_tile[:, :OPERAND]
+            else:
+                packed_tile = keep.tile([P, OPERAND], U32, name="packed_last%d" % x, align_bytes=64)
+                operand = packed_tile[:]
+            packed[(g, x)] = operand
+            quarters = QUARTERS[x]
+            q = 0
+            while q < 4:
+                count = 1
+                while q + count < 4 and quarters[q + count] == quarters[q] + count:
+                    count += 1
+                src = 32 * quarters[q]
+                nc.sync.dma_start(
+                    out=operand[32 * q : 32 * (q + count), :].bitcast(I32),
+                    in_=vv_tiles[g][src : src + 32 * count, :].bitcast(I32),
+                )
+                q += count
 
         HALF = K_PASS // 2
         jobs = []
@@ -281,11 +306,11 @@ def tile_interpretablemultiheadattention_pa_kernel(tc, qh, kh, v, Wv, bv, out):
             else:
                 for n in range(0, NH, pack):
                     jobs.append((qt, m, pack, False, list(range(n, n + pack))))
-        LIGHT = 11
+        LAST_QT = jobs[-1][0]
         TILES_OF = {}
         for qt in range(S_TILES):
             m = qt % TILES_PER_GROUP
-            TILES_OF[qt] = {0: 1, 1: 2, 2: 4, 3: 4}[m] + (NH if qt >= TILES_PER_GROUP else 0)
+            TILES_OF[qt] = m + 1 + (NH if qt >= TILES_PER_GROUP else 0)
 
         diag_bank = {}
         full_bank = {}
@@ -297,6 +322,7 @@ def tile_interpretablemultiheadattention_pa_kernel(tc, qh, kh, v, Wv, bv, out):
         recips = {}
         p_full = {}
         p_diag = {}
+        p_three = {}
         tr_banks = {}
         p_groupeds = {}
         p_operands = {}
@@ -427,17 +453,9 @@ def tile_interpretablemultiheadattention_pa_kernel(tc, qh, kh, v, Wv, bv, out):
             qt, m, pack, heavy, heads = jobs[i]
             key = diag_key(i)
             width = P * (m + 1)
-            if pack == 1:
-                e_tile = soft.tile([P, 2 * K_PASS], F32, name="e_tile")
-                e_full[i] = e_tile[:, :K_PASS]
-                e_diag[key] = e_tile[:, K_PASS:]
-            else:
-                if heavy:
-                    e_tile = soft.tile([P, K_PASS], F32, name="e_full")
-                    e_full[i] = e_tile[:]
-                if opens(i):
-                    e_tile = soft.tile([P, K_PASS], F32, name="e_diag")
-                    e_diag[key] = e_tile[:]
+            e_tile = soft.tile([P, (1 + heavy) * K_PASS], F32, name="e_heavy" if heavy else "e_light")
+            e_full[i] = e_tile[:, K_PASS:] if heavy else None
+            e_diag[i] = [e_tile[:, b * width : (b + 1) * width] for b in range(len(heads))]
             sums = stats.tile([P, 4], F32, name="sums")
             if heavy:
                 nc.scalar.activation(
@@ -447,8 +465,8 @@ def tile_interpretablemultiheadattention_pa_kernel(tc, qh, kh, v, Wv, bv, out):
             for b, n in enumerate(heads):
                 h = n % pack
                 nc.scalar.activation(
-                    out=diag_region(e_diag[key], i, h),
-                    in_=diag_bank[key][:, h * width : (h + 1) * width].rearrange("p (u x) -> p u x", u=2),
+                    out=e_diag[i][b],
+                    in_=diag_bank[key][:, h * width : (h + 1) * width],
                     func=ACT.Exp,
                     bias=shifts[i][:, b : b + 1],
                     scale=SCALE,
@@ -474,9 +492,14 @@ def tile_interpretablemultiheadattention_pa_kernel(tc, qh, kh, v, Wv, bv, out):
             qt, m, pack, heavy, heads = jobs[i]
             key = diag_key(i)
             if m == 2:
-                p_tile = p_two[i % 2]
-                p_full[i] = p_tile[:, :K_PASS]
-                p_diag[key] = p_tile[:, K_PASS:]
+                if heavy:
+                    p_tile = soft.tile([P, K_PASS], BF16, name="p_full")
+                    p_full[i] = p_tile[:]
+                if heads[0] == 0:
+                    p_three[qt] = []
+                if heads[0] < 3:
+                    p_tile = three.tile([P, K_PASS], BF16, name="p_three")
+                    p_three[qt].append(p_tile)
             elif pack == 1:
                 p_tile = soft.tile([P, 2 * K_PASS], BF16, name="p_tile")
                 p_full[i] = p_tile[:, :K_PASS]
@@ -497,16 +520,34 @@ def tile_interpretablemultiheadattention_pa_kernel(tc, qh, kh, v, Wv, bv, out):
                     nc.vector.tensor_scalar(
                         out=p_full[i], in0=e_full[i], scalar1=recips[i][:], scalar2=None, op0=ALU.mult
                     )
+            todo = []
             for b, n in enumerate(heads):
                 h = n % pack
+                e_halves = e_diag[i][b].rearrange("p (u x) -> p u x", u=2)
+                if m == 2:
+                    pieces = []
+                    for x in range(3):
+                        c_from = max(3 * n, 4 * x)
+                        c_to = min(3 * n + 3, 4 * x + 4)
+                        if c_from < c_to:
+                            pieces.append((
+                                p_three[qt][x][:].rearrange("p (u y) -> p u y", u=2)[
+                                    :, :, 64 * (c_from - 4 * x) : 64 * (c_to - 4 * x)
+                                ],
+                                e_halves[:, :, 64 * (c_from - 3 * n) : 64 * (c_to - 3 * n)],
+                            ))
+                else:
+                    pieces = [(diag_region(p_diag[key], i, h), e_halves)]
+                todo.extend([(b, x, y) for x, y in pieces])
+            for b, p_region, e_region in todo:
                 if ("D" if heavy else "L") in NORM_G:
                     nc.gpsimd.tensor_scalar(
-                        out=diag_region(p_diag[key], i, h), in0=diag_region(e_diag[key], i, h),
+                        out=p_region, in0=e_region,
                         scalar1=recips[i][:, b : b + 1], scalar2=0.0, op0=ALU.mult, op1=ALU.add,
                     )
                 else:
                     nc.vector.tensor_scalar(
-                        out=diag_region(p_diag[key], i, h), in0=diag_region(e_diag[key], i, h),
+                        out=p_region, in0=e_region,
                         scalar1=recips[i][:, b : b + 1], scalar2=None, op0=ALU.mult,
                     )
 
@@ -515,35 +556,37 @@ def tile_interpretablemultiheadattention_pa_kernel(tc, qh, kh, v, Wv, bv, out):
             g = qt // TILES_PER_GROUP
             tiles = []
             if heavy:
-                tiles.append((p_full[i], vv_codes, vv_scales, 0))
-            if closes(i):
-                if pack == 1:
-                    tiles.append((p_diag[diag_key(i)], vv_codes, vv_scales, g * V))
-                else:
-                    tiles.append(
-                        (p_diag[diag_key(i)], packed_codes[(g, m)], packed_scales[:, (2 * g + m) * V : (2 * g + m + 1) * V], 0)
-                    )
+                words = p_full[i].bitcast(F32)
+                tiles.append(([words[:, :P], words[:, P:]], vv_tiles[0]))
+            if m == 3:
+                words = p_diag[diag_key(i)].bitcast(F32)
+                tiles.append(([words[:, :P], words[:, P:]], vv_tiles[g]))
+            elif m == 2:
+                if heads[0] > 0:
+                    x = heads[0] - 1
+                    words = p_three[qt][x][:].bitcast(F32)
+                    tiles.append(([words[:, :P], words[:, P:]], packed.get((g, 2 + x))))
+            elif closes(i):
+                words = p_diag[diag_key(i)].bitcast(F32)
+                tiles.append(([words[:, :P], words[:, P:]], packed.get((g, m))))
             return tiles
 
         def transposes(i):
-            if not live(i):
+            if not live(i) or not tiles_of(i):
                 return
             if jobs[i][3]:
                 tr = bank("tr%d" % (i % 2))[:]
             else:
-                if i == 0:
+                if "light" not in tr_banks:
                     tr_banks["light"] = bank("tr0")
                 tr = tr_banks["light"][:, (i % 2) * 2 * P : (i % 2 + 1) * 2 * P]
-            for slot, tile in enumerate(tiles_of(i)):
-                p_words = tile[0].bitcast(F32)
+            for slot, (words, operand) in enumerate(tiles_of(i)):
                 for u in range(2):
-                    nc.tensor.transpose(
-                        tr[:, (2 * slot + u) * P : (2 * slot + u + 1) * P], p_words[:, u * P : (u + 1) * P], ident_f[:]
-                    )
+                    nc.tensor.transpose(tr[:, (2 * slot + u) * P : (2 * slot + u + 1) * P], words[u], ident_f[:])
             tr_banks[i] = tr
 
         def copy_out(i):
-            if not live(i):
+            if not live(i) or not tiles_of(i):
                 return
             n_tiles = len(tiles_of(i))
             p_grouped = soft.tile([P, 2 * K_PASS], BF16, name="p_grouped", align_bytes=64)
@@ -556,7 +599,7 @@ def tile_interpretablemultiheadattention_pa_kernel(tc, qh, kh, v, Wv, bv, out):
             p_groupeds[i] = p_grouped
 
         def quantise(i):
-            if not live(i):
+            if not live(i) or not tiles_of(i):
                 return
             n_tiles = len(tiles_of(i))
             if jobs[i][3]:
@@ -572,29 +615,41 @@ def tile_interpretablemultiheadattention_pa_kernel(tc, qh, kh, v, Wv, bv, out):
             )
             p_operands[i] = (p_codes, p_scales)
 
-        def weighted_sum(i, slot):
-            qt = jobs[i][0]
-            p_codes, p_scales = p_operands[i]
+        def weighted_sums(tiles):
+            qt = jobs[tiles[0][0]][0]
             if qt not in acc:
                 acc[qt] = [bank("acc%d" % half) for half in range(V // BANK)]
                 done[qt] = 0
-            for p_ap, codes, scales, c0 in [tiles_of(i)[slot]]:
+            passes = [(idx, half) for idx in range(len(tiles)) for half in range(V // BANK)]
+            if qt == LAST_QT:
+                passes = [(idx, half) for half in range(V // BANK) for idx in range(len(tiles))]
+            for idx, half in passes:
+                i, slot = tiles[idx]
+                p_codes, p_scales = p_operands[i]
+                words, operand = tiles_of(i)[slot]
                 lcols = slice(slot * P, (slot + 1) * P)
-                for half in range(V // BANK):
-                    rcols = slice(c0 + half * BANK, c0 + (half + 1) * BANK)
-                    nc.tensor.matmul_mx(
-                        out=acc[qt][half][:],
-                        lhsT=p_codes[:, lcols].bitcast(FP8X4),
-                        lhsT_scale=p_scales[:, lcols],
-                        rhs=codes[:, rcols].bitcast(FP8X4),
-                        rhs_scale=scales[:, rcols],
-                        start=(done[qt] == 0),
-                        stop=(done[qt] == TILES_OF[qt] - 1),
-                    )
-                done[qt] += 1
+                rcols = slice(half * BANK, (half + 1) * BANK)
+                nc.tensor.matmul_mx(
+                    out=acc[qt][half][:],
+                    lhsT=p_codes[:, lcols].bitcast(FP8X4),
+                    lhsT_scale=p_scales[:, lcols],
+                    rhs=codes_of(operand)[:, rcols],
+                    rhs_scale=scales_of(operand)[:, rcols],
+                    start=(done[qt] + idx == 0),
+                    stop=(done[qt] + idx == TILES_OF[qt] - 1),
+                )
+            done[qt] += len(tiles)
 
         def store_out(qt):
-            o_tile = stage.tile([P, V], F32, name="o_tile")
+            o_tile = out_stage.tile([P, V], F32, name="o_tile")
+            if qt == LAST_QT:
+                nc.scalar.mul(out=o_tile[:, :BANK], in_=acc[qt][0][:], mul=1.0 / NH)
+                nc.sync.dma_start(out=out[0, qt * P : (qt + 1) * P, :BANK], in_=o_tile[:, :BANK])
+                nc.vector.tensor_scalar(
+                    out=o_tile[:, BANK:], in0=acc[qt][1][:], scalar1=1.0 / NH, scalar2=None, op0=ALU.mult
+                )
+                nc.sync.dma_start(out=out[0, qt * P : (qt + 1) * P, BANK:], in_=o_tile[:, BANK:])
+                return
             nc.scalar.mul(out=o_tile[:, :BANK], in_=acc[qt][0][:], mul=1.0 / NH)
             if EVAC == "s":
                 nc.scalar.mul(out=o_tile[:, BANK:], in_=acc[qt][1][:], mul=1.0 / NH)
@@ -618,17 +673,18 @@ def tile_interpretablemultiheadattention_pa_kernel(tc, qh, kh, v, Wv, bv, out):
             else:
                 qk_copy(name, idx % NH, idx // NH, tr, copy)
 
-        EXTRA = {0: [("v", 0, "tr1"), ("k", 2, "acc0"), ("q", 2, "acc1")], 1: [("v", 1, "tr1"), ("k", 3, "acc0"), ("q", 3, "acc1")], 2: [("v", 2, "tr1"), ("v", 3, "acc0")], 4: [("v", 4, "tr1")], 5: [("v", 5, "tr1"), ("v", 6, "acc0"), ("v", 7, "acc1")], 6: [("k", 4, "tr1"), ("q", 4, "acc0")], 7: [("k", 5, "tr1"), ("q", 5, "acc0")], 8: [("k", 6, "tr1"), ("q", 6, "acc0")], 9: [("k", 7, "tr1"), ("q", 7, "acc0")]}
-        W_REGROUP = {1: [(0, 0, "v", 0, 1), (0, 1, "v", 0, 1)], 3: [(1, 0, "v", 0, 1), (1, 1, "v", 0, 1)]}
-        W_QUANT = {2: 0, 4: 1}
-        UNITS_AT = {3: [0, 1], 4: [2, 3], 5: [4, 5], 6: [6, 7], 7: [8, 9], 8: [10, 11], 9: [12, 13], 10: [14, 15]}
-        UNIT_BANKS = ["mm2", "mm3"]
+        EXTRA = {0: [("k", 2, "acc0"), ("q", 2, "acc1")], 1: [("v", 0, "tr1"), ("k", 3, "acc0"), ("q", 3, "acc1")], 2: [("v", 1, "tr1"), ("v", 2, "acc0"), ("v", 3, "acc1")], 4: [("v", 4, "tr1")], 5: [("v", 5, "tr1"), ("v", 6, "acc0"), ("v", 7, "acc1")], 6: [("k", 4, "tr1"), ("q", 4, "acc0")], 7: [("k", 5, "tr1"), ("q", 5, "acc0")], 8: [("k", 6, "tr1"), ("q", 6, "acc0")], 9: [("k", 7, "tr1"), ("q", 7, "acc0")]}
+        W_REGROUP = {2: [(0, 0, "v", 0, 1), (0, 1, "v", 0, 1)], 4: [(1, 0, "v", 0, 1), (1, 1, "s", 0, 2)], 5: [(1, 1, "s", 1, 2)]}
+        W_QUANT = {3: 0, 5: 1}
+        UNITS_AT = {4: [0, 1], 5: [2, 3], 6: [4, 5], 7: [6, 7], 8: [8, 9], 9: [10, 11], 10: [12, 13], 11: [14, 15]}
+        UNIT_BANKS = ["mm2", "mm3", "acc0", "acc1"]
         PV_START = 10
         PV_MAX = 2
         SUM_G = False
         EVAC = "v"
         NORM_G = "LD"
         PAIR = 0
+        REPL = 2
         tr_pending = []
         v_pending = []
         for idx, (name, n) in enumerate((("k", 0), ("q", 0), ("k", 1), ("q", 1))):
@@ -637,6 +693,7 @@ def tile_interpretablemultiheadattention_pa_kernel(tc, qh, kh, v, Wv, bv, out):
         tr_pending = []
         add_pending = []
         stores = []
+        replicas = []
         pv_tiles = []
         steps = len(jobs) + LAG_OUT + 1
         s = 0
@@ -665,32 +722,29 @@ def tile_interpretablemultiheadattention_pa_kernel(tc, qh, kh, v, Wv, bv, out):
             for unit in added:
                 value_quantise(unit)
                 if unit % 8 == 7:
-                    replicate(unit // 8)
+                    replicas.extend([(unit // 8, x) for x in (2, 3, 4, 1, 0)])
+            for g, x in replicas[:REPL]:
+                replicate(g, x)
+            replicas = replicas[REPL:]
             for half, G, engine, piece, pieces in W_REGROUP.get(s, []):
                 regroup_w(half, G, engine, piece, pieces)
             if s in W_QUANT:
                 quantise_w(W_QUANT[s])
-            if not PAIR:
-                transposes(s - 3)
-            elif s % 2 == PAIR - 1:
-                transposes(s - 4)
-                transposes(s - 3)
-            for name, idx, bank_name in EXTRA.get(s, []):
-                take_tile(name, idx, bank_name)
             scores_second(s)
             maximum_second(s)
+            transposes(s - 3)
+            for name, idx, bank_name in EXTRA.get(s, []):
+                take_tile(name, idx, bank_name)
             if live(s - (5 + (PAIR > 0)) - 1):
                 pv_tiles.extend([(s - (5 + (PAIR > 0)) - 1, slot) for slot in range(len(tiles_of(s - (5 + (PAIR > 0)) - 1)))])
             if s >= PV_START:
-                for count in range(PV_MAX):
-                    if pv_tiles:
-                        i, slot = pv_tiles[0]
-                        if stores:
-                            break
-                        pv_tiles = pv_tiles[1:]
-                        weighted_sum(i, slot)
-                        if done[jobs[i][0]] == TILES_OF[jobs[i][0]]:
-                            stores.append(jobs[i][0])
+                now = [x for x in pv_tiles[:PV_MAX] if jobs[x[0]][0] == jobs[pv_tiles[0][0]][0]]
+                pv_tiles = pv_tiles[len(now):]
+                if now:
+                    weighted_sums(now)
+                    qt = jobs[now[0][0]][0]
+                    if done[qt] == TILES_OF[qt]:
+                        stores.append(qt)
             for idx, unit in enumerate(UNITS_AT.get(s, [])):
                 value_passes(unit, UNIT_BANKS[idx])
                 add_pending.append(unit)

@@ -46,6 +46,7 @@ def tile_interpretablemultiheadattention_pa_kernel(tc, qh, kh, v, Wv, bv, out):
         out_stage = ctx.enter_context(tc.tile_pool(name="out_stage", bufs=3))
         soft = ctx.enter_context(tc.tile_pool(name="soft", bufs=3))
         three = ctx.enter_context(tc.tile_pool(name="three", bufs=4))
+        heavy_codes = ctx.enter_context(tc.tile_pool(name="heavy_codes", bufs=8))
         light = ctx.enter_context(tc.tile_pool(name="light", bufs=8))
         stats = ctx.enter_context(tc.tile_pool(name="stats", bufs=6))
         psum = ctx.enter_context(tc.psum_pool(name="psum", bufs=1))
@@ -263,8 +264,9 @@ def tile_interpretablemultiheadattention_pa_kernel(tc, qh, kh, v, Wv, bv, out):
 
         QUARTERS = [(0, 0, 0, 0), (0, 1, 0, 1), (0, 1, 2, 0), (1, 2, 0, 1), (2, 0, 1, 2)]
         packed = {}
+        ready_at = {}
 
-        def replicate(g, x):
+        def replicate(g, x, s):
             if (g, x) in ((0, 2), (0, 3)):
                 packed_tile = keep.tile([P, 2 * V], U32, name="packed_w%d" % x, tag="w_raw%d" % (x - 2), align_bytes=64)
                 operand = packed_tile[:, :OPERAND]
@@ -281,6 +283,7 @@ def tile_interpretablemultiheadattention_pa_kernel(tc, qh, kh, v, Wv, bv, out):
                 packed_tile = keep.tile([P, OPERAND], U32, name="packed_last%d" % x, align_bytes=64)
                 operand = packed_tile[:]
             packed[(g, x)] = operand
+            ready_at[(g, x)] = s + PACK_WAIT
             quarters = QUARTERS[x]
             q = 0
             while q < 4:
@@ -557,18 +560,18 @@ def tile_interpretablemultiheadattention_pa_kernel(tc, qh, kh, v, Wv, bv, out):
             tiles = []
             if heavy:
                 words = p_full[i].bitcast(F32)
-                tiles.append(([words[:, :P], words[:, P:]], vv_tiles[0]))
+                tiles.append(([words[:, :P], words[:, P:]], vv_tiles[0], None))
             if m == 3:
                 words = p_diag[diag_key(i)].bitcast(F32)
-                tiles.append(([words[:, :P], words[:, P:]], vv_tiles[g]))
+                tiles.append(([words[:, :P], words[:, P:]], vv_tiles[g], None))
             elif m == 2:
                 if heads[0] > 0:
                     x = heads[0] - 1
                     words = p_three[qt][x][:].bitcast(F32)
-                    tiles.append(([words[:, :P], words[:, P:]], packed.get((g, 2 + x))))
+                    tiles.append(([words[:, :P], words[:, P:]], packed.get((g, 2 + x)), (g, 2 + x)))
             elif closes(i):
                 words = p_diag[diag_key(i)].bitcast(F32)
-                tiles.append(([words[:, :P], words[:, P:]], packed.get((g, m))))
+                tiles.append(([words[:, :P], words[:, P:]], packed.get((g, m)), (g, m)))
             return tiles
 
         def transposes(i):
@@ -580,7 +583,7 @@ def tile_interpretablemultiheadattention_pa_kernel(tc, qh, kh, v, Wv, bv, out):
                 if "light" not in tr_banks:
                     tr_banks["light"] = bank("tr0")
                 tr = tr_banks["light"][:, (i % 2) * 2 * P : (i % 2 + 1) * 2 * P]
-            for slot, (words, operand) in enumerate(tiles_of(i)):
+            for slot, (words, operand, source) in enumerate(tiles_of(i)):
                 for u in range(2):
                     nc.tensor.transpose(tr[:, (2 * slot + u) * P : (2 * slot + u + 1) * P], words[u], ident_f[:])
             tr_banks[i] = tr
@@ -603,8 +606,8 @@ def tile_interpretablemultiheadattention_pa_kernel(tc, qh, kh, v, Wv, bv, out):
                 return
             n_tiles = len(tiles_of(i))
             if jobs[i][3]:
-                p_codes = soft.tile([P, 2 * P], U32, name="p_codes", align_bytes=64)
-                p_scales = soft.tile([P, 2 * P], U8, name="p_scales", align_bytes=64)
+                p_codes = heavy_codes.tile([P, 2 * P], U32, name="p_codes", align_bytes=64)
+                p_scales = heavy_codes.tile([P, 2 * P], U8, name="p_scales", align_bytes=64)
             else:
                 p_codes = light.tile([P, P], U32, name="l_codes", align_bytes=64)
                 p_scales = light.tile([P, P], U8, name="l_scales", align_bytes=64)
@@ -618,7 +621,7 @@ def tile_interpretablemultiheadattention_pa_kernel(tc, qh, kh, v, Wv, bv, out):
         def weighted_sums(tiles):
             qt = jobs[tiles[0][0]][0]
             if qt not in acc:
-                acc[qt] = [bank("acc%d" % half) for half in range(V // BANK)]
+                acc[qt] = [bank(ACC_BANKS.get(qt, ("acc0", "acc1"))[half]) for half in range(V // BANK)]
                 done[qt] = 0
             passes = [(idx, half) for idx in range(len(tiles)) for half in range(V // BANK)]
             if qt == LAST_QT:
@@ -626,7 +629,7 @@ def tile_interpretablemultiheadattention_pa_kernel(tc, qh, kh, v, Wv, bv, out):
             for idx, half in passes:
                 i, slot = tiles[idx]
                 p_codes, p_scales = p_operands[i]
-                words, operand = tiles_of(i)[slot]
+                words, operand, source = tiles_of(i)[slot]
                 lcols = slice(slot * P, (slot + 1) * P)
                 rcols = slice(half * BANK, (half + 1) * BANK)
                 nc.tensor.matmul_mx(
@@ -644,7 +647,7 @@ def tile_interpretablemultiheadattention_pa_kernel(tc, qh, kh, v, Wv, bv, out):
             o_tile = out_stage.tile([P, V], F32, name="o_tile")
             if qt == LAST_QT:
                 nc.scalar.mul(out=o_tile[:, :BANK], in_=acc[qt][0][:], mul=1.0 / NH)
-                nc.sync.dma_start(out=out[0, qt * P : (qt + 1) * P, :BANK], in_=o_tile[:, :BANK])
+                (nc.scalar if OUTQ == "s" else nc.sync).dma_start(out=out[0, qt * P : (qt + 1) * P, :BANK], in_=o_tile[:, :BANK])
                 nc.vector.tensor_scalar(
                     out=o_tile[:, BANK:], in0=acc[qt][1][:], scalar1=1.0 / NH, scalar2=None, op0=ALU.mult
                 )
@@ -657,7 +660,10 @@ def tile_interpretablemultiheadattention_pa_kernel(tc, qh, kh, v, Wv, bv, out):
                 nc.vector.tensor_scalar(
                     out=o_tile[:, BANK:], in0=acc[qt][1][:], scalar1=1.0 / NH, scalar2=None, op0=ALU.mult
                 )
-            nc.sync.dma_start(out=out[0, qt * P : (qt + 1) * P, :], in_=o_tile[:])
+            if OUTQ == "s":
+                out_tiles.append((qt, o_tile))
+            else:
+                nc.sync.dma_start(out=out[0, qt * P : (qt + 1) * P, :], in_=o_tile[:])
 
         def take_tile(name, idx, bank_name):
             tr = bank(bank_name)
@@ -674,9 +680,9 @@ def tile_interpretablemultiheadattention_pa_kernel(tc, qh, kh, v, Wv, bv, out):
                 qk_copy(name, idx % NH, idx // NH, tr, copy)
 
         EXTRA = {0: [("k", 2, "acc0"), ("q", 2, "acc1")], 1: [("v", 0, "tr1"), ("k", 3, "acc0"), ("q", 3, "acc1")], 2: [("v", 1, "tr1"), ("v", 2, "acc0"), ("v", 3, "acc1")], 4: [("v", 4, "tr1")], 5: [("v", 5, "tr1"), ("v", 6, "acc0"), ("v", 7, "acc1")], 6: [("k", 4, "tr1"), ("q", 4, "acc0")], 7: [("k", 5, "tr1"), ("q", 5, "acc0")], 8: [("k", 6, "tr1"), ("q", 6, "acc0")], 9: [("k", 7, "tr1"), ("q", 7, "acc0")]}
-        W_REGROUP = {2: [(0, 0, "v", 0, 1), (0, 1, "v", 0, 1)], 4: [(1, 0, "v", 0, 1), (1, 1, "s", 0, 2)], 5: [(1, 1, "s", 1, 2)]}
+        W_REGROUP = {2: [(0, 0, "v", 0, 1), (0, 1, "v", 0, 1)], 3: [(1, 1, "s", 0, 2)], 4: [(1, 0, "v", 0, 1), (1, 1, "s", 1, 2)]}
         W_QUANT = {3: 0, 5: 1}
-        UNITS_AT = {4: [0, 1], 5: [2, 3], 6: [4, 5], 7: [6, 7], 8: [8, 9], 9: [10, 11], 10: [12, 13], 11: [14, 15]}
+        UNITS_AT = {4: [0, 1], 5: [2, 3], 6: [4, 5], 7: [6, 7, 8], 8: [9, 10], 9: [11, 12], 10: [13, 14], 11: [15]}
         UNIT_BANKS = ["mm2", "mm3", "acc0", "acc1"]
         PV_START = 10
         PV_MAX = 2
@@ -685,6 +691,9 @@ def tile_interpretablemultiheadattention_pa_kernel(tc, qh, kh, v, Wv, bv, out):
         NORM_G = "LD"
         PAIR = 0
         REPL = 2
+        ACC_BANKS = {4: ("mm2", "mm1")}
+        OUTQ = "s"
+        PACK_WAIT = 5
         tr_pending = []
         v_pending = []
         for idx, (name, n) in enumerate((("k", 0), ("q", 0), ("k", 1), ("q", 1))):
@@ -693,11 +702,15 @@ def tile_interpretablemultiheadattention_pa_kernel(tc, qh, kh, v, Wv, bv, out):
         tr_pending = []
         add_pending = []
         stores = []
+        out_tiles = []
         replicas = []
         pv_tiles = []
         steps = len(jobs) + LAG_OUT + 1
         s = 0
-        while s < steps or pv_tiles or stores:
+        while s < steps or pv_tiles or stores or out_tiles:
+            for qt, o_tile in out_tiles:
+                nc.scalar.dma_start(out=out[0, qt * P : (qt + 1) * P, :], in_=o_tile[:])
+            out_tiles = []
             for qt in stores:
                 store_out(qt)
             stores = []
@@ -724,7 +737,7 @@ def tile_interpretablemultiheadattention_pa_kernel(tc, qh, kh, v, Wv, bv, out):
                 if unit % 8 == 7:
                     replicas.extend([(unit // 8, x) for x in (2, 3, 4, 1, 0)])
             for g, x in replicas[:REPL]:
-                replicate(g, x)
+                replicate(g, x, s)
             replicas = replicas[REPL:]
             for half, G, engine, piece, pieces in W_REGROUP.get(s, []):
                 regroup_w(half, G, engine, piece, pieces)
@@ -738,7 +751,12 @@ def tile_interpretablemultiheadattention_pa_kernel(tc, qh, kh, v, Wv, bv, out):
             if live(s - (5 + (PAIR > 0)) - 1):
                 pv_tiles.extend([(s - (5 + (PAIR > 0)) - 1, slot) for slot in range(len(tiles_of(s - (5 + (PAIR > 0)) - 1)))])
             if s >= PV_START:
-                now = [x for x in pv_tiles[:PV_MAX] if jobs[x[0]][0] == jobs[pv_tiles[0][0]][0]]
+                now = []
+                for i, slot in pv_tiles[:PV_MAX]:
+                    source = tiles_of(i)[slot][2]
+                    if jobs[i][0] != jobs[pv_tiles[0][0]][0] or s < ready_at.get(source, 0 if source is None else s + 1):
+                        break
+                    now.append((i, slot))
                 pv_tiles = pv_tiles[len(now):]
                 if now:
                     weighted_sums(now)

@@ -76,6 +76,10 @@ def tile_interpretablemultiheadattention_pa_kernel(tc, qh, kh, v, Wv, bv, out):
         warm_out = const.tile([P, 1], F32, name="warm_out")
         nc.vector.memset(warm_in[:], 0.0)
         nc.scalar.activation(out=warm_out[:], in_=warm_in[:], func=ACT.Exp)
+        ones_b = const.tile([P, P], BF16, name="ones_b")
+        nc.vector.memset(ones_b[:], 1.0)
+        bias_row = const.tile([P, V], BF16, name="bias_row")
+        nc.vector.memset(bias_row[:], 0.0)
         bias_all = const.tile([P, V], BF16, name="bias_all")
 
         causal_b = const.tile([P, P], BF16, name="causal_b")
@@ -95,8 +99,8 @@ def tile_interpretablemultiheadattention_pa_kernel(tc, qh, kh, v, Wv, bv, out):
             nc.sync.dma_start(out=raw[:], in_=rows_of[name][n, g])
             raw_of[(name, n, g)] = raw
 
-        w_raw = [keep.tile([P, 4 * 2 * BANK], BF16, name="w_raw%d" % half, align_bytes=64) for half in range(V // BANK)]
-        w_rows = Wv.rearrange("(a p e) c -> a p e c", a=4, p=P, e=2)
+        w_raw = [keep.tile([P, 4 * V], BF16, name="w_raw%d" % G, align_bytes=64) for G in range(H // K_PASS)]
+        w_rows = Wv.rearrange("(a p e) c -> a p (e c)", a=4, p=P, e=2)
         v_raw = [keep.tile([P, 4 * H], BF16, name="v_raw%d" % g, align_bytes=64) for g in range(2)]
         v_rows = v.rearrange("o (g p t) h -> (o g) p (t h)", p=P, t=4)
 
@@ -109,17 +113,13 @@ def tile_interpretablemultiheadattention_pa_kernel(tc, qh, kh, v, Wv, bv, out):
         for n in range(3):
             load_qk("k", n, 0)
             load_qk("q", n, 0)
+        nc.sync.dma_start(out=bias_row[0:1, :], in_=bv.rearrange("(o c) -> o c", o=1))
         load_v(0)
         load_qk("k", 3, 0)
         load_qk("q", 3, 0)
         load_v(1)
-        for half in range(V // BANK):
-            cols = slice(half * BANK, (half + 1) * BANK)
-            for a in range(4):
-                nc.sync.dma_start(
-                    out=w_raw[half][:].rearrange("p (a e c) -> p a e c", a=4, e=2)[:, a], in_=w_rows[a][:, :, cols]
-                )
-        nc.sync.dma_start(out=bias_all[:], in_=bv.partition_broadcast(P))
+        for a in range(4):
+            nc.sync.dma_start(out=w_raw[a // 2][:, a % 2 * 2 * V : (a % 2 + 1) * 2 * V], in_=w_rows[a])
         load_v(2)
         load_v(3)
         for n in range(NH):
@@ -176,17 +176,23 @@ def tile_interpretablemultiheadattention_pa_kernel(tc, qh, kh, v, Wv, bv, out):
 
         w_codes = keep.tile([P, 2 * V], U32, name="w_codes", align_bytes=64)
         w_scales = keep.tile([P, 2 * V], U8, name="w_scales", align_bytes=64)
+        def spread_bias(half, name, copy):
+            cols = slice(half * BANK, (half + 1) * BANK)
+            bias_ps = bank(name)
+            nc.tensor.matmul(out=bias_ps[:], lhsT=ones_b[:], rhs=bias_row[:, cols], start=True, stop=True)
+            copy(out=bias_all[:, cols], in_=bias_ps[:])
+
         w_groupeds = {}
 
         def regroup_w(half, G, engine, piece, pieces):
             if True:
-                rows_t_c = w_raw[half][:, G * 4 * BANK : (G + 1) * 4 * BANK].rearrange("p (t c) -> p t c", t=4)
+                rows_t_c = w_raw[G][:].rearrange("p (t c) -> p t c", t=4)
                 if piece == 0:
                     w_grouped = w_stage.tile([P, 4 * BANK], BF16, name="w_grouped", align_bytes=64)
                     w_groupeds[(half, G)] = w_grouped
                 regroup = {"v": nc.vector.tensor_copy, "s": nc.scalar.copy, "g": nc.gpsimd.tensor_copy}[engine]
                 width = BANK // pieces
-                c0 = piece * width
+                c0 = half * BANK + piece * width
                 regroup(
                     out=w_groupeds[(half, G)][:, 4 * piece * width : 4 * (piece + 1) * width].rearrange(
                         "p (c i t) -> p c t i", i=4, t=4
@@ -288,7 +294,7 @@ def tile_interpretablemultiheadattention_pa_kernel(tc, qh, kh, v, Wv, bv, out):
             q = 0
             while q < 4:
                 count = 1
-                while q + count < 4 and quarters[q + count] == quarters[q] + count:
+                while count < 2 and q + count < 4 and quarters[q + count] == quarters[q] + count:
                     count += 1
                 src = 32 * quarters[q]
                 nc.sync.dma_start(
@@ -679,21 +685,22 @@ def tile_interpretablemultiheadattention_pa_kernel(tc, qh, kh, v, Wv, bv, out):
             else:
                 qk_copy(name, idx % NH, idx // NH, tr, copy)
 
-        EXTRA = {0: [("k", 2, "acc0"), ("q", 2, "acc1")], 1: [("v", 0, "tr1"), ("k", 3, "acc0"), ("q", 3, "acc1")], 2: [("v", 1, "tr1"), ("v", 2, "acc0"), ("v", 3, "acc1")], 4: [("v", 4, "tr1")], 5: [("v", 5, "tr1"), ("v", 6, "acc0"), ("v", 7, "acc1")], 6: [("k", 4, "tr1"), ("q", 4, "acc0")], 7: [("k", 5, "tr1"), ("q", 5, "acc0")], 8: [("k", 6, "tr1"), ("q", 6, "acc0")], 9: [("k", 7, "tr1"), ("q", 7, "acc0")]}
+        EXTRA = {0: [("k", 2, "tr1"), ("q", 2, "acc0")], 1: [("v", 0, "tr1"), ("v", 1, "acc0"), ("k", 3, "acc1")], 2: [("q", 3, "tr1"), ("v", 2, "acc0"), ("v", 3, "acc1")], 5: [("v", 4, "tr1"), ("v", 5, "acc0"), ("v", 6, "acc1")], 6: [("v", 7, "tr1"), ("k", 4, "acc0"), ("q", 4, "acc1")], 7: [("k", 5, "tr1"), ("q", 5, "acc0")], 8: [("k", 6, "tr1"), ("q", 6, "acc0")], 9: [("k", 7, "tr1"), ("q", 7, "acc0")]}
         W_REGROUP = {2: [(0, 0, "v", 0, 1), (0, 1, "v", 0, 1)], 3: [(1, 1, "s", 0, 2)], 4: [(1, 0, "v", 0, 1), (1, 1, "s", 1, 2)]}
         W_QUANT = {3: 0, 5: 1}
-        UNITS_AT = {4: [0, 1], 5: [2, 3], 6: [4, 5], 7: [6, 7, 8], 8: [9, 10], 9: [11, 12], 10: [13, 14], 11: [15]}
+        UNITS_AT = {4: [0, 1], 5: [2, 3], 6: [4, 5], 7: [6, 7], 8: [8, 9], 9: [10, 11, 12], 10: [13, 14, 15]}
         UNIT_BANKS = ["mm2", "mm3", "acc0", "acc1"]
-        PV_START = 10
+        PV_START = 11
         PV_MAX = 2
         SUM_G = False
         EVAC = "v"
         NORM_G = "LD"
         PAIR = 0
-        REPL = 2
+        REPL = 1
         ACC_BANKS = {4: ("mm2", "mm1")}
         OUTQ = "s"
-        PACK_WAIT = 5
+        PACK_WAIT = 4
+        BIAS = {1: [(0, "mm2", "v"), (1, "mm3", "v")]}
         tr_pending = []
         v_pending = []
         for idx, (name, n) in enumerate((("k", 0), ("q", 0), ("k", 1), ("q", 1))):
@@ -739,6 +746,8 @@ def tile_interpretablemultiheadattention_pa_kernel(tc, qh, kh, v, Wv, bv, out):
             for g, x in replicas[:REPL]:
                 replicate(g, x, s)
             replicas = replicas[REPL:]
+            for half, bank_name, copy in BIAS.get(s, []):
+                spread_bias(half, bank_name, nc.scalar.copy if copy == "s" else nc.vector.tensor_copy)
             for half, G, engine, piece, pieces in W_REGROUP.get(s, []):
                 regroup_w(half, G, engine, piece, pieces)
             if s in W_QUANT:

@@ -47,7 +47,7 @@ def tile_interpretablemultiheadattention_pa_kernel(tc, qh, kh, v, Wv, bv, out):
         soft = ctx.enter_context(tc.tile_pool(name="soft", bufs=3))
         three = ctx.enter_context(tc.tile_pool(name="three", bufs=4))
         heavy_codes = ctx.enter_context(tc.tile_pool(name="heavy_codes", bufs=8))
-        light = ctx.enter_context(tc.tile_pool(name="light", bufs=8))
+        light = ctx.enter_context(tc.tile_pool(name="light", bufs=10))
         stats = ctx.enter_context(tc.tile_pool(name="stats", bufs=6))
         psum = ctx.enter_context(tc.psum_pool(name="psum", bufs=1))
         ctx.enter_context(tc.manual_schedule())
@@ -110,13 +110,11 @@ def tile_interpretablemultiheadattention_pa_kernel(tc, qh, kh, v, Wv, bv, out):
                 out=v_raw[g][:, pair * 2 * H : (pair + 1) * 2 * H], in_=v_rows[g][:, pair * 2 * H : (pair + 1) * 2 * H]
             )
 
-        for n in range(3):
+        for n in range(NH):
             load_qk("k", n, 0)
             load_qk("q", n, 0)
         nc.sync.dma_start(out=bias_row[0:1, :], in_=bv.rearrange("(o c) -> o c", o=1))
         load_v(0)
-        load_qk("k", 3, 0)
-        load_qk("q", 3, 0)
         load_v(1)
         for a in range(4):
             nc.sync.dma_start(out=w_raw[a // 2][:, a % 2 * 2 * V : (a % 2 + 1) * 2 * V], in_=w_rows[a])
@@ -404,6 +402,12 @@ def tile_interpretablemultiheadattention_pa_kernel(tc, qh, kh, v, Wv, bv, out):
 
         second_calls = {}
 
+        def turn(i):
+            return i + 4 if PAIR and i >= 11 and i % 2 == 1 else i + 3
+
+        def copy_turn(i):
+            return i + 5 if PAIR and i >= 11 and i < 26 else i + 4
+
         def emit(calls):
             for out_ap, lhsT, rhs, start, stop in calls:
                 nc.tensor.matmul(out=out_ap, lhsT=lhsT, rhs=rhs, start=start, stop=stop)
@@ -685,13 +689,13 @@ def tile_interpretablemultiheadattention_pa_kernel(tc, qh, kh, v, Wv, bv, out):
             else:
                 qk_copy(name, idx % NH, idx // NH, tr, copy)
 
-        EXTRA = {0: [("k", 2, "tr1"), ("q", 2, "acc0")], 1: [("v", 0, "tr1"), ("v", 1, "acc0"), ("k", 3, "acc1")], 2: [("q", 3, "tr1"), ("v", 2, "acc0"), ("v", 3, "acc1")], 5: [("v", 4, "tr1"), ("v", 5, "acc0"), ("v", 6, "acc1")], 6: [("v", 7, "tr1"), ("k", 4, "acc0"), ("q", 4, "acc1")], 7: [("k", 5, "tr1"), ("q", 5, "acc0")], 8: [("k", 6, "tr1"), ("q", 6, "acc0")], 9: [("k", 7, "tr1"), ("q", 7, "acc0")]}
-        W_REGROUP = {2: [(0, 0, "v", 0, 1), (0, 1, "v", 0, 1)], 3: [(1, 1, "s", 0, 2)], 4: [(1, 0, "v", 0, 1), (1, 1, "s", 1, 2)]}
-        W_QUANT = {3: 0, 5: 1}
-        UNITS_AT = {4: [0, 1], 5: [2, 3], 6: [4, 5], 7: [6, 7], 8: [8, 9], 9: [10, 11, 12], 10: [13, 14, 15]}
+        EXTRA = {0: [("k", 2, "tr1"), ("q", 2, "acc0")], 1: [("k", 3, "tr1"), ("q", 3, "acc0")], 2: [("v", 0, "tr1"), ("v", 1, "acc0")], 3: [("v", 2, "tr1"), ("v", 3, "acc0")], 5: [("v", 4, "tr1")], 6: [("v", 5, "tr1"), ("v", 6, "acc0")], 7: [("v", 7, "tr1"), ("k", 4, "acc0")], 8: [("q", 4, "tr1"), ("k", 5, "acc0"), ("q", 5, "acc1")], 10: [("k", 6, "tr1"), ("q", 6, "acc0")], 11: [("k", 7, "tr1"), ("q", 7, "acc0")]}
+        W_REGROUP = {3: [(0, 0, "v", 0, 1)], 4: [(0, 1, "v", 0, 1), (1, 1, "s", 0, 2)], 5: [(1, 0, "v", 0, 1), (1, 1, "s", 1, 2)]}
+        W_QUANT = {5: 0, 6: 1}
+        UNITS_AT = {6: [0, 1, 2], 7: [3, 4, 5], 8: [6, 7, 8], 9: [9, 10, 11], 10: [12, 13, 14, 15]}
         UNIT_BANKS = ["mm2", "mm3", "acc0", "acc1"]
-        PV_START = 11
-        PV_MAX = 2
+        PV_START = 12
+        PV_MAX = 3
         SUM_G = False
         EVAC = "v"
         NORM_G = "LD"
@@ -699,8 +703,9 @@ def tile_interpretablemultiheadattention_pa_kernel(tc, qh, kh, v, Wv, bv, out):
         REPL = 1
         ACC_BANKS = {4: ("mm2", "mm1")}
         OUTQ = "s"
-        PACK_WAIT = 4
-        BIAS = {1: [(0, "mm2", "v"), (1, "mm3", "v")]}
+        PACK_WAIT = 3
+        BIAS = {2: [(0, "mm2", "v")], 3: [(1, "mm3", "s")]}
+        LATE_BANKS = ["acc0", "acc1", "tr1", "tr0"]
         tr_pending = []
         v_pending = []
         for idx, (name, n) in enumerate((("k", 0), ("q", 0), ("k", 1), ("q", 1))):
@@ -728,9 +733,13 @@ def tile_interpretablemultiheadattention_pa_kernel(tc, qh, kh, v, Wv, bv, out):
             for name, idx, tr in tr_pending:
                 empty_tile(name, idx, tr, nc.scalar.copy)
             tr_pending = []
-            copy_out(s - (4 + (PAIR > 0)))
+            for i in (s - 5, s - 4):
+                if copy_turn(i) == s:
+                    copy_out(i)
             sum_of_sums(s - LAG_NORM)
-            quantise(s - (5 + (PAIR > 0)))
+            for i in (s - 6, s - 5):
+                if copy_turn(i) == s - 1:
+                    quantise(i)
             reciprocal(s - LAG_NORM)
             scores_first(s)
             maximum_first(s)
@@ -754,11 +763,14 @@ def tile_interpretablemultiheadattention_pa_kernel(tc, qh, kh, v, Wv, bv, out):
                 quantise_w(W_QUANT[s])
             scores_second(s)
             maximum_second(s)
-            transposes(s - 3)
+            for i in (s - 4, s - 3):
+                if turn(i) == s:
+                    transposes(i)
             for name, idx, bank_name in EXTRA.get(s, []):
                 take_tile(name, idx, bank_name)
-            if live(s - (5 + (PAIR > 0)) - 1):
-                pv_tiles.extend([(s - (5 + (PAIR > 0)) - 1, slot) for slot in range(len(tiles_of(s - (5 + (PAIR > 0)) - 1)))])
+            for i in (s - 7, s - 6):
+                if live(i) and copy_turn(i) == s - 2:
+                    pv_tiles.extend([(i, slot) for slot in range(len(tiles_of(i)))])
             if s >= PV_START:
                 now = []
                 for i, slot in pv_tiles[:PV_MAX]:
@@ -773,6 +785,6 @@ def tile_interpretablemultiheadattention_pa_kernel(tc, qh, kh, v, Wv, bv, out):
                     if done[qt] == TILES_OF[qt]:
                         stores.append(qt)
             for idx, unit in enumerate(UNITS_AT.get(s, [])):
-                value_passes(unit, UNIT_BANKS[idx])
+                value_passes(unit, (UNIT_BANKS if s < 11 else LATE_BANKS)[idx])
                 add_pending.append(unit)
             s += 1

@@ -590,9 +590,7 @@ def tile_interpretablemultiheadattention_pa_kernel(tc, qh, kh, v, Wv, bv, out):
             if jobs[i][3]:
                 tr = bank("tr%d" % (i % 2))[:]
             else:
-                if "light" not in tr_banks:
-                    tr_banks["light"] = bank("tr0")
-                tr = tr_banks["light"][:, (i % 2) * 2 * P : (i % 2 + 1) * 2 * P]
+                tr = bank(LIGHT_TR[i % len(LIGHT_TR)])[:, : 2 * P]
             for slot, (words, operand, source) in enumerate(tiles_of(i)):
                 for u in range(2):
                     nc.tensor.transpose(tr[:, (2 * slot + u) * P : (2 * slot + u + 1) * P], words[u], ident_f[:])
@@ -689,11 +687,11 @@ def tile_interpretablemultiheadattention_pa_kernel(tc, qh, kh, v, Wv, bv, out):
             else:
                 qk_copy(name, idx % NH, idx // NH, tr, copy)
 
-        EXTRA = {0: [("k", 2, "tr1"), ("q", 2, "acc0")], 1: [("k", 3, "tr1"), ("q", 3, "acc0")], 2: [("v", 0, "tr1"), ("v", 1, "acc0")], 3: [("v", 2, "tr1"), ("v", 3, "acc0")], 5: [("v", 4, "tr1")], 6: [("v", 5, "tr1"), ("v", 6, "acc0")], 7: [("v", 7, "tr1"), ("k", 4, "acc0")], 8: [("q", 4, "tr1"), ("k", 5, "acc0"), ("q", 5, "acc1")], 10: [("k", 6, "tr1"), ("q", 6, "acc0")], 11: [("k", 7, "tr1"), ("q", 7, "acc0")]}
+        EXTRA = {0: [("k", 2, "acc1"), ("q", 2, "acc0")], 1: [("k", 3, "acc1"), ("q", 3, "acc0")], 2: [("v", 0, "acc1"), ("v", 1, "acc0")], 3: [("v", 2, "acc1"), ("v", 3, "acc0")], 5: [("v", 4, "acc1"), ("v", 5, "acc0")], 6: [("v", 6, "acc1"), ("v", 7, "acc0")], 7: [("k", 4, "acc1"), ("q", 4, "acc0")], 8: [("k", 5, "acc1"), ("q", 5, "acc0")], 10: [("k", 6, "acc1"), ("q", 6, "acc0")], 11: [("k", 7, "acc1"), ("q", 7, "acc0")]}
         W_REGROUP = {3: [(0, 0, "v", 0, 1)], 4: [(0, 1, "v", 0, 1), (1, 1, "s", 0, 2)], 5: [(1, 0, "v", 0, 1), (1, 1, "s", 1, 2)]}
         W_QUANT = {5: 0, 6: 1}
         UNITS_AT = {6: [0, 1, 2], 7: [3, 4, 5], 8: [6, 7, 8], 9: [9, 10, 11], 10: [12, 13, 14, 15]}
-        UNIT_BANKS = ["mm2", "mm3", "acc0", "acc1"]
+        UNIT_BANKS = {2: "acc0", 5: "acc0", 8: "acc0", 11: "acc0", 14: "acc0", 15: "acc1"}
         PV_START = 12
         PV_MAX = 3
         SUM_G = False
@@ -705,7 +703,11 @@ def tile_interpretablemultiheadattention_pa_kernel(tc, qh, kh, v, Wv, bv, out):
         OUTQ = "s"
         PACK_WAIT = 3
         BIAS = {2: [(0, "mm2", "v")], 3: [(1, "mm3", "s")]}
-        LATE_BANKS = ["acc0", "acc1", "tr1", "tr0"]
+
+        TRPOS = 0
+        COPYPOS = 0
+        QPOS = 0
+        LIGHT_TR = ["tr0", "tr1"]
         tr_pending = []
         v_pending = []
         for idx, (name, n) in enumerate((("k", 0), ("q", 0), ("k", 1), ("q", 1))):
@@ -733,17 +735,19 @@ def tile_interpretablemultiheadattention_pa_kernel(tc, qh, kh, v, Wv, bv, out):
             for name, idx, tr in tr_pending:
                 empty_tile(name, idx, tr, nc.scalar.copy)
             tr_pending = []
-            for i in (s - 5, s - 4):
-                if copy_turn(i) == s:
-                    copy_out(i)
+            if not COPYPOS:
+                copy_out(s - 4)
             sum_of_sums(s - LAG_NORM)
-            for i in (s - 6, s - 5):
-                if copy_turn(i) == s - 1:
-                    quantise(i)
+            if not QPOS:
+                quantise(s - 5)
             reciprocal(s - LAG_NORM)
             scores_first(s)
             maximum_first(s)
+            if QPOS:
+                quantise(s - 5)
             exponentials(s - LAG_EXP)
+            if COPYPOS:
+                copy_out(s - 4)
             normalise(s - LAG_NORM)
             for idx, v_grouped in v_pending:
                 v_quantise(idx, v_grouped)
@@ -761,15 +765,16 @@ def tile_interpretablemultiheadattention_pa_kernel(tc, qh, kh, v, Wv, bv, out):
                 regroup_w(half, G, engine, piece, pieces)
             if s in W_QUANT:
                 quantise_w(W_QUANT[s])
+            if TRPOS == 0:
+                transposes(s - 3)
             scores_second(s)
             maximum_second(s)
-            for i in (s - 4, s - 3):
-                if turn(i) == s:
-                    transposes(i)
+            if TRPOS == 1:
+                transposes(s - 3)
             for name, idx, bank_name in EXTRA.get(s, []):
                 take_tile(name, idx, bank_name)
-            for i in (s - 7, s - 6):
-                if live(i) and copy_turn(i) == s - 2:
+            for i in (s - 6,):
+                if live(i):
                     pv_tiles.extend([(i, slot) for slot in range(len(tiles_of(i)))])
             if s >= PV_START:
                 now = []
@@ -784,7 +789,9 @@ def tile_interpretablemultiheadattention_pa_kernel(tc, qh, kh, v, Wv, bv, out):
                     qt = jobs[now[0][0]][0]
                     if done[qt] == TILES_OF[qt]:
                         stores.append(qt)
+            if TRPOS == 2:
+                transposes(s - 3)
             for idx, unit in enumerate(UNITS_AT.get(s, [])):
-                value_passes(unit, (UNIT_BANKS if s < 11 else LATE_BANKS)[idx])
+                value_passes(unit, UNIT_BANKS[unit] if unit in UNIT_BANKS else "mm%d" % (2 + idx))
                 add_pending.append(unit)
             s += 1

from contextlib import ExitStack

import concourse.masks as masks
import concourse.mybir as mybir

F32 = mybir.dt.float32
BF16 = mybir.dt.bfloat16
U32 = mybir.dt.uint32
U8 = mybir.dt.uint8
I32 = mybir.dt.int32
FP8X4 = mybir.dt.float8_e4m3fn_x4
ALU = mybir.AluOpType
ACT = mybir.ActivationFunctionType
AXIS = mybir.AxisListType

P = 128
NH, S, D, H, V = 4, 1024, 256, 1024, 1024
K_PASS = 512
BANK = 512
S_TILES = S // P
TILES_PER_GROUP = K_PASS // P
SCALE = D ** -0.5
MASKED = -1.0e30

FLOPS = 2 * S * H * V + NH * 2 * (512 * 512 + 512 * 1024) * (D + V)


LAG_EXP = 1
LAG_NORM = 2
LAG_TRANSPOSE = 3
LAG_COPY = 4

LAG_SUM = 6
LAG_OUT = 7


def tile_interpretablemultiheadattention_pa_kernel(tc, qh, kh, v, Wv, bv, out):
    nc = tc.nc
    with ExitStack() as ctx:
        const = ctx.enter_context(tc.tile_pool(name="const", bufs=1))
        WARM = 4
        keep = ctx.enter_context(tc.tile_pool(name="keep", bufs=1))
        raw_qk = ctx.enter_context(tc.tile_pool(name="raw_qk", bufs=10))
        w_stage = ctx.enter_context(tc.tile_pool(name="w_stage", bufs=4))
        stage = ctx.enter_context(tc.tile_pool(name="stage", bufs=2))
        out_stage = ctx.enter_context(tc.tile_pool(name="out_stage", bufs=3))
        soft = ctx.enter_context(tc.tile_pool(name="soft", bufs=3))
        three = ctx.enter_context(tc.tile_pool(name="three", bufs=4))
        heavy_codes = ctx.enter_context(tc.tile_pool(name="heavy_codes", bufs=8))
        light = ctx.enter_context(tc.tile_pool(name="light", bufs=10))
        stats = ctx.enter_context(tc.tile_pool(name="stats", bufs=6))
        psum = ctx.enter_context(tc.psum_pool(name="psum", bufs=1))
        ctx.enter_context(tc.manual_schedule())

        def bank(name):
            return psum.tile([P, BANK], F32, name=name, tag=name)

        ident_f = const.tile([P, P], F32, name="ident_f")
        masks.make_identity(nc, ident_f[:])
        ident_b = const.tile([P, P], BF16, name="ident_b")
        masks.make_identity(nc, ident_b[:])
        causal_f = const.tile([P, P], F32, name="causal_f")
        nc.gpsimd.memset(causal_f[:], 0.0)
        nc.gpsimd.affine_select(
            out=causal_f[:],
            in_=causal_f[:],
            compare_op=ALU.is_ge,
            fill=MASKED,
            base=0,
            pattern=[[-1, P]],
            channel_multiplier=1,
        )
        warm_b = const.tile([P, BANK], BF16, name="warm_b")
        nc.vector.memset(warm_b[:], 0.0)
        warm_in = const.tile([P, 1], F32, name="warm_in")
        warm_out = const.tile([P, 1], F32, name="warm_out")
        nc.vector.memset(warm_in[:], 0.0)
        nc.scalar.activation(out=warm_out[:], in_=warm_in[:], func=ACT.Exp)
        ones_b = const.tile([P, P], BF16, name="ones_b")
        nc.vector.memset(ones_b[:], 1.0)
        bias_row = const.tile([P, V], BF16, name="bias_row")
        nc.vector.memset(bias_row[:], 0.0)
        bias_all = const.tile([P, V], BF16, name="bias_all")

        causal_b = const.tile([P, P], BF16, name="causal_b")
        nc.vector.tensor_copy(
            out=causal_b[:].rearrange("p (u w e) -> p u w e", u=2, e=2),
            in_=causal_f[:].rearrange("p (w u e) -> p u w e", u=2, e=2),
        )

        rows_of = {
            "q": qh.rearrange("n o (g p t) d -> (n o) g p (t d)", p=P, t=4),
            "k": kh.rearrange("n o (g p t) d -> (n o) g p (t d)", p=P, t=4),
        }
        raw_of = {}

        def load_qk(name, n, g):
            raw = raw_qk.tile([P, 4 * D], BF16, name="%s_raw%d%d" % (name, n, g), tag="raw_qk")
            nc.sync.dma_start(out=raw[:], in_=rows_of[name][n, g])
            raw_of[(name, n, g)] = raw

        w_raw = [keep.tile([P, 4 * V], BF16, name="w_raw%d" % G, align_bytes=64) for G in range(H // K_PASS)]
        w_rows = Wv.rearrange("(a p e) c -> a p (e c)", a=4, p=P, e=2)
        v_raw = [keep.tile([P, 4 * H], BF16, name="v_raw%d" % g, align_bytes=64) for g in range(2)]
        v_rows = v.rearrange("o (g p t) h -> (o g) p (t h)", p=P, t=4)

        def load_v(a):
            g, pair = a // 2, a % 2
            nc.sync.dma_start(
                out=v_raw[g][:, pair * 2 * H : (pair + 1) * 2 * H], in_=v_rows[g][:, pair * 2 * H : (pair + 1) * 2 * H]
            )

        for n in range(NH):
            load_qk("k", n, 0)
            load_qk("q", n, 0)
        nc.sync.dma_start(out=bias_row[0:1, :], in_=bv.rearrange("(o c) -> o c", o=1))
        load_v(0)
        load_v(1)
        for a in range(4):
            nc.sync.dma_start(out=w_raw[a // 2][:, a % 2 * 2 * V : (a % 2 + 1) * 2 * V], in_=w_rows[a])
        load_v(2)
        load_v(3)
        for n in range(NH):
            load_qk("k", n, 1)
            load_qk("q", n, 1)
        warm_ps = bank("tr0")
        for rep in range(WARM):
            nc.tensor.matmul(out=warm_ps[:], lhsT=warm_b[:, :P], rhs=warm_b[:], start=True, stop=True)
        words_T = {"q": keep.tile([P, NH * S], F32, name="qT"), "k": keep.tile([P, NH * S], F32, name="kT")}

        def qk_transposes(name, n, g, tr):
            words = raw_of[(name, n, g)][:].bitcast(F32)
            for t in range(4):
                nc.tensor.transpose(tr[:, t * P : (t + 1) * P], words[:, t * P : (t + 1) * P], ident_f[:])

        def qk_copy(name, n, g, tr, copy):
            out_words = words_T[name][:, (n * 2 + g) * K_PASS : (n * 2 + g + 1) * K_PASS]
            if name == "q":
                copy(
                    out=out_words.rearrange("p (s t) -> p s t", t=4),
                    in_=tr[:].rearrange("p (t s) -> p s t", t=4),
                )
            else:
                copy(
                    out=out_words.rearrange("p (u s e) -> p u s e", u=2, e=2),
                    in_=tr[:].rearrange("p (u e s) -> p u s e", u=2, e=2),
                )

        qT_b = words_T["q"][:].bitcast(BF16).rearrange("p (n s e) -> p n s e", n=NH, e=2)
        kT_b = words_T["k"][:].bitcast(BF16).rearrange("p (n g u x e) -> p g n u x e", g=2, n=NH, u=2, e=2)

        v_codes = keep.tile([P, S_TILES * 2 * P], U32, name="v_codes", align_bytes=64)
        v_scales = keep.tile([P, S_TILES * 2 * P], U8, name="v_scales", align_bytes=64)

        def v_transposes(st, tr):
            for b in range(4):
                nc.tensor.transpose(
                    tr[:, b * P : (b + 1) * P],
                    v_raw[st // 4][:].bitcast(F32)[:, st % 4 * (H // 2) + b * P : st % 4 * (H // 2) + (b + 1) * P],
                    ident_f[:],
                )

        def v_copy(tr):
            v_grouped = soft.tile([P, 2 * K_PASS], BF16, name="v_grouped", align_bytes=64)
            nc.scalar.copy(
                out=v_grouped[:].bitcast(F32).rearrange("p (g s u) -> p g s u", g=2, u=2),
                in_=tr[:].rearrange("p (g u s) -> p g s u", g=2, u=2),
            )
            return v_grouped

        def v_quantise(st, v_grouped):
            cols = slice(st * 2 * P, (st + 1) * 2 * P)
            nc.vector.quantize_mx(out=v_codes[:, cols].bitcast(FP8X4), scales=v_scales[:, cols], in_=v_grouped[:])

        w_codes = keep.tile([P, 2 * V], U32, name="w_codes", align_bytes=64)
        w_scales = keep.tile([P, 2 * V], U8, name="w_scales", align_bytes=64)
        def spread_bias(half, name, copy):
            cols = slice(half * BANK, (half + 1) * BANK)
            bias_ps = bank(name)
            nc.tensor.matmul(out=bias_ps[:], lhsT=ones_b[:], rhs=bias_row[:, cols], start=True, stop=True)
            copy(out=bias_all[:, cols], in_=bias_ps[:])

        w_groupeds = {}

        def regroup_w(half, G, engine, piece, pieces):
            if True:
                rows_t_c = w_raw[G][:].rearrange("p (t c) -> p t c", t=4)
                if piece == 0:
                    w_grouped = w_stage.tile([P, 4 * BANK], BF16, name="w_grouped", align_bytes=64)
                    w_groupeds[(half, G)] = w_grouped
                regroup = {"v": nc.vector.tensor_copy, "s": nc.scalar.copy, "g": nc.gpsimd.tensor_copy}[engine]
                width = BANK // pieces
                c0 = half * BANK + piece * width
                regroup(
                    out=w_groupeds[(half, G)][:, 4 * piece * width : 4 * (piece + 1) * width].rearrange(
                        "p (c i t) -> p c t i", i=4, t=4
                    ),
                    in_=rows_t_c[:, :, c0 : c0 + width].rearrange("p t (c i) -> p c t i", i=4),
                )

        def quantise_w(half):
            for G in range(H // K_PASS):
                cols = slice(G * V + half * BANK, G * V + (half + 1) * BANK)
                nc.vector.quantize_mx(
                    out=w_codes[:, cols].bitcast(FP8X4), scales=w_scales[:, cols], in_=w_groupeds[(half, G)][:]
                )

        OPERAND = V + V // 4
        vv_tiles = []
        for g in range(2):
            vv_tile = keep.tile([P, OPERAND], U32, name="vv%d" % g, align_bytes=64)
            nc.gpsimd.memset(vv_tile[:, V:], 0)
            vv_tiles.append(vv_tile)

        def codes_of(operand):
            return operand[:, :V].bitcast(FP8X4)

        def scales_of(operand):
            return operand[:, V:].bitcast(U8)

        UNITS = (S // K_PASS) * (V // P)
        unit_banks = {}
        unit_grouped = {}

        def value_passes(unit, bank_name):
            g = unit // (V // P)
            c0 = unit % (V // P) * P
            vv_ps = bank(bank_name)
            unit_banks[unit] = vv_ps
            for t in range(4):
                for G in range(H // K_PASS):
                    lcols = slice(((4 * g + t) * 2 + G) * P, ((4 * g + t) * 2 + G + 1) * P)
                    rcols = slice(G * V + c0, G * V + c0 + P)
                    nc.tensor.matmul_mx(
                        out=vv_ps[:, t * P : (t + 1) * P],
                        lhsT=v_codes[:, lcols].bitcast(FP8X4),
                        lhsT_scale=v_scales[:, lcols],
                        rhs=w_codes[:, rcols].bitcast(FP8X4),
                        rhs_scale=w_scales[:, rcols],
                        start=(G == 0),
                        stop=(G == H // K_PASS - 1),
                    )

        def value_add(unit):
            if unit not in unit_banks:
                return
            quarter = unit % 4
            c0 = unit % (V // P) * P
            if quarter == 0:
                unit_grouped[unit // 4] = stage.tile([P, 4 * BANK], BF16, name="vv_grouped", align_bytes=64)
            nc.vector.tensor_tensor(
                out=unit_grouped[unit // 4][:, quarter * 4 * P : (quarter + 1) * 4 * P].rearrange(
                    "p (c t) -> p c t", t=4
                ),
                in0=unit_banks[unit][:].rearrange("p (t c) -> p c t", t=4),
                in1=bias_all[:, c0 : c0 + P].unsqueeze(2).to_broadcast([P, P, 4]),
                op=ALU.add,
            )

        def value_quantise(unit):
            if unit not in unit_banks or unit % 4 != 3:
                return
            operand = vv_tiles[unit // 8]
            cols = slice(unit // 4 % 2 * BANK, (unit // 4 % 2 + 1) * BANK)
            nc.vector.quantize_mx(
                out=codes_of(operand)[:, cols], scales=scales_of(operand)[:, cols], in_=unit_grouped[unit // 4][:]
            )

        QUARTERS = [(0, 0, 0, 0), (0, 1, 0, 1), (0, 1, 2, 0), (1, 2, 0, 1), (2, 0, 1, 2)]
        packed = {}
        ready_at = {}

        def replicate(g, x, s):
            if (g, x) in ((0, 2), (0, 3)):
                packed_tile = keep.tile([P, 2 * V], U32, name="packed_w%d" % x, tag="w_raw%d" % (x - 2), align_bytes=64)
                operand = packed_tile[:, :OPERAND]
            elif (g, x) in ((0, 4), (0, 1), (0, 0), (1, 2)):
                packed_tile = w_stage.tile([P, OPERAND], U32, name="packed_s", tag="w_grouped", align_bytes=64)
                operand = packed_tile[:]
            elif x == 3:
                packed_tile = keep.tile([P, 2 * V], U32, name="packed_v0", tag="v_raw0", align_bytes=64)
                operand = packed_tile[:, :OPERAND]
            elif x == 4:
                packed_tile = keep.tile([P, 2 * V], U32, name="packed_v1", tag="v_raw1", align_bytes=64)
                operand = packed_tile[:, :OPERAND]
            else:
                packed_tile = keep.tile([P, OPERAND], U32, name="packed_last%d" % x, align_bytes=64)
                operand = packed_tile[:]
            packed[(g, x)] = operand
            ready_at[(g, x)] = s + PACK_WAIT
            quarters = QUARTERS[x]
            q = 0
            while q < 4:
                count = 1
                while count < 2 and q + count < 4 and quarters[q + count] == quarters[q] + count:
                    count += 1
                src = 32 * quarters[q]
                nc.sync.dma_start(
                    out=operand[32 * q : 32 * (q + count), :].bitcast(I32),
                    in_=vv_tiles[g][src : src + 32 * count, :].bitcast(I32),
                )
                q += count

        HALF = K_PASS // 2
        jobs = []
        for qt in (3, 2, 1, 0, 7, 6, 5, 4):
            m = qt % TILES_PER_GROUP
            pack = {0: 4, 1: 2, 2: 1, 3: 1}[m]
            heavy = qt >= TILES_PER_GROUP
            if heavy:
                for n in range(NH):
                    jobs.append((qt, m, pack, True, [n]))
            else:
                for n in range(0, NH, pack):
                    jobs.append((qt, m, pack, False, list(range(n, n + pack))))
        LAST_QT = jobs[-1][0]
        TILES_OF = {}
        for qt in range(S_TILES):
            m = qt % TILES_PER_GROUP
            TILES_OF[qt] = m + 1 + (NH if qt >= TILES_PER_GROUP else 0)

        diag_bank = {}
        full_bank = {}
        diag_max = {}
        shifts = {}
        e_full = {}
        e_diag = {}
        sums_of = {}
        recips = {}
        p_full = {}
        p_diag = {}
        p_three = {}
        tr_banks = {}
        p_groupeds = {}
        p_operands = {}
        acc = {}
        done = {}

        def live(i):
            return 0 <= i < len(jobs)

        def diag_key(i):
            qt, m, pack, heavy, heads = jobs[i]
            return (qt, heads[0] // pack)

        def opens(i):
            qt, m, pack, heavy, heads = jobs[i]
            return heads[0] % pack == 0

        def closes(i):
            qt, m, pack, heavy, heads = jobs[i]
            return heads[-1] % pack == pack - 1

        def diag_heads(i):
            qt, m, pack, heavy, heads = jobs[i]
            n0 = heads[0] // pack * pack
            return list(range(n0, n0 + pack))

        def score_calls(i):
            qt, m, pack, heavy, heads = jobs[i]
            calls = []
            if heavy:
                sc = bank("mm%d" % (2 * ((i + 1) % 2) + 1))
                full_bank[i] = sc
                for e in range(2):
                    calls.append((
                        sc[:].rearrange("p (u x) -> p u x", u=2),
                        qT_b[:, heads[0], qt * P : (qt + 1) * P, e],
                        kT_b[:, 0, heads[0], :, :, e],
                        e == 0,
                        e == 1,
                    ))
            n_first = len(calls)
            if opens(i):
                if heavy:
                    name = "mm%d" % (2 * ((i + 1 + (heads[0] // 2 if pack == 2 else 0)) % 2))
                else:
                    name = "mm%d" % (i % 2)
                sc = bank(name)
                diag_bank[diag_key(i)] = sc
                width = P * (m + 1)
                for h, n in enumerate(diag_heads(i)):
                    region = sc[:, h * width : (h + 1) * width].rearrange("p (u x) -> p u x", u=2)
                    for e in range(2):
                        calls.append((
                            region,
                            qT_b[:, n, qt * P : (qt + 1) * P, e],
                            kT_b[:, qt // TILES_PER_GROUP, n, :, : 64 * (m + 1), e],
                            e == 0,
                            False,
                        ))
                    calls.append((
                        region[:, :, 64 * m : 64 * (m + 1)],
                        ident_b[:],
                        causal_b[:].rearrange("p (u c) -> p u c", u=2),
                        False,
                        True,
                    ))
            if not heavy:
                n_first = len(calls) // 2
            return calls[:n_first], calls[n_first:]

        second_calls = {}

        def turn(i):
            return i + 4 if PAIR and i >= 11 and i % 2 == 1 else i + 3

        def copy_turn(i):
            return i + 5 if PAIR and i >= 11 and i < 26 else i + 4

        def emit(calls):
            for out_ap, lhsT, rhs, start, stop in calls:
                nc.tensor.matmul(out=out_ap, lhsT=lhsT, rhs=rhs, start=start, stop=stop)

        def scores_first(i):
            if live(i):
                first, second_calls[i] = score_calls(i)
                emit(first)

        def scores_second(i):
            if live(i):
                emit(second_calls[i])

        full_max = {}

        def maximum_first(i):
            if live(i) and jobs[i][3]:
                full_max[i] = stats.tile([P, 1], F32, name="full_max")
                nc.vector.reduce_max(out=full_max[i][:], in_=full_bank[i][:], axis=AXIS.X)

        def maximum_second(i):
            if not live(i):
                return
            qt, m, pack, heavy, heads = jobs[i]
            key = diag_key(i)
            if opens(i):
                diag_max[key] = stats.tile([P, pack], F32, name="diag_max%d" % pack)
                width = P * (m + 1)
                nc.vector.reduce_max(
                    out=diag_max[key][:],
                    in_=diag_bank[key][:, : pack * width].rearrange("p (h x) -> p h x", h=pack),
                    axis=AXIS.X,
                )
            if heavy:
                h = heads[0] % pack
                shift = stats.tile([P, 1], F32, name="shift")
                nc.gpsimd.tensor_scalar(
                    out=shift[:], in0=diag_max[key][:, h : h + 1], scalar1=full_max[i][:], scalar2=-SCALE,
                    op0=ALU.max, op1=ALU.mult,
                )
            else:
                shift = stats.tile([P, pack], F32, name="shift%d" % pack)
                nc.gpsimd.tensor_scalar(
                    out=shift[:], in0=diag_max[key][:], scalar1=-SCALE, scalar2=0.0, op0=ALU.mult, op1=ALU.add
                )
            shifts[i] = shift

        def diag_region(tile_ap, i, h):
            m = jobs[i][1]
            c = 64 * (m + 1)
            return tile_ap.rearrange("p (u x) -> p u x", u=2)[:, :, h * c : (h + 1) * c]

        def exponentials(i):
            if not live(i):
                return
            qt, m, pack, heavy, heads = jobs[i]
            key = diag_key(i)
            width = P * (m + 1)
            e_tile = soft.tile([P, (1 + heavy) * K_PASS], F32, name="e_heavy" if heavy else "e_light")
            e_full[i] = e_tile[:, K_PASS:] if heavy else None
            e_diag[i] = [e_tile[:, b * width : (b + 1) * width] for b in range(len(heads))]
            sums = stats.tile([P, 4], F32, name="sums")
            if heavy:
                nc.scalar.activation(
                    out=e_full[i], in_=full_bank[i][:], func=ACT.Exp, bias=shifts[i][:], scale=SCALE,
                    accum_out=sums[:, 1:2],
                )
            for b, n in enumerate(heads):
                h = n % pack
                nc.scalar.activation(
                    out=e_diag[i][b],
                    in_=diag_bank[key][:, h * width : (h + 1) * width],
                    func=ACT.Exp,
                    bias=shifts[i][:, b : b + 1],
                    scale=SCALE,
                    accum_out=sums[:, b : b + 1],
                )
            sums_of[i] = sums

        def sum_of_sums(i):
            if live(i) and jobs[i][3]:
                total = stats.tile([P, 1], F32, name="total")
                (nc.gpsimd if SUM_G else nc.vector).tensor_tensor(out=total[:], in0=sums_of[i][:, 0:1], in1=sums_of[i][:, 1:2], op=ALU.add)
                sums_of[i] = total

        def reciprocal(i):
            if live(i):
                count = len(jobs[i][4])
                recips[i] = stats.tile([P, count], F32, name="recip%d" % count)
                nc.vector.reciprocal(out=recips[i][:], in_=sums_of[i][:, :count])

        def normalise(i):
            if not live(i):
                return
            qt, m, pack, heavy, heads = jobs[i]
            key = diag_key(i)
            if m == 2:
                if heavy:
                    p_tile = soft.tile([P, K_PASS], BF16, name="p_full")
                    p_full[i] = p_tile[:]
                if heads[0] == 0:
                    p_three[qt] = []
                if heads[0] < 3:
                    p_tile = three.tile([P, K_PASS], BF16, name="p_three")
                    p_three[qt].append(p_tile)
            elif pack == 1:
                p_tile = soft.tile([P, 2 * K_PASS], BF16, name="p_tile")
                p_full[i] = p_tile[:, :K_PASS]
                p_diag[key] = p_tile[:, K_PASS:]
            else:
                if heavy:
                    p_tile = soft.tile([P, K_PASS], BF16, name="p_full")
                    p_full[i] = p_tile[:]
                if opens(i):
                    p_tile = soft.tile([P, K_PASS], BF16, name="p_diag")
                    p_diag[key] = p_tile[:]
            if heavy:
                if "F" in NORM_G:
                    nc.gpsimd.tensor_scalar(
                        out=p_full[i], in0=e_full[i], scalar1=recips[i][:], scalar2=0.0, op0=ALU.mult, op1=ALU.add
                    )
                else:
                    nc.vector.tensor_scalar(
                        out=p_full[i], in0=e_full[i], scalar1=recips[i][:], scalar2=None, op0=ALU.mult
                    )
            todo = []
            for b, n in enumerate(heads):
                h = n % pack
                e_halves = e_diag[i][b].rearrange("p (u x) -> p u x", u=2)
                if m == 2:
                    pieces = []
                    for x in range(3):
                        c_from = max(3 * n, 4 * x)
                        c_to = min(3 * n + 3, 4 * x + 4)
                        if c_from < c_to:
                            pieces.append((
                                p_three[qt][x][:].rearrange("p (u y) -> p u y", u=2)[
                                    :, :, 64 * (c_from - 4 * x) : 64 * (c_to - 4 * x)
                                ],
                                e_halves[:, :, 64 * (c_from - 3 * n) : 64 * (c_to - 3 * n)],
                            ))
                else:
                    pieces = [(diag_region(p_diag[key], i, h), e_halves)]
                todo.extend([(b, x, y) for x, y in pieces])
            for b, p_region, e_region in todo:
                if ("D" if heavy else "L") in NORM_G:
                    nc.gpsimd.tensor_scalar(
                        out=p_region, in0=e_region,
                        scalar1=recips[i][:, b : b + 1], scalar2=0.0, op0=ALU.mult, op1=ALU.add,
                    )
                else:
                    nc.vector.tensor_scalar(
                        out=p_region, in0=e_region,
                        scalar1=recips[i][:, b : b + 1], scalar2=None, op0=ALU.mult,
                    )

        def tiles_of(i):
            qt, m, pack, heavy, heads = jobs[i]
            g = qt // TILES_PER_GROUP
            tiles = []
            if heavy:
                words = p_full[i].bitcast(F32)
                tiles.append(([words[:, :P], words[:, P:]], vv_tiles[0], None))
            if m == 3:
                words = p_diag[diag_key(i)].bitcast(F32)
                tiles.append(([words[:, :P], words[:, P:]], vv_tiles[g], None))
            elif m == 2:
                if heads[0] > 0:
                    x = heads[0] - 1
                    words = p_three[qt][x][:].bitcast(F32)
                    tiles.append(([words[:, :P], words[:, P:]], packed.get((g, 2 + x)), (g, 2 + x)))
            elif closes(i):
                words = p_diag[diag_key(i)].bitcast(F32)
                tiles.append(([words[:, :P], words[:, P:]], packed.get((g, m)), (g, m)))
            return tiles

        def transposes(i):
            if not live(i) or not tiles_of(i):
                return
            if jobs[i][3]:
                tr = bank("tr%d" % (i % 2))[:]
            else:
                tr = bank(LIGHT_TR[i % len(LIGHT_TR)])[:, : 2 * P]
            for slot, (words, operand, source) in enumerate(tiles_of(i)):
                for u in range(2):
                    nc.tensor.transpose(tr[:, (2 * slot + u) * P : (2 * slot + u + 1) * P], words[u], ident_f[:])
            tr_banks[i] = tr

        def copy_out(i):
            if not live(i) or not tiles_of(i):
                return
            n_tiles = len(tiles_of(i))
            p_grouped = soft.tile([P, 2 * K_PASS], BF16, name="p_grouped", align_bytes=64)
            nc.scalar.copy(
                out=p_grouped[:].bitcast(F32)[:, : n_tiles * 2 * P].rearrange(
                    "p (g q u) -> p g q u", g=n_tiles, u=2
                ),
                in_=tr_banks[i][:, : n_tiles * 2 * P].rearrange("p (g u q) -> p g q u", g=n_tiles, u=2),
            )
            p_groupeds[i] = p_grouped

        def quantise(i):
            if not live(i) or not tiles_of(i):
                return
            n_tiles = len(tiles_of(i))
            if jobs[i][3]:
                p_codes = heavy_codes.tile([P, 2 * P], U32, name="p_codes", align_bytes=64)
                p_scales = heavy_codes.tile([P, 2 * P], U8, name="p_scales", align_bytes=64)
            else:
                p_codes = light.tile([P, P], U32, name="l_codes", align_bytes=64)
                p_scales = light.tile([P, P], U8, name="l_scales", align_bytes=64)
            nc.vector.quantize_mx(
                out=p_codes[:, : n_tiles * P].bitcast(FP8X4),
                scales=p_scales[:, : n_tiles * P],
                in_=p_groupeds[i][:, : n_tiles * K_PASS],
            )
            p_operands[i] = (p_codes, p_scales)

        def weighted_sums(tiles):
            qt = jobs[tiles[0][0]][0]
            if qt not in acc:
                acc[qt] = [bank(ACC_BANKS.get(qt, ("acc0", "acc1"))[half]) for half in range(V // BANK)]
                done[qt] = 0
            passes = [(idx, half) for idx in range(len(tiles)) for half in range(V // BANK)]
            if qt == LAST_QT:
                passes = [(idx, half) for half in range(V // BANK) for idx in range(len(tiles))]
            for idx, half in passes:
                i, slot = tiles[idx]
                p_codes, p_scales = p_operands[i]
                words, operand, source = tiles_of(i)[slot]
                lcols = slice(slot * P, (slot + 1) * P)
                rcols = slice(half * BANK, (half + 1) * BANK)
                nc.tensor.matmul_mx(
                    out=acc[qt][half][:],
                    lhsT=p_codes[:, lcols].bitcast(FP8X4),
                    lhsT_scale=p_scales[:, lcols],
                    rhs=codes_of(operand)[:, rcols],
                    rhs_scale=scales_of(operand)[:, rcols],
                    start=(done[qt] + idx == 0),
                    stop=(done[qt] + idx == TILES_OF[qt] - 1),
                )
            done[qt] += len(tiles)

        def store_out(qt):
            o_tile = out_stage.tile([P, V], F32, name="o_tile")
            if qt == LAST_QT:
                nc.scalar.mul(out=o_tile[:, :BANK], in_=acc[qt][0][:], mul=1.0 / NH)
                (nc.scalar if OUTQ == "s" else nc.sync).dma_start(out=out[0, qt * P : (qt + 1) * P, :BANK], in_=o_tile[:, :BANK])
                nc.vector.tensor_scalar(
                    out=o_tile[:, BANK:], in0=acc[qt][1][:], scalar1=1.0 / NH, scalar2=None, op0=ALU.mult
                )
                nc.sync.dma_start(out=out[0, qt * P : (qt + 1) * P, BANK:], in_=o_tile[:, BANK:])
                return
            nc.scalar.mul(out=o_tile[:, :BANK], in_=acc[qt][0][:], mul=1.0 / NH)
            if EVAC == "s":
                nc.scalar.mul(out=o_tile[:, BANK:], in_=acc[qt][1][:], mul=1.0 / NH)
            else:
                nc.vector.tensor_scalar(
                    out=o_tile[:, BANK:], in0=acc[qt][1][:], scalar1=1.0 / NH, scalar2=None, op0=ALU.mult
                )
            if OUTQ == "s":
                out_tiles.append((qt, o_tile))
            else:
                nc.sync.dma_start(out=out[0, qt * P : (qt + 1) * P, :], in_=o_tile[:])

        def take_tile(name, idx, bank_name):
            tr = bank(bank_name)
            if name == "v":
                v_transposes(idx, tr)
            else:
                qk_transposes(name, idx % NH, idx // NH, tr)
            tr_pending.append((name, idx, tr))

        def empty_tile(name, idx, tr, copy):
            if name == "v":
                v_pending.append((idx, v_copy(tr)))
            else:
                qk_copy(name, idx % NH, idx // NH, tr, copy)

        EXTRA = {0: [("k", 2, "acc1"), ("q", 2, "acc0")], 1: [("k", 3, "acc1"), ("q", 3, "acc0")], 2: [("v", 0, "acc1"), ("v", 1, "acc0")], 3: [("v", 2, "acc1"), ("v", 3, "acc0")], 5: [("v", 4, "acc1"), ("v", 5, "acc0")], 6: [("v", 6, "acc1"), ("v", 7, "acc0")], 7: [("k", 4, "acc1"), ("q", 4, "acc0")], 8: [("k", 5, "acc1"), ("q", 5, "acc0")], 10: [("k", 6, "acc1"), ("q", 6, "acc0")], 11: [("k", 7, "acc1"), ("q", 7, "acc0")]}
        W_REGROUP = {3: [(0, 0, "v", 0, 1)], 4: [(0, 1, "v", 0, 1), (1, 1, "s", 0, 2)], 5: [(1, 0, "v", 0, 1), (1, 1, "s", 1, 2)]}
        W_QUANT = {5: 0, 6: 1}
        UNITS_AT = {6: [0, 1, 2], 7: [3, 4, 5], 8: [6, 7, 8], 9: [9, 10, 11], 10: [12, 13, 14, 15]}
        UNIT_BANKS = {2: "acc0", 5: "acc0", 8: "acc0", 11: "acc0", 14: "acc0", 15: "acc1"}
        PV_START = 12
        PV_MAX = 3
        SUM_G = False
        EVAC = "v"
        NORM_G = "LD"
        PAIR = 0
        REPL = 1
        ACC_BANKS = {4: ("mm2", "mm1")}
        OUTQ = "s"
        PACK_WAIT = 3
        BIAS = {2: [(0, "mm2", "v")], 3: [(1, "mm3", "s")]}

        TRPOS = 0
        COPYPOS = 0
        QPOS = 0
        LIGHT_TR = ["tr0", "tr1"]
        tr_pending = []
        v_pending = []
        for idx, (name, n) in enumerate((("k", 0), ("q", 0), ("k", 1), ("q", 1))):
            take_tile(name, n, ("acc0", "acc1", "mm2", "mm3")[idx])
            empty_tile(name, n, tr_pending[idx][2], nc.vector.tensor_copy if idx % 2 else nc.scalar.copy)
        tr_pending = []
        add_pending = []
        stores = []
        out_tiles = []
        replicas = []
        pv_tiles = []
        steps = len(jobs) + LAG_OUT + 1
        s = 0
        while s < steps or pv_tiles or stores or out_tiles:
            for qt, o_tile in out_tiles:
                nc.scalar.dma_start(out=out[0, qt * P : (qt + 1) * P, :], in_=o_tile[:])
            out_tiles = []
            for qt in stores:
                store_out(qt)
            stores = []
            added = add_pending
            add_pending = []
            for unit in added:
                value_add(unit)
            for name, idx, tr in tr_pending:
                empty_tile(name, idx, tr, nc.scalar.copy)
            tr_pending = []
            if not COPYPOS:
                copy_out(s - 4)
            sum_of_sums(s - LAG_NORM)
            if not QPOS:
                quantise(s - 5)
            reciprocal(s - LAG_NORM)
            scores_first(s)
            maximum_first(s)
            if QPOS:
                quantise(s - 5)
            exponentials(s - LAG_EXP)
            if COPYPOS:
                copy_out(s - 4)
            normalise(s - LAG_NORM)
            for idx, v_grouped in v_pending:
                v_quantise(idx, v_grouped)
            v_pending = []
            for unit in added:
                value_quantise(unit)
                if unit % 8 == 7:
                    replicas.extend([(unit // 8, x) for x in (2, 3, 4, 1, 0)])
            for g, x in replicas[:REPL]:
                replicate(g, x, s)
            replicas = replicas[REPL:]
            for half, bank_name, copy in BIAS.get(s, []):
                spread_bias(half, bank_name, nc.scalar.copy if copy == "s" else nc.vector.tensor_copy)
            for half, G, engine, piece, pieces in W_REGROUP.get(s, []):
                regroup_w(half, G, engine, piece, pieces)
            if s in W_QUANT:
                quantise_w(W_QUANT[s])
            if TRPOS == 0:
                transposes(s - 3)
            scores_second(s)
            maximum_second(s)
            if TRPOS == 1:
                transposes(s - 3)
            for name, idx, bank_name in EXTRA.get(s, []):
                take_tile(name, idx, bank_name)
            for i in (s - 6,):
                if live(i):
                    pv_tiles.extend([(i, slot) for slot in range(len(tiles_of(i)))])
            if s >= PV_START:
                now = []
                for i, slot in pv_tiles[:PV_MAX]:
                    source = tiles_of(i)[slot][2]
                    if jobs[i][0] != jobs[pv_tiles[0][0]][0] or s < ready_at.get(source, 0 if source is None else s + 1):
                        break
                    now.append((i, slot))
                pv_tiles = pv_tiles[len(now):]
                if now:
                    weighted_sums(now)
                    qt = jobs[now[0][0]][0]
                    if done[qt] == TILES_OF[qt]:
                        stores.append(qt)
            if TRPOS == 2:
                transposes(s - 3)
            for idx, unit in enumerate(UNITS_AT.get(s, [])):
                value_passes(unit, UNIT_BANKS[unit] if unit in UNIT_BANKS else "mm%d" % (2 + idx))
                add_pending.append(unit)
            s += 1
